import numpy as np
import ml_dtypes


BF16 = ml_dtypes.bfloat16


def bf(x):
    return np.asarray(x, np.float32).astype(BF16)


def f64(x):
    return np.asarray(x).astype(np.float64)


E2M1 = np.array([0.0, 0.5, 1.0, 1.5, 2.0, 3.0, 4.0, 6.0, -0.0, -0.5, -1.0, -1.5, -2.0, -3.0, -4.0, -6.0])


def pack_weight(w, fmt):
    k, n = w.shape
    w = f64(bf(w)).reshape(k // 32, 32, n)
    amax = np.abs(w).max(1)
    if fmt == "e4m3":
        byte = np.frexp(amax)[1] - 1 + 127 - 7
    else:
        mant, ex = np.frexp(amax / 6.0)
        byte = np.where(mant > 0.5, ex, ex - 1) + 127
    byte = np.clip(np.where(amax > 0, byte, 1), 1, 254)
    scaled = (w * np.exp2(127.0 - byte)[:, None, :]).reshape(k, n).astype(np.float32)
    by_word = np.ascontiguousarray(scaled.reshape(k // 512, 128, 4, n).transpose(0, 1, 3, 2))
    if fmt == "e4m3":
        words = by_word.astype(ml_dtypes.float8_e4m3fn).view(np.uint8)
    else:
        c = by_word.astype(ml_dtypes.float4_e2m1fn).view(np.uint8) & 0xF
        words = c[..., 0::2] | (c[..., 1::2] << 4)
    return np.ascontiguousarray(words), np.ascontiguousarray(byte.astype(np.uint8).reshape(k // 512, 16, n))


def unpack_weight(words, scales, fmt):
    g, p, n, _ = words.shape
    if fmt == "e4m3":
        vals = np.ascontiguousarray(words).view(ml_dtypes.float8_e4m3fn).astype(np.float64)
    else:
        nib = np.empty((g, p, n, 4), np.uint8)
        nib[..., 0::2] = words & 0xF
        nib[..., 1::2] = words >> 4
        vals = E2M1[nib]
    vals = vals * np.repeat(np.exp2(scales.astype(np.float64) - 127.0), 8, axis=1)[..., None]
    return vals.transpose(0, 1, 3, 2).reshape(g * 512, n)

def pack4(w):
    words, scales = pack_weight(w, "e2m1")
    return words.reshape(words.shape[0], 128, -1), scales


def unpack4(words, scales):
    return unpack_weight(words.reshape(words.shape[0], 128, -1, 2), scales, "e2m1")


def kspread(k):
    return np.exp2(np.repeat(np.random.randint(-6, 7, k // 32), 32).astype(np.float64))


B, H, W, C, F, K, G, RR = 8, 32, 32, 4096, 512, 3, 16, 4
KK = K * K
P = B * H * W


def setup_inputs():
    s = kspread(C)
    x = np.random.standard_normal((B, H, W, C)) * s
    x_words, x_scales = pack4(np.ascontiguousarray(x.reshape(P, C).T))
    Wi_words, Wi_scales = pack4(np.random.standard_normal((C, F)) / np.sqrt(C) / s[:, None])
    bi = bf(np.random.standard_normal(F) * 0.3)
    w_span = bf(np.random.standard_normal((B, H, W, KK * G)) * 0.7)
    return {"x_words": x_words,
            "x_scales": x_scales,
            "Wi_words": Wi_words,
            "Wi_scales": Wi_scales,
            "bi": bi,
            "w_span": w_span}


def reference(x_words, x_scales, Wi_words, Wi_scales, bi, w_span):
    xi = ((unpack4(x_words, x_scales).T @ unpack4(Wi_words, Wi_scales)) + f64(bi)).reshape(B, H, W, F)
    pad = (K - 1) // 2
    xp = np.pad(xi, ((0, 0), (pad, pad), (pad, pad), (0, 0)))
    patches = np.stack([xp[:, i:i + H, j:j + W, :] for i in range(K) for j in range(K)], axis=-2)
    patches = patches.reshape(B, H, W, G, F // G, KK)
    w = f64(w_span).reshape(B, H, W, G, KK)[:, :, :, :, None, :]
    return (w * patches).sum(-1).reshape(B, H, W, F)

@@ -1,0 +1,423 @@
+from contextlib import ExitStack
+
+import concourse.mybir as mybir
+from concourse.masks import make_identity
+
+FLOPS = 2 * 8192 * 4096 * 512
+
+F32 = mybir.dt.float32
+BF16 = mybir.dt.bfloat16
+U8 = mybir.dt.uint8
+I32 = mybir.dt.int32
+FP4 = mybir.dt.float4_e2m1fn_x4
+ALU = mybir.AluOpType
+ACT = mybir.ActivationFunctionType
+AX = mybir.AxisListType
+
+P = 128
+NT = 64
+PASSES = 8
+NB = 4
+XW = 530
+YW = 560
+RV = 7
+NWP = 252
+DELTA = [32 * (t // 3 - 1) + (t % 3 - 1) for t in range(9)]
+GLO = [max(57 * t - 1, 0) // 32 for t in range(9)]
+GHI = [min(57 * t + 56, 511) // 32 for t in range(9)]
+PAIRS = [(t, g) for t in range(9) for g in range(GLO[t], GHI[t] + 1)]
+COL = dict((pr, 9 * i) for i, pr in enumerate(PAIRS))
+WHOLE = [(0, 0), (2, 1), (4, 2), (6, 3), (9, 5), (11, 6), (13, 7), (15, 8)]
+SPLIT = [(1, 0), (3, 1), (5, 2), (7, 3), (8, 4), (10, 5), (12, 6), (14, 7)]
+START = [57 * t + 1 for t in range(9)]
+WID = [56] * 8 + [64]
+
+
+def tile_involution2d_pa_kernel(tc, x_words, x_scales, Wi_words, Wi_scales, bi, w_span, out):
+    nc = tc.nc
+    out_flat = out.flatten_outer_dims()
+    w_flat = w_span.flatten_outer_dims()
+
+    with ExitStack() as ctx:
+        sb = ctx.enter_context(tc.tile_pool(name="sb", bufs=1))
+        ps = ctx.enter_context(tc.psum_pool(name="ps", bufs=1))
+
+        wic = sb.tile([P, PASSES, 1024], U8, name="wic", align_bytes=64)
+        wis = sb.tile([P, PASSES, 512], U8, name="wis", align_bytes=64)
+        xcs = [sb.tile([P, PASSES, 1024], U8, name="xc%d" % i, align_bytes=64) for i in range(3)]
+        xss = [sb.tile([P, PASSES, 512], U8, name="xs%d" % i, align_bytes=64) for i in range(3)]
+        w_sb = sb.tile([P, NT, 144], BF16, name="w_sb")
+        bias_bf = sb.tile([P, 512], BF16, name="bias_bf")
+        ident = sb.tile([P, P], F32, name="ident")
+        e32 = sb.tile([P, 384], F32, name="e32")
+        ebf = [sb.tile([P, 384], BF16, name="ebf%d" % j) for j in range(3)]
+        edge = sb.tile([P, 2], F32, name="edge")
+        mask = sb.tile([P, 2], F32, name="mask")
+        zt = sb.tile([P, 64], F32, name="zt")
+        xps = [sb.tile([P, 2, XW], F32, name="xp%d" % i) for i in range(3)]
+        xrs = [sb.tile([P, 2, 9, 57], F32, name="xr%d" % i) for i in range(3)]
+        bias_r = sb.tile([P, 9, 56], BF16, name="bias_r")
+        wss = [sb.tile([P, 2, 72], F32, name="wS%d" % i) for i in range(3)]
+        pvs = [sb.tile([P, 2, 2376], F32, name="pv%d" % i) for i in range(2)]
+        pms = [sb.tile([P, 2, 9, 256], F32, name="pm%d" % i) for i in range(2)]
+        ys = [sb.tile([P, NB + 1, YW], F32, name="y%d" % i) for i in range(3)]
+        lsrc = sb.tile([P, NT + 2, 72], F32, name="lsrc")
+        gdep = sb.tile([P, 1], F32, name="gdep")
+        yt = sb.tile([P, 2, P], F32, name="yt")
+
+        xips = [ps.tile([P, 512], F32, name="xiP%d" % i) for i in range(3)]
+        wps = [ps.tile([P, 2, NWP], F32, name="wP%d" % i) for i in range(2)]
+        lsh = ps.tile([P, NB + 1, 72], F32, name="lsh")
+        acct = ps.tile([P, 2, P], F32, name="acct")
+        yb = ps.tile([P, 2, P], F32, name="yb")
+
+        def load_scales(dst, src, c0, c1):
+            for q in range(4):
+                nc.sync.dma_start(
+                    out=dst[32 * q:32 * q + 4, :, :].bitcast(I32),
+                    in_=src[:, 4 * q:4 * q + 4, c0:c1].rearrange("g r n -> r g n").bitcast(I32),
+                )
+
+        def load_chunk(c):
+            xc = xcs[c % 3]
+            xs = xss[c % 3]
+            nc.sync.dma_start(
+                out=xc[:].bitcast(I32),
+                in_=x_words[:, :, 1024 * c:1024 * (c + 1)].rearrange("g p n -> p g n").bitcast(I32),
+            )
+            load_scales(xs, x_scales, 512 * c, 512 * (c + 1))
+
+        def load_w(q):
+            nc.sync.dma_start(
+                out=w_sb[:, 8 * q:8 * q + 8, :],
+                in_=w_flat[1024 * q:1024 * (q + 1), :].rearrange("(n p) c -> p n c", p=P),
+            )
+
+        nc.vector.memset(wis[:].bitcast(I32), 0)
+        nc.vector.memset(xss[0][:].bitcast(I32), 0)
+        load_scales(wis, Wi_scales, 0, 512)
+        load_chunk(0)
+        for q in range(4):
+            nc.sync.dma_start(
+                out=wic[:, 2 * q:2 * q + 2, :].bitcast(I32),
+                in_=Wi_words[2 * q:2 * q + 2, :, :].rearrange("g p n -> p g n").bitcast(I32))
+        nc.scalar.dma_start(
+            out=w_sb[:, 0:8, :], in_=w_flat[0:1024, :].rearrange("(n p) c -> p n c", p=P))
+        nc.scalar.dma_start(out=bias_bf[:], in_=bi.partition_broadcast(P))
+
+        make_identity(nc, ident[:])
+        nc.vector.memset(e32[:], 0.0)
+        nc.vector.tensor_copy(out=e32[:, 128:256], in_=ident[:])
+        nc.vector.tensor_reduce(out=edge[:, 0:1], in_=ident[:, 0:128:32], axis=AX.X, op=ALU.add)
+        nc.vector.tensor_reduce(out=edge[:, 1:2], in_=ident[:, 31:128:32], axis=AX.X, op=ALU.add)
+        nc.vector.tensor_scalar(out=mask[:], in0=edge[:], scalar1=-1.0, scalar2=1.0, op0=ALU.mult, op1=ALU.add)
+        nc.vector.tensor_scalar(out=ebf[0][:], in0=e32[:], scalar1=mask[:, 0:1], scalar2=None, op0=ALU.mult)
+        nc.vector.tensor_copy(out=ebf[1][:], in_=e32[:])
+        nc.vector.tensor_scalar(out=ebf[2][:], in0=e32[:], scalar1=mask[:, 1:2], scalar2=None, op0=ALU.mult)
+        for i in range(3):
+            nc.vector.memset(xps[i][:], 0.0)
+        for i in range(1, 3):
+            nc.vector.memset(xss[i][:].bitcast(I32), 0)
+        nc.vector.memset(zt[:], 0.0)
+        nc.vector.memset(lsrc[:, 0, :], 0.0)
+        nc.vector.memset(lsrc[:, NT + 1, :], 0.0)
+        nc.vector.memset(ys[(NT // NB - 1) % 3][:, NB, :], 0.0)
+        nc.vector.tensor_copy(out=bias_r[:], in_=bias_bf[:, 0:504].rearrange("p (a r) -> p r a", r=9))
+
+        nu = NT // 2
+        nbat = NT // NB
+
+        def mx(u, k, g0, g1):
+            if not 0 <= u < nu:
+                return
+            xc = xcs[(u // 2) % 3]
+            xs = xss[(u // 2) % 3]
+            kk = 2 * (u % 2) + k
+            acc = xips[(2 * u + k) % 3]
+            for g in range(g0, g1):
+                nc.tensor.matmul_mx(
+                    out=acc[:],
+                    lhsT=xc[:, g, 256 * kk:256 * (kk + 1)].bitcast(FP4),
+                    lhsT_scale=xs[:, g, 128 * kk:128 * (kk + 1)],
+                    rhs=wic[:, g, :].bitcast(FP4),
+                    rhs_scale=wis[:, g, :],
+                    start=(g == 0),
+                    stop=(g == PASSES - 1),
+                )
+
+        def wshift(u):
+            if not 0 <= u < nu:
+                return
+            wp = wps[u % 2]
+            t0 = 2 * u
+            for t in range(9):
+                d = DELTA[t]
+                e = ebf[t % 3]
+                c0 = COL[(t, GLO[t])]
+                ncol = 9 * (GHI[t] - GLO[t] + 1)
+                w0 = 9 * GLO[t]
+                if t // 3 == 0:
+                    ks = [k for k in range(2) if (t0 + k) % 8 != 7]
+                    off, step = -d, 1
+                elif t // 3 == 2:
+                    ks = [k for k in range(2) if (t0 + k) % 8 != 0]
+                    off, step = 256 - d, -1
+                else:
+                    ks = []
+                    off, step = 0, 0
+                nc.tensor.matmul(
+                    out=wp[:, :, c0:c0 + ncol],
+                    lhsT=e[:, 128 - d:256 - d],
+                    rhs=w_sb[:, t0:t0 + 2, w0:w0 + ncol],
+                    start=True,
+                    stop=(len(ks) == 0),
+                )
+                if ks:
+                    nc.tensor.matmul(
+                        out=wp[:, ks[0]:ks[-1] + 1, c0:c0 + ncol],
+                        lhsT=e[:, off:off + 128],
+                        rhs=w_sb[:, t0 + ks[0] + step:t0 + ks[-1] + 1 + step, w0:w0 + ncol],
+                        start=False,
+                        stop=True,
+                    )
+
+        def bias(u):
+            if not 0 <= u < nu:
+                return
+            for k in range(2):
+                acc = xips[(2 * u + k) % 3]
+                nc.vector.tensor_tensor(out=xps[u % 3][:, k, 9:521], in0=acc[:], in1=bias_bf[:], op=ALU.add)
+                nc.vector.tensor_tensor(
+                    out=xrs[u % 3][:, k, 0:RV, 0:56], in0=acc[:, 0:504].rearrange("p (a r) -> p r a", r=9)[:, 0:RV, :],
+                    in1=bias_r[:, 0:RV, :], op=ALU.add)
+
+        def xrcopy(u):
+            if not 0 <= u < nu:
+                return
+            nc.scalar.copy(
+                out=xrs[u % 3][:, :, RV:9, :],
+                in_=xps[u % 3][:, :, 9:522].rearrange("p k (a r) -> p k r a", r=9)[:, :, RV:9, :])
+            nc.scalar.copy(out=xrs[u % 3][:, :, 0:RV, 56], in_=xps[u % 3][:, :, 513:513 + RV])
+
+        def wsevac(u):
+            if not 0 <= u < nu:
+                return
+            for k in range(2):
+                nc.scalar.copy(
+                    out=wss[u % 3][:, k, :].rearrange("p (h q c) -> p h q c", h=2, q=4),
+                    in_=wps[u % 2][:, k, :].rearrange("p (h x) -> p h x", x=126)[:, :, 0:108].rearrange(
+                        "p h (q c) -> p h q c", c=27)[:, :, :, 0:9],
+                )
+
+        def vmult(u):
+            if not 0 <= u < nu:
+                return
+            xp = xps[u % 3]
+            wp = wps[u % 2]
+            pv = pvs[u % 2]
+            for b, (g, ta) in [(i, SPLIT[i]) for i in (3, 4, 5, 6, 7, 0, 1, 2)]:
+                n1 = 57 * ta + 56 - 32 * g + 1
+                n2 = 33 - n1
+                segs = []
+                if not (g == 8):
+                    segs.append((ta, ta + 9 * (32 * g - 57 * ta + 1), n1, 33 * b))
+                if not (g == 7):
+                    segs.append((ta + 1, ta + 1, n2, 33 * b + n1))
+                for (t, a, n, o) in segs:
+                    cw = COL[(t, g)]
+                    nc.vector.tensor_tensor(
+                        out=pv[:, :, 9 * o:9 * (o + n)].rearrange("p k (s m) -> p k s m", m=9),
+                        in0=xp[:, :, a:a + 9 * n].rearrange("p k (s m) -> p k s m", m=9),
+                        in1=wp[:, :, cw:cw + 9].unsqueeze(2).to_broadcast([P, 2, n, 9]),
+                        op=ALU.mult,
+                    )
+                if g == 7:
+                    for k in range(2):
+                        cw = COL[(4, 7)]
+                        nc.vector.tensor_tensor(
+                            out=pv[:, k, 9 * 103:9 * 161].rearrange("p (h s m) -> p h s m", h=2, m=9),
+                            in0=xp[:, k, 4:4 + 522].rearrange("p (h s m) -> p h s m", h=2, m=9),
+                            in1=wp[:, k, cw:cw + 18].rearrange("p (h m) -> p h m", m=9).unsqueeze(2).to_broadcast(
+                                [P, 2, 29, 9]),
+                            op=ALU.mult,
+                        )
+
+        def vreduce(u):
+            if not 0 <= u < nu:
+                return
+            pv = pvs[u % 2]
+            y = ys[(u // 2) % 3]
+            s0 = 2 * (u % 2)
+            nc.vector.tensor_reduce(
+                out=y[:, s0:s0 + 2, 257:294],
+                in_=pv[:, :, 9 * 128:9 * 165].rearrange("p k (s m) -> p k s m", m=9),
+                axis=AX.X, op=ALU.add)
+            nc.vector.tensor_reduce(
+                out=y[:, s0:s0 + 2, 326:326 + 195].rearrange("p k (q c) -> p k q c", c=65)[:, :, :, 0:33],
+                in_=pv[:, :, 9 * 165:9 * 264].rearrange("p k (q s m) -> p k q s m", q=3, m=9),
+                axis=AX.X, op=ALU.add)
+
+        def smult(u, k):
+            if not 0 <= u < nu:
+                return
+            xr = xrs[u % 3]
+            ws = wss[u % 3]
+            pm = pms[u % 2]
+            for gi, (g, t) in enumerate(WHOLE):
+                c0 = 288 * g - 512 * t
+                for m in range(9):
+                    nc.scalar.activation(
+                        out=pm[:, k, m, 32 * gi:32 * gi + 32],
+                        in_=xr[:, k, (c0 + m) % 9, (c0 + m) // 9:(c0 + m) // 9 + 32],
+                        func=ACT.Copy,
+                        scale=ws[:, k, 9 * gi + m:9 * gi + m + 1],
+                    )
+
+        def fwd(u, k):
+            if not 0 <= u < nu:
+                return
+            pv = pvs[u % 2]
+            for m in range(9):
+                nc.tensor.matmul(
+                    out=acct[:, k, :], lhsT=pv[:, k, m:1152:9], rhs=ident[:],
+                    is_transpose=True, start=(m == 0), stop=(m == 8))
+
+        def evact(u):
+            if not 0 <= u < nu:
+                return
+            nc.scalar.copy(out=yt[:], in_=acct[:])
+
+        def back(u):
+            if not 0 <= u < nu:
+                return
+            for k in range(2):
+                nc.tensor.transpose(out=yb[:, k, :], in_=yt[:, k, :], identity=ident[:])
+
+        def evacy(u):
+            if not 0 <= u < nu:
+                return
+            y = ys[(u // 2) % 3]
+            s0 = 2 * (u % 2)
+            nc.scalar.copy(
+                out=y[:, s0:s0 + 2, 33:33 + 195].rearrange("p k (q c) -> p k q c", c=65)[:, :, :, 0:33],
+                in_=yb[:, :, 0:99].rearrange("p k (q c) -> p k q c", c=33))
+            nc.scalar.copy(out=y[:, s0:s0 + 2, 228:257], in_=yb[:, :, 99:128])
+
+        def gadds(u):
+            if not 0 <= u < nu:
+                return
+            pm = pms[u % 2]
+            y = ys[(u // 2) % 3]
+            s0 = 2 * (u % 2)
+            nc.gpsimd.tensor_tensor(out=pm[:, :, 0:4, :], in0=pm[:, :, 0:4, :], in1=pm[:, :, 4:8, :], op=ALU.add)
+            nc.gpsimd.tensor_tensor(out=pm[:, :, 0:2, :], in0=pm[:, :, 0:2, :], in1=pm[:, :, 2:4, :], op=ALU.add)
+            nc.gpsimd.tensor_tensor(out=pm[:, :, 0, :], in0=pm[:, :, 0, :], in1=pm[:, :, 1, :], op=ALU.add)
+            nc.gpsimd.tensor_copy(out=gdep[:], in_=y[:, s0 + 1, 326:327])
+            for h in (1, 0):
+                nc.gpsimd.tensor_tensor(
+                    out=y[:, s0:s0 + 2, 1 + 293 * h:1 + 293 * h + 260].rearrange(
+                        "p k (q c) -> p k q c", c=65)[:, :, :, 0:32],
+                    in0=pm[:, :, 0, 128 * h:128 * (h + 1)].rearrange("p k (q c) -> p k q c", c=32),
+                    in1=pm[:, :, 8, 128 * h:128 * (h + 1)].rearrange("p k (q c) -> p k q c", c=32),
+                    op=ALU.add,
+                )
+
+        def fin_a(b):
+            if not 0 <= b < nbat:
+                return
+            nc.scalar.copy(
+                out=lsrc[:, NB * b + 1:NB * b + 1 + NB, 0:64].rearrange("p n (t c) -> p n t c", c=8),
+                in_=ys[b % 3][:, 0:NB, 50:514].rearrange("p n (t c) -> p n t c", c=58)[:, :, :, 0:8],
+            )
+
+        def fin_b(b):
+            if not 0 <= b < nbat:
+                return
+            t0 = NB * b
+            n = NB + (1 if b == nbat - 1 else 0)
+            cur = lsrc[:, t0 + 1:t0 + 1 + n, :].rearrange("p n (a b) -> p n a b", b=24)
+            prv = lsrc[:, t0:t0 + n, :].rearrange("p n (a b) -> p n a b", b=24)
+            l4 = lsh[:, 0:n, :].rearrange("p n (a b) -> p n a b", b=24)
+            nc.tensor.matmul(out=l4[:, :, :, 0:16], lhsT=e32[:, 127:255], rhs=cur[:, :, :, 0:16], start=True, stop=False)
+            nc.tensor.matmul(out=l4[:, :, :, 0:16], lhsT=e32[:, 255:383], rhs=prv[:, :, :, 0:16], start=False, stop=True)
+            nc.tensor.matmul(out=l4[:, :, 0:2, 16:24], lhsT=e32[:, 98:226], rhs=cur[:, :, 0:2, 16:24], start=True, stop=False)
+            nc.tensor.matmul(out=l4[:, :, 0:2, 16:24], lhsT=e32[:, 226:354], rhs=prv[:, :, 0:2, 16:24], start=False, stop=True)
+
+        def fin_c(b):
+            if not 0 <= b < nbat:
+                return
+            t0 = NB * b
+            n = NB + (1 if b == nbat - 1 else 0)
+            y = ys[b % 3]
+            for t in range(2, 9):
+                nc.scalar.copy(
+                    out=y[:, 0:n, 57 * t + 1:58 * t],
+                    in_=lsh[:, 0:n, 8 * (t - 1) + 8 - t:8 * (t - 1) + 7],
+                )
+            nc.vector.tensor_tensor(
+                out=y[:, 0:n, 58:465:58], in0=lsh[:, 0:n, 7:64:8], in1=y[:, 0:n, 58:465:58], op=ALU.add)
+            for t in range(9):
+                d = DELTA[t]
+                c0 = 56 * t
+                wd = WID[t]
+                st = START[t]
+                k0, k1 = 0, NB
+                if b == 0 and d > 0:
+                    nc.sync.dma_start(out=out_flat[0:P - d, c0:c0 + wd], in_=y[d:P, 0, st:st + wd])
+                    k0 = 1
+                if b == nbat - 1 and d < 0:
+                    r0 = P * (NT - 1) - d
+                    nc.sync.dma_start(out=out_flat[r0:P * NT, c0:c0 + wd], in_=y[0:P + d, NB - 1, st:st + wd])
+                    k1 = NB - 1
+                if b == nbat - 1 and d > 1:
+                    nc.sync.dma_start(out=out_flat[P * NT - d:P * NT, c0:c0 + wd], in_=y[0:d, NB, st:st + wd])
+                if b == nbat - 1 and d == 1:
+                    nc.sync.dma_start(
+                        out=out_flat[P * NT - 1:P * NT, c0:c0 + wd].rearrange("o (a c) -> (o a) c", c=8),
+                        in_=y[0:7, NB, st:st + 8],
+                    )
+                r0 = P * (t0 + k0) - d
+                nc.sync.dma_start(
+                    out=out_flat[r0:r0 + P * (k1 - k0), c0:c0 + wd].rearrange("(n p) c -> p n c", p=P),
+                    in_=y[:, k0:k1, st:st + wd],
+                )
+
+        for t in range(9):
+            if DELTA[t] < -1:
+                nc.sync.dma_start(out=out_flat[0:-DELTA[t], 56 * t:56 * t + WID[t]], in_=zt[0:-DELTA[t], 0:WID[t]])
+            if DELTA[t] == -1:
+                nc.sync.dma_start(
+                    out=out_flat[0:1, 56 * t:56 * t + WID[t]].rearrange("o (a c) -> (o a) c", c=8),
+                    in_=zt[0:7, 0:8],
+                )
+
+        with tc.manual_schedule():
+            for u in range(-2, nu + 3):
+                if u < 0:
+                    load_chunk(u + 3)
+                if u >= 0 and u % 2 == 0 and u // 2 + 3 < nbat:
+                    load_chunk(u // 2 + 3)
+                if u % 4 == 2 and (u + 2) // 4 + 1 < 8:
+                    load_w((u + 2) // 4 + 1)
+                fwd(u - 1, 0)
+                bias(u + 1)
+                mx(u + 2, 0, 0, 8)
+                fwd(u - 1, 1)
+                wsevac(u + 1)
+                if u % 2 == 1:
+                    fin_a((u - 3) // 2)
+                    fin_b((u - 3) // 2)
+                else:
+                    fin_c((u - 4) // 2)
+                vmult(u)
+                vreduce(u)
+                smult(u, 0)
+                xrcopy(u + 1)
+                evact(u - 1)
+                back(u - 1)
+                mx(u + 2, 1, 0, 4)
+                wshift(u + 2)
+                mx(u + 2, 1, 4, 8)
+                smult(u, 1)
+                evacy(u - 1)
+                gadds(u)

@@ -266,6 +266,8 @@ def tile_involution2d_pa_kernel(tc, x_words, x_scales, Wi_words, Wi_scales, bi, 
             for gi, (g, t) in enumerate(WHOLE):
                 c0 = 288 * g - 512 * t
                 for m in range(9):
+                    if k == 1 and gi == 7 and m == 8:
+                        nc.scalar.copy(out=gdep[:], in_=ys[(u // 2) % 3][:, 2 * (u % 2) + 1, 326:327])
                     nc.scalar.activation(
                         out=pm[:, k, m, 32 * gi:32 * gi + 32],
                         in_=xr[:, k, (c0 + m) % 9, (c0 + m) // 9:(c0 + m) // 9 + 32],
@@ -312,7 +314,6 @@ def tile_involution2d_pa_kernel(tc, x_words, x_scales, Wi_words, Wi_scales, bi, 
             nc.gpsimd.tensor_tensor(out=pm[:, :, 0:4, :], in0=pm[:, :, 0:4, :], in1=pm[:, :, 4:8, :], op=ALU.add)
             nc.gpsimd.tensor_tensor(out=pm[:, :, 0:2, :], in0=pm[:, :, 0:2, :], in1=pm[:, :, 2:4, :], op=ALU.add)
             nc.gpsimd.tensor_tensor(out=pm[:, :, 0, :], in0=pm[:, :, 0, :], in1=pm[:, :, 1, :], op=ALU.add)
-            nc.gpsimd.tensor_copy(out=gdep[:], in_=y[:, s0 + 1, 326:327])
             for h in (1, 0):
                 nc.gpsimd.tensor_tensor(
                     out=y[:, s0:s0 + 2, 1 + 293 * h:1 + 293 * h + 260].rearrange(
@@ -350,7 +351,7 @@ def tile_involution2d_pa_kernel(tc, x_words, x_scales, Wi_words, Wi_scales, bi, 
             n = NB + (1 if b == nbat - 1 else 0)
             y = ys[b % 3]
             for t in range(2, 9):
-                nc.scalar.copy(
+                nc.vector.tensor_copy(
                     out=y[:, 0:n, 57 * t + 1:58 * t],
                     in_=lsh[:, 0:n, 8 * (t - 1) + 8 - t:8 * (t - 1) + 7],
                 )

@@ -26,7 +26,8 @@ DELTA = [32 * (t // 3 - 1) + (t % 3 - 1) for t in range(9)]
 GLO = [max(57 * t - 1, 0) // 32 for t in range(9)]
 GHI = [min(57 * t + 56, 511) // 32 for t in range(9)]
 PAIRS = [(t, g) for t in range(9) for g in range(GLO[t], GHI[t] + 1)]
-COL = dict((pr, 9 * i) for i, pr in enumerate(PAIRS))
+WTP = 28
+COL = dict(((t, g), WTP * t + 9 * (g - GLO[t])) for (t, g) in PAIRS)
 WHOLE = [(0, 0), (2, 1), (4, 2), (6, 3), (9, 5), (11, 6), (13, 7), (15, 8)]
 SPLIT = [(1, 0), (3, 1), (5, 2), (7, 3), (8, 4), (10, 5), (12, 6), (14, 7)]
 START = [57 * t + 1 for t in range(9)]
@@ -46,7 +47,7 @@ def tile_involution2d_pa_kernel(tc, x_words, x_scales, Wi_words, Wi_scales, bi, 
         wis = sb.tile([P, PASSES, 512], U8, name="wis", align_bytes=64)
         xcs = [sb.tile([P, PASSES, 1024], U8, name="xc%d" % i, align_bytes=64) for i in range(3)]
         xss = [sb.tile([P, PASSES, 512], U8, name="xs%d" % i, align_bytes=64) for i in range(3)]
-        w_sb = sb.tile([P, NT, 144], BF16, name="w_sb")
+        w_sb = sb.tile([P, 3 * 8, 144], BF16, name="w_sb")
         bias_bf = sb.tile([P, 512], BF16, name="bias_bf")
         ident = sb.tile([P, P], F32, name="ident")
         e32 = sb.tile([P, 384], F32, name="e32")
@@ -57,16 +58,16 @@ def tile_involution2d_pa_kernel(tc, x_words, x_scales, Wi_words, Wi_scales, bi, 
         xps = [sb.tile([P, 2, XW], F32, name="xp%d" % i) for i in range(3)]
         xrs = [sb.tile([P, 2, 9, 57], F32, name="xr%d" % i) for i in range(3)]
         bias_r = sb.tile([P, 9, 56], BF16, name="bias_r")
-        wss = [sb.tile([P, 2, 72], F32, name="wS%d" % i) for i in range(3)]
+        wss = [sb.tile([P, 2, 81], F32, name="wS%d" % i) for i in range(3)]
         pvs = [sb.tile([P, 2, 2376], F32, name="pv%d" % i) for i in range(2)]
-        pms = [sb.tile([P, 2, 9, 256], F32, name="pm%d" % i) for i in range(2)]
+        pms = [sb.tile([P, NB, 9, 256], F32, name="pm%d" % i) for i in range(2)]
         ys = [sb.tile([P, NB + 1, YW], F32, name="y%d" % i) for i in range(3)]
-        lsrc = sb.tile([P, NT + 2, 72], F32, name="lsrc")
+        lbs = [sb.tile([P, NB + 2, 72], F32, name="lb%d" % i) for i in range(2)]
         gdep = sb.tile([P, 1], F32, name="gdep")
         yt = sb.tile([P, 2, P], F32, name="yt")
 
         xips = [ps.tile([P, 512], F32, name="xiP%d" % i) for i in range(3)]
-        wps = [ps.tile([P, 2, NWP], F32, name="wP%d" % i) for i in range(2)]
+        wps = [ps.tile([P, NB, NWP], BF16, name="wP%d" % i) for i in range(2)]
         lsh = ps.tile([P, NB + 1, 72], F32, name="lsh")
         acct = ps.tile([P, 2, P], F32, name="acct")
         yb = ps.tile([P, 2, P], F32, name="yb")
@@ -89,7 +90,7 @@ def tile_involution2d_pa_kernel(tc, x_words, x_scales, Wi_words, Wi_scales, bi, 
 
         def load_w(q):
             nc.sync.dma_start(
-                out=w_sb[:, 8 * q:8 * q + 8, :],
+                out=w_sb[:, 8 * (q % 3):8 * (q % 3) + 8, :],
                 in_=w_flat[1024 * q:1024 * (q + 1), :].rearrange("(n p) c -> p n c", p=P),
             )
 
@@ -119,8 +120,8 @@ def tile_involution2d_pa_kernel(tc, x_words, x_scales, Wi_words, Wi_scales, bi, 
         for i in range(1, 3):
             nc.vector.memset(xss[i][:].bitcast(I32), 0)
         nc.vector.memset(zt[:], 0.0)
-        nc.vector.memset(lsrc[:, 0, :], 0.0)
-        nc.vector.memset(lsrc[:, NT + 1, :], 0.0)
+        nc.vector.memset(lbs[0][:, 0, :], 0.0)
+        nc.vector.memset(lbs[(NT // NB - 1) % 2][:, NB + 1, :], 0.0)
         nc.vector.memset(ys[(NT // NB - 1) % 3][:, NB, :], 0.0)
         nc.vector.tensor_copy(out=bias_r[:], in_=bias_bf[:, 0:504].rearrange("p (a r) -> p r a", r=9))
 
@@ -145,11 +146,12 @@ def tile_involution2d_pa_kernel(tc, x_words, x_scales, Wi_words, Wi_scales, bi, 
                     stop=(g == PASSES - 1),
                 )
 
-        def wshift(u):
-            if not 0 <= u < nu:
+        def wshift(b):
+            if not 0 <= b < nbat:
                 return
-            wp = wps[u % 2]
-            t0 = 2 * u
+            wp = wps[b % 2]
+            t0 = NB * b
+            w0t = 8 * ((t0 // 8) % 3) + t0 % 8
             for t in range(9):
                 d = DELTA[t]
                 e = ebf[t % 3]
@@ -157,10 +159,10 @@ def tile_involution2d_pa_kernel(tc, x_words, x_scales, Wi_words, Wi_scales, bi, 
                 ncol = 9 * (GHI[t] - GLO[t] + 1)
                 w0 = 9 * GLO[t]
                 if t // 3 == 0:
-                    ks = [k for k in range(2) if (t0 + k) % 8 != 7]
+                    ks = [k for k in range(NB) if (t0 + k) % 8 != 7]
                     off, step = -d, 1
                 elif t // 3 == 2:
-                    ks = [k for k in range(2) if (t0 + k) % 8 != 0]
+                    ks = [k for k in range(NB) if (t0 + k) % 8 != 0]
                     off, step = 256 - d, -1
                 else:
                     ks = []
@@ -168,7 +170,7 @@ def tile_involution2d_pa_kernel(tc, x_words, x_scales, Wi_words, Wi_scales, bi, 
                 nc.tensor.matmul(
                     out=wp[:, :, c0:c0 + ncol],
                     lhsT=e[:, 128 - d:256 - d],
-                    rhs=w_sb[:, t0:t0 + 2, w0:w0 + ncol],
+                    rhs=w_sb[:, w0t:w0t + NB, w0:w0 + ncol],
                     start=True,
                     stop=(len(ks) == 0),
                 )
@@ -176,7 +178,7 @@ def tile_involution2d_pa_kernel(tc, x_words, x_scales, Wi_words, Wi_scales, bi, 
                     nc.tensor.matmul(
                         out=wp[:, ks[0]:ks[-1] + 1, c0:c0 + ncol],
                         lhsT=e[:, off:off + 128],
-                        rhs=w_sb[:, t0 + ks[0] + step:t0 + ks[-1] + 1 + step, w0:w0 + ncol],
+                        rhs=w_sb[:, w0t + ks[0] + step:w0t + ks[-1] + 1 + step, w0:w0 + ncol],
                         start=False,
                         stop=True,
                     )
@@ -202,18 +204,16 @@ def tile_involution2d_pa_kernel(tc, x_words, x_scales, Wi_words, Wi_scales, bi, 
         def wsevac(u):
             if not 0 <= u < nu:
                 return
-            for k in range(2):
-                nc.scalar.copy(
-                    out=wss[u % 3][:, k, :].rearrange("p (h q c) -> p h q c", h=2, q=4),
-                    in_=wps[u % 2][:, k, :].rearrange("p (h x) -> p h x", x=126)[:, :, 0:108].rearrange(
-                        "p h (q c) -> p h q c", c=27)[:, :, :, 0:9],
-                )
+            wp4 = wps[(u // 2) % 2][:, 2 * (u % 2):2 * (u % 2) + 2, :].rearrange("p k (t x) -> p k t x", x=WTP)
+            nc.scalar.copy(out=wss[u % 3][:, :, 0:9], in_=wp4[:, :, 0, 0:9])
+            nc.scalar.copy(
+                out=wss[u % 3][:, :, 9:81].rearrange("p k (t c) -> p k t c", c=9), in_=wp4[:, :, 1:9, 9:18])
 
         def vmult(u):
             if not 0 <= u < nu:
                 return
             xp = xps[u % 3]
-            wp = wps[u % 2]
+            wp = wps[(u // 2) % 2][:, 2 * (u % 2):2 * (u % 2) + 2, :]
             pv = pvs[u % 2]
             for b, (g, ta) in [(i, SPLIT[i]) for i in (3, 4, 5, 6, 7, 0, 1, 2)]:
                 n1 = 57 * ta + 56 - 32 * g + 1
@@ -262,17 +262,18 @@ def tile_involution2d_pa_kernel(tc, x_words, x_scales, Wi_words, Wi_scales, bi, 
                 return
             xr = xrs[u % 3]
             ws = wss[u % 3]
-            pm = pms[u % 2]
+            pm = pms[(u // 2) % 2]
+            kk = 2 * (u % 2) + k
             for gi, (g, t) in enumerate(WHOLE):
                 c0 = 288 * g - 512 * t
                 for m in range(9):
-                    if k == 1 and gi == 7 and m == 8:
-                        nc.scalar.copy(out=gdep[:], in_=ys[(u // 2) % 3][:, 2 * (u % 2) + 1, 326:327])
+                    if (kk == NB - 1 or (kk == 1 and u // 2 == nbat - 1)) and gi == 7 and m == 8:
+                        nc.scalar.copy(out=gdep[:], in_=ys[(u // 2) % 3][:, kk, 326:327])
                     nc.scalar.activation(
-                        out=pm[:, k, m, 32 * gi:32 * gi + 32],
+                        out=pm[:, kk, m, 32 * gi:32 * gi + 32],
                         in_=xr[:, k, (c0 + m) % 9, (c0 + m) // 9:(c0 + m) // 9 + 32],
                         func=ACT.Copy,
-                        scale=ws[:, k, 9 * gi + m:9 * gi + m + 1],
+                        scale=ws[:, k, 9 * t + m:9 * t + m + 1],
                     )
 
         def fwd(u, k):
@@ -305,18 +306,17 @@ def tile_involution2d_pa_kernel(tc, x_words, x_scales, Wi_words, Wi_scales, bi, 
                 in_=yb[:, :, 0:99].rearrange("p k (q c) -> p k q c", c=33))
             nc.scalar.copy(out=y[:, s0:s0 + 2, 228:257], in_=yb[:, :, 99:128])
 
-        def gadds(u):
-            if not 0 <= u < nu:
+        def gadds(b, n0, n1):
+            if not 0 <= b < nbat:
                 return
-            pm = pms[u % 2]
-            y = ys[(u // 2) % 3]
-            s0 = 2 * (u % 2)
+            pm = pms[b % 2][:, n0:n1, :, :]
+            y = ys[b % 3]
             nc.gpsimd.tensor_tensor(out=pm[:, :, 0:4, :], in0=pm[:, :, 0:4, :], in1=pm[:, :, 4:8, :], op=ALU.add)
             nc.gpsimd.tensor_tensor(out=pm[:, :, 0:2, :], in0=pm[:, :, 0:2, :], in1=pm[:, :, 2:4, :], op=ALU.add)
             nc.gpsimd.tensor_tensor(out=pm[:, :, 0, :], in0=pm[:, :, 0, :], in1=pm[:, :, 1, :], op=ALU.add)
             for h in (1, 0):
                 nc.gpsimd.tensor_tensor(
-                    out=y[:, s0:s0 + 2, 1 + 293 * h:1 + 293 * h + 260].rearrange(
+                    out=y[:, n0:n1, 1 + 293 * h:1 + 293 * h + 260].rearrange(
                         "p k (q c) -> p k q c", c=65)[:, :, :, 0:32],
                     in0=pm[:, :, 0, 128 * h:128 * (h + 1)].rearrange("p k (q c) -> p k q c", c=32),
                     in1=pm[:, :, 8, 128 * h:128 * (h + 1)].rearrange("p k (q c) -> p k q c", c=32),
@@ -327,17 +327,22 @@ def tile_involution2d_pa_kernel(tc, x_words, x_scales, Wi_words, Wi_scales, bi, 
             if not 0 <= b < nbat:
                 return
             nc.scalar.copy(
-                out=lsrc[:, NB * b + 1:NB * b + 1 + NB, 0:64].rearrange("p n (t c) -> p n t c", c=8),
+                out=lbs[b % 2][:, 1:1 + NB, 0:64].rearrange("p n (t c) -> p n t c", c=8),
                 in_=ys[b % 3][:, 0:NB, 50:514].rearrange("p n (t c) -> p n t c", c=58)[:, :, :, 0:8],
             )
+            if b + 1 < nbat:
+                nc.scalar.copy(
+                    out=lbs[(b + 1) % 2][:, 0, 0:64].rearrange("p (t c) -> p t c", c=8),
+                    in_=ys[b % 3][:, NB - 1, 50:514].rearrange("p (t c) -> p t c", c=58)[:, :, 0:8],
+                )
 
         def fin_b(b):
             if not 0 <= b < nbat:
                 return
             t0 = NB * b
             n = NB + (1 if b == nbat - 1 else 0)
-            cur = lsrc[:, t0 + 1:t0 + 1 + n, :].rearrange("p n (a b) -> p n a b", b=24)
-            prv = lsrc[:, t0:t0 + n, :].rearrange("p n (a b) -> p n a b", b=24)
+            cur = lbs[b % 2][:, 1:1 + n, :].rearrange("p n (a b) -> p n a b", b=24)
+            prv = lbs[b % 2][:, 0:n, :].rearrange("p n (a b) -> p n a b", b=24)
             l4 = lsh[:, 0:n, :].rearrange("p n (a b) -> p n a b", b=24)
             nc.tensor.matmul(out=l4[:, :, :, 0:16], lhsT=e32[:, 127:255], rhs=cur[:, :, :, 0:16], start=True, stop=False)
             nc.tensor.matmul(out=l4[:, :, :, 0:16], lhsT=e32[:, 255:383], rhs=prv[:, :, :, 0:16], start=False, stop=True)
@@ -351,7 +356,7 @@ def tile_involution2d_pa_kernel(tc, x_words, x_scales, Wi_words, Wi_scales, bi, 
             n = NB + (1 if b == nbat - 1 else 0)
             y = ys[b % 3]
             for t in range(2, 9):
-                nc.vector.tensor_copy(
+                nc.scalar.copy(
                     out=y[:, 0:n, 57 * t + 1:58 * t],
                     in_=lsh[:, 0:n, 8 * (t - 1) + 8 - t:8 * (t - 1) + 7],
                 )
@@ -393,7 +398,7 @@ def tile_involution2d_pa_kernel(tc, x_words, x_scales, Wi_words, Wi_scales, bi, 
                 )
 
         with tc.manual_schedule():
-            for u in range(-2, nu + 3):
+            for u in range(-2, nu + 4):
                 if u < 0:
                     load_chunk(u + 3)
                 if u >= 0 and u % 2 == 0 and u // 2 + 3 < nbat:
@@ -405,20 +410,24 @@ def tile_involution2d_pa_kernel(tc, x_words, x_scales, Wi_words, Wi_scales, bi, 
                 mx(u + 2, 0, 0, 8)
                 fwd(u - 1, 1)
                 wsevac(u + 1)
-                if u % 2 == 1:
-                    fin_a((u - 3) // 2)
-                    fin_b((u - 3) // 2)
+                if u % 2 == 0:
+                    fin_a((u - 4) // 2)
+                    fin_b((u - 4) // 2)
                 else:
-                    fin_c((u - 4) // 2)
+                    fin_c((u - 5) // 2)
                 vmult(u)
                 vreduce(u)
                 smult(u, 0)
                 xrcopy(u + 1)
                 evact(u - 1)
-                back(u - 1)
                 mx(u + 2, 1, 0, 4)
-                wshift(u + 2)
+                back(u - 1)
+                if u % 2 == 0:
+                    wshift((u + 2) // 2)
                 mx(u + 2, 1, 4, 8)
                 smult(u, 1)
                 evacy(u - 1)
-                gadds(u)
+                if u // 2 == nbat - 1:
+                    gadds(u // 2, 2 * (u % 2), 2 * (u % 2) + 2)
+                elif u % 2 == 1:
+                    gadds(u // 2, 0, NB)

@@ -65,6 +65,7 @@ def tile_involution2d_pa_kernel(tc, x_words, x_scales, Wi_words, Wi_scales, bi, 
         lbs = [sb.tile([P, NB + 2, 72], F32, name="lb%d" % i) for i in range(2)]
         gdep = sb.tile([P, 1], F32, name="gdep")
         yt = sb.tile([P, 2, P], F32, name="yt")
+        yts = sb.tile([P, 4 * P], F32, name="yts")
 
         xips = [ps.tile([P, 512], F32, name="xiP%d" % i) for i in range(3)]
         wps = [ps.tile([P, NB, NWP], BF16, name="wP%d" % i) for i in range(2)]
@@ -267,7 +268,7 @@ def tile_involution2d_pa_kernel(tc, x_words, x_scales, Wi_words, Wi_scales, bi, 
             for gi, (g, t) in enumerate(WHOLE):
                 c0 = 288 * g - 512 * t
                 for m in range(9):
-                    if (kk == NB - 1 or (kk == 1 and u // 2 == nbat - 1)) and gi == 7 and m == 8:
+                    if kk == NB - 1 and u // 2 < nbat - 1 and gi == 7 and m == 8:
                         nc.scalar.copy(out=gdep[:], in_=ys[(u // 2) % 3][:, kk, 326:327])
                     nc.scalar.activation(
                         out=pm[:, kk, m, 32 * gi:32 * gi + 32],
@@ -284,6 +285,35 @@ def tile_involution2d_pa_kernel(tc, x_words, x_scales, Wi_words, Wi_scales, bi, 
                 nc.tensor.matmul(
                     out=acct[:, k, :], lhsT=pv[:, k, m:1152:9], rhs=ident[:],
                     is_transpose=True, start=(m == 0), stop=(m == 8))
+
+        def tail(u):
+            return 0 <= u < nu and u // 2 == nbat - 1
+
+        def fwd_s(u):
+            if tail(u):
+                for c in range(4):
+                    for m in range(9):
+                        nc.tensor.matmul(
+                            out=xips[1][:, P * c:P * (c + 1)], lhsT=pms[(u // 2) % 2][:, 2 * (u % 2) + c // 2, m, P * (c % 2):P * (c % 2 + 1)],
+                            rhs=ident[:], is_transpose=True, start=(m == 0), stop=(m == 8))
+
+        def evact_s(u):
+            if tail(u):
+                nc.vector.tensor_copy(out=yts[:], in_=xips[1][:])
+
+        def back_s(u):
+            if tail(u):
+                for c in range(4):
+                    nc.tensor.transpose(out=xips[2][:, P * c:P * (c + 1)], in_=yts[:, P * c:P * (c + 1)], identity=ident[:])
+
+        def evacy_s(u):
+            if tail(u):
+                s0 = 2 * (u % 2)
+                for h in range(2):
+                    nc.scalar.copy(
+                        out=ys[(u // 2) % 3][:, s0:s0 + 2, 1 + 293 * h:1 + 293 * h + 260].rearrange(
+                            "p k (q c) -> p k q c", c=65)[:, :, :, 0:32],
+                        in_=xips[2][:].rearrange("p (k h q c) -> p k h q c", k=2, h=2, c=32)[:, :, h, :, :])
 
         def evact(u):
             if not 0 <= u < nu:
@@ -409,6 +439,7 @@ def tile_involution2d_pa_kernel(tc, x_words, x_scales, Wi_words, Wi_scales, bi, 
                 bias(u + 1)
                 mx(u + 2, 0, 0, 8)
                 fwd(u - 1, 1)
+                fwd_s(u - 1)
                 wsevac(u + 1)
                 if u % 2 == 0:
                     fin_a((u - 4) // 2)
@@ -420,14 +451,15 @@ def tile_involution2d_pa_kernel(tc, x_words, x_scales, Wi_words, Wi_scales, bi, 
                 smult(u, 0)
                 xrcopy(u + 1)
                 evact(u - 1)
+                evact_s(u - 1)
                 mx(u + 2, 1, 0, 4)
                 back(u - 1)
+                back_s(u - 1)
                 if u % 2 == 0:
                     wshift((u + 2) // 2)
                 mx(u + 2, 1, 4, 8)
                 smult(u, 1)
                 evacy(u - 1)
-                if u // 2 == nbat - 1:
-                    gadds(u // 2, 2 * (u % 2), 2 * (u % 2) + 2)
-                elif u % 2 == 1:
+                evacy_s(u - 1)
+                if u % 2 == 1 and u // 2 < nbat - 1:
                     gadds(u // 2, 0, NB)

@@ -58,7 +58,7 @@ def tile_involution2d_pa_kernel(tc, x_words, x_scales, Wi_words, Wi_scales, bi, 
         xps = [sb.tile([P, 2, XW], F32, name="xp%d" % i) for i in range(3)]
         xrs = [sb.tile([P, 2, 9, 57], F32, name="xr%d" % i) for i in range(3)]
         bias_r = sb.tile([P, 9, 56], BF16, name="bias_r")
-        wss = [sb.tile([P, 2, 81], F32, name="wS%d" % i) for i in range(3)]
+        wss = [sb.tile([P, NB, 81], F32, name="wS%d" % i) for i in range(2)]
         pvs = [sb.tile([P, 2, 2376], F32, name="pv%d" % i) for i in range(2)]
         pms = [sb.tile([P, NB, 9, 256], F32, name="pm%d" % i) for i in range(2)]
         ys = [sb.tile([P, NB + 1, YW], F32, name="y%d" % i) for i in range(3)]
@@ -194,21 +194,21 @@ def tile_involution2d_pa_kernel(tc, x_words, x_scales, Wi_words, Wi_scales, bi, 
                     out=xrs[u % 3][:, k, 0:RV, 0:56], in0=acc[:, 0:504].rearrange("p (a r) -> p r a", r=9)[:, 0:RV, :],
                     in1=bias_r[:, 0:RV, :], op=ALU.add)
 
-        def xrcopy(u):
+        def xrcopy(u, k0=0, k1=2):
             if not 0 <= u < nu:
                 return
             nc.scalar.copy(
-                out=xrs[u % 3][:, :, RV:9, :],
-                in_=xps[u % 3][:, :, 9:522].rearrange("p k (a r) -> p k r a", r=9)[:, :, RV:9, :])
-            nc.scalar.copy(out=xrs[u % 3][:, :, 0:RV, 56], in_=xps[u % 3][:, :, 513:513 + RV])
+                out=xrs[u % 3][:, k0:k1, RV:9, :],
+                in_=xps[u % 3][:, k0:k1, 9:522].rearrange("p k (a r) -> p k r a", r=9)[:, :, RV:9, :])
+            nc.scalar.copy(out=xrs[u % 3][:, k0:k1, 0:RV, 56], in_=xps[u % 3][:, k0:k1, 513:513 + RV])
 
-        def wsevac(u):
-            if not 0 <= u < nu:
+        def wsevac(b):
+            if not 0 <= b < nbat:
                 return
-            wp4 = wps[(u // 2) % 2][:, 2 * (u % 2):2 * (u % 2) + 2, :].rearrange("p k (t x) -> p k t x", x=WTP)
-            nc.scalar.copy(out=wss[u % 3][:, :, 0:9], in_=wp4[:, :, 0, 0:9])
+            wp4 = wps[b % 2][:].rearrange("p k (t x) -> p k t x", x=WTP)
+            nc.scalar.copy(out=wss[b % 2][:, :, 0:9], in_=wp4[:, :, 0, 0:9])
             nc.scalar.copy(
-                out=wss[u % 3][:, :, 9:81].rearrange("p k (t c) -> p k t c", c=9), in_=wp4[:, :, 1:9, 9:18])
+                out=wss[b % 2][:, :, 9:81].rearrange("p k (t c) -> p k t c", c=9), in_=wp4[:, :, 1:9, 9:18])
 
         def vmult(u):
             if not 0 <= u < nu:
@@ -262,19 +262,17 @@ def tile_involution2d_pa_kernel(tc, x_words, x_scales, Wi_words, Wi_scales, bi, 
             if not 0 <= u < nu:
                 return
             xr = xrs[u % 3]
-            ws = wss[u % 3]
+            ws = wss[(u // 2) % 2]
             pm = pms[(u // 2) % 2]
             kk = 2 * (u % 2) + k
             for gi, (g, t) in enumerate(WHOLE):
                 c0 = 288 * g - 512 * t
                 for m in range(9):
-                    if kk == NB - 1 and u // 2 < nbat - 1 and gi == 7 and m == 8:
-                        nc.scalar.copy(out=gdep[:], in_=ys[(u // 2) % 3][:, kk, 326:327])
                     nc.scalar.activation(
                         out=pm[:, kk, m, 32 * gi:32 * gi + 32],
                         in_=xr[:, k, (c0 + m) % 9, (c0 + m) // 9:(c0 + m) // 9 + 32],
                         func=ACT.Copy,
-                        scale=ws[:, k, 9 * t + m:9 * t + m + 1],
+                        scale=ws[:, kk, 9 * t + m:9 * t + m + 1],
                     )
 
         def fwd(u, k):
@@ -344,6 +342,7 @@ def tile_involution2d_pa_kernel(tc, x_words, x_scales, Wi_words, Wi_scales, bi, 
             nc.gpsimd.tensor_tensor(out=pm[:, :, 0:4, :], in0=pm[:, :, 0:4, :], in1=pm[:, :, 4:8, :], op=ALU.add)
             nc.gpsimd.tensor_tensor(out=pm[:, :, 0:2, :], in0=pm[:, :, 0:2, :], in1=pm[:, :, 2:4, :], op=ALU.add)
             nc.gpsimd.tensor_tensor(out=pm[:, :, 0, :], in0=pm[:, :, 0, :], in1=pm[:, :, 1, :], op=ALU.add)
+            nc.gpsimd.tensor_copy(out=gdep[:], in_=y[:, n1 - 1, 326:327])
             for h in (1, 0):
                 nc.gpsimd.tensor_tensor(
                     out=y[:, n0:n1, 1 + 293 * h:1 + 293 * h + 260].rearrange(
@@ -428,6 +427,7 @@ def tile_involution2d_pa_kernel(tc, x_words, x_scales, Wi_words, Wi_scales, bi, 
                 )
 
         with tc.manual_schedule():
+            wshift(0)
             for u in range(-2, nu + 4):
                 if u < 0:
                     load_chunk(u + 3)
@@ -440,7 +440,8 @@ def tile_involution2d_pa_kernel(tc, x_words, x_scales, Wi_words, Wi_scales, bi, 
                 mx(u + 2, 0, 0, 8)
                 fwd(u - 1, 1)
                 fwd_s(u - 1)
-                wsevac(u + 1)
+                if u % 2 == 1:
+                    wsevac((u + 1) // 2)
                 if u % 2 == 0:
                     fin_a((u - 4) // 2)
                     fin_b((u - 4) // 2)
@@ -449,13 +450,19 @@ def tile_involution2d_pa_kernel(tc, x_words, x_scales, Wi_words, Wi_scales, bi, 
                 vmult(u)
                 vreduce(u)
                 smult(u, 0)
-                xrcopy(u + 1)
+                if u == -1:
+                    xrcopy(0, 0, 1)
+                elif u == 0:
+                    xrcopy(0, 1, 2)
+                    xrcopy(1)
+                else:
+                    xrcopy(u + 1)
                 evact(u - 1)
                 evact_s(u - 1)
                 mx(u + 2, 1, 0, 4)
                 back(u - 1)
                 back_s(u - 1)
-                if u % 2 == 0:
+                if u % 2 == 0 and u >= 0:
                     wshift((u + 2) // 2)
                 mx(u + 2, 1, 4, 8)
                 smult(u, 1)

@@ -95,20 +95,27 @@ def tile_involution2d_pa_kernel(tc, x_words, x_scales, Wi_words, Wi_scales, bi, 
                 in_=w_flat[1024 * q:1024 * (q + 1), :].rearrange("(n p) c -> p n c", p=P),
             )
 
+        ctx.enter_context(tc.manual_schedule())
+
         nc.vector.memset(wis[:].bitcast(I32), 0)
         nc.vector.memset(xss[0][:].bitcast(I32), 0)
-        load_scales(wis, Wi_scales, 0, 512)
-        load_chunk(0)
+        nc.scalar.dma_start(
+            out=w_sb[:, 0:8, :], in_=w_flat[0:1024, :].rearrange("(n p) c -> p n c", p=P))
+        nc.gpsimd.dma_start(out=bias_bf[:], in_=bi.partition_broadcast(P))
         for q in range(4):
+            nc.sync.dma_start(
+                out=xcs[0][:, 2 * q:2 * q + 2, :].bitcast(I32),
+                in_=x_words[2 * q:2 * q + 2, :, 0:1024].rearrange("g p n -> p g n").bitcast(I32))
             nc.sync.dma_start(
                 out=wic[:, 2 * q:2 * q + 2, :].bitcast(I32),
                 in_=Wi_words[2 * q:2 * q + 2, :, :].rearrange("g p n -> p g n").bitcast(I32))
-        nc.scalar.dma_start(
-            out=w_sb[:, 0:8, :], in_=w_flat[0:1024, :].rearrange("(n p) c -> p n c", p=P))
-        nc.scalar.dma_start(out=bias_bf[:], in_=bi.partition_broadcast(P))
+            if q == 0:
+                load_scales(wis, Wi_scales, 0, 512)
+                load_scales(xss[0], x_scales, 0, 512)
 
         make_identity(nc, ident[:])
         nc.vector.memset(e32[:], 0.0)
+        nc.vector.memset(xps[0][:], 0.0)
         nc.vector.tensor_copy(out=e32[:, 128:256], in_=ident[:])
         nc.vector.tensor_reduce(out=edge[:, 0:1], in_=ident[:, 0:128:32], axis=AX.X, op=ALU.add)
         nc.vector.tensor_reduce(out=edge[:, 1:2], in_=ident[:, 31:128:32], axis=AX.X, op=ALU.add)
@@ -116,10 +123,9 @@ def tile_involution2d_pa_kernel(tc, x_words, x_scales, Wi_words, Wi_scales, bi, 
         nc.vector.tensor_scalar(out=ebf[0][:], in0=e32[:], scalar1=mask[:, 0:1], scalar2=None, op0=ALU.mult)
         nc.vector.tensor_copy(out=ebf[1][:], in_=e32[:])
         nc.vector.tensor_scalar(out=ebf[2][:], in0=e32[:], scalar1=mask[:, 1:2], scalar2=None, op0=ALU.mult)
-        for i in range(3):
-            nc.vector.memset(xps[i][:], 0.0)
         for i in range(1, 3):
             nc.vector.memset(xss[i][:].bitcast(I32), 0)
+            nc.vector.memset(xps[i][:], 0.0)
         nc.vector.memset(zt[:], 0.0)
         nc.vector.memset(lbs[0][:, 0, :], 0.0)
         nc.vector.memset(lbs[(NT // NB - 1) % 2][:, NB + 1, :], 0.0)
@@ -417,56 +423,58 @@ def tile_involution2d_pa_kernel(tc, x_words, x_scales, Wi_words, Wi_scales, bi, 
                     in_=y[:, k0:k1, st:st + wd],
                 )
 
-        for t in range(9):
-            if DELTA[t] < -1:
-                nc.sync.dma_start(out=out_flat[0:-DELTA[t], 56 * t:56 * t + WID[t]], in_=zt[0:-DELTA[t], 0:WID[t]])
-            if DELTA[t] == -1:
-                nc.sync.dma_start(
-                    out=out_flat[0:1, 56 * t:56 * t + WID[t]].rearrange("o (a c) -> (o a) c", c=8),
-                    in_=zt[0:7, 0:8],
-                )
+        def zero_rows():
+            for t in range(9):
+                if DELTA[t] < -1:
+                    nc.sync.dma_start(out=out_flat[0:-DELTA[t], 56 * t:56 * t + WID[t]], in_=zt[0:-DELTA[t], 0:WID[t]])
+                if DELTA[t] == -1:
+                    nc.sync.dma_start(
+                        out=out_flat[0:1, 56 * t:56 * t + WID[t]].rearrange("o (a c) -> (o a) c", c=8),
+                        in_=zt[0:7, 0:8],
+                    )
 
-        with tc.manual_schedule():
-            wshift(0)
-            for u in range(-2, nu + 4):
-                if u < 0:
-                    load_chunk(u + 3)
-                if u >= 0 and u % 2 == 0 and u // 2 + 3 < nbat:
-                    load_chunk(u // 2 + 3)
-                if u % 4 == 2 and (u + 2) // 4 + 1 < 8:
-                    load_w((u + 2) // 4 + 1)
-                fwd(u - 1, 0)
-                bias(u + 1)
-                mx(u + 2, 0, 0, 8)
-                fwd(u - 1, 1)
-                fwd_s(u - 1)
-                if u % 2 == 1:
-                    wsevac((u + 1) // 2)
-                if u % 2 == 0:
-                    fin_a((u - 4) // 2)
-                    fin_b((u - 4) // 2)
-                else:
-                    fin_c((u - 5) // 2)
-                vmult(u)
-                vreduce(u)
-                smult(u, 0)
-                if u == -1:
-                    xrcopy(0, 0, 1)
-                elif u == 0:
-                    xrcopy(0, 1, 2)
-                    xrcopy(1)
-                else:
-                    xrcopy(u + 1)
-                evact(u - 1)
-                evact_s(u - 1)
-                mx(u + 2, 1, 0, 4)
-                back(u - 1)
-                back_s(u - 1)
-                if u % 2 == 0 and u >= 0:
-                    wshift((u + 2) // 2)
-                mx(u + 2, 1, 4, 8)
-                smult(u, 1)
-                evacy(u - 1)
-                evacy_s(u - 1)
-                if u % 2 == 1 and u // 2 < nbat - 1:
-                    gadds(u // 2, 0, NB)
+        wshift(0)
+        for u in range(-2, nu + 4):
+            if u < 0:
+                load_chunk(u + 3)
+            if u >= 0 and u % 2 == 0 and u // 2 + 3 < nbat:
+                load_chunk(u // 2 + 3)
+            if u == 0:
+                zero_rows()
+            if u % 4 == 2 and (u + 2) // 4 + 1 < 8:
+                load_w((u + 2) // 4 + 1)
+            fwd(u - 1, 0)
+            bias(u + 1)
+            mx(u + 2, 0, 0, 8)
+            fwd(u - 1, 1)
+            fwd_s(u - 1)
+            if u % 2 == 1:
+                wsevac((u + 1) // 2)
+            if u % 2 == 0:
+                fin_a((u - 4) // 2)
+                fin_b((u - 4) // 2)
+            else:
+                fin_c((u - 5) // 2)
+            vmult(u)
+            vreduce(u)
+            smult(u, 0)
+            if u == -1:
+                xrcopy(0, 0, 1)
+            elif u == 0:
+                xrcopy(0, 1, 2)
+                xrcopy(1)
+            else:
+                xrcopy(u + 1)
+            evact(u - 1)
+            evact_s(u - 1)
+            mx(u + 2, 1, 0, 4)
+            back(u - 1)
+            back_s(u - 1)
+            if u % 2 == 0 and u >= 0:
+                wshift((u + 2) // 2)
+            mx(u + 2, 1, 4, 8)
+            smult(u, 1)
+            evacy(u - 1)
+            evacy_s(u - 1)
+            if u % 2 == 1 and u // 2 < nbat - 1:
+                gadds(u // 2, 0, NB)

@@ -444,7 +444,8 @@ def tile_involution2d_pa_kernel(tc, x_words, x_scales, Wi_words, Wi_scales, bi, 
             if u % 4 == 2 and (u + 2) // 4 + 1 < 8:
                 load_w((u + 2) // 4 + 1)
             fwd(u - 1, 0)
-            bias(u + 1)
+            if u != 0:
+                bias(u + 1)
             mx(u + 2, 0, 0, 8)
             fwd(u - 1, 1)
             fwd_s(u - 1)
@@ -456,13 +457,14 @@ def tile_involution2d_pa_kernel(tc, x_words, x_scales, Wi_words, Wi_scales, bi, 
             else:
                 fin_c((u - 5) // 2)
             vmult(u)
+            if u == 0:
+                bias(u + 1)
             vreduce(u)
             smult(u, 0)
             if u == -1:
                 xrcopy(0, 0, 1)
             elif u == 0:
                 xrcopy(0, 1, 2)
-                xrcopy(1)
             else:
                 xrcopy(u + 1)
             evact(u - 1)
@@ -474,6 +476,8 @@ def tile_involution2d_pa_kernel(tc, x_words, x_scales, Wi_words, Wi_scales, bi, 
                 wshift((u + 2) // 2)
             mx(u + 2, 1, 4, 8)
             smult(u, 1)
+            if u == 0:
+                xrcopy(1)
             evacy(u - 1)
             evacy_s(u - 1)
             if u % 2 == 1 and u // 2 < nbat - 1:

@@ -216,13 +216,13 @@ def tile_involution2d_pa_kernel(tc, x_words, x_scales, Wi_words, Wi_scales, bi, 
             nc.scalar.copy(
                 out=wss[b % 2][:, :, 9:81].rearrange("p k (t c) -> p k t c", c=9), in_=wp4[:, :, 1:9, 9:18])
 
-        def vmult(u):
+        def vmult(u, order=(3, 4, 5, 6, 7, 0, 1, 2)):
             if not 0 <= u < nu:
                 return
             xp = xps[u % 3]
             wp = wps[(u // 2) % 2][:, 2 * (u % 2):2 * (u % 2) + 2, :]
             pv = pvs[u % 2]
-            for b, (g, ta) in [(i, SPLIT[i]) for i in (3, 4, 5, 6, 7, 0, 1, 2)]:
+            for b, (g, ta) in [(i, SPLIT[i]) for i in order]:
                 n1 = 57 * ta + 56 - 32 * g + 1
                 n2 = 33 - n1
                 segs = []
@@ -291,19 +291,22 @@ def tile_involution2d_pa_kernel(tc, x_words, x_scales, Wi_words, Wi_scales, bi, 
                     is_transpose=True, start=(m == 0), stop=(m == 8))
 
         def tail(u):
-            return 0 <= u < nu and u // 2 == nbat - 1
+            return nu - 3 <= u < nu
 
-        def fwd_s(u):
+        def fwd_s(u, c0=0, c1=4):
             if tail(u):
-                for c in range(4):
+                for c in range(c0, c1):
                     for m in range(9):
                         nc.tensor.matmul(
-                            out=xips[1][:, P * c:P * (c + 1)], lhsT=pms[(u // 2) % 2][:, 2 * (u % 2) + c // 2, m, P * (c % 2):P * (c % 2 + 1)],
+                            out=xips[u % 2][:, P * c:P * (c + 1)], lhsT=pms[(u // 2) % 2][:, 2 * (u % 2) + c // 2, m, P * (c % 2):P * (c % 2 + 1)],
                             rhs=ident[:], is_transpose=True, start=(m == 0), stop=(m == 8))
 
-        def evact_s(u):
+        def evact_s(u, eng=None):
             if tail(u):
-                nc.vector.tensor_copy(out=yts[:], in_=xips[1][:])
+                if eng == "S":
+                    nc.scalar.copy(out=yts[:], in_=xips[u % 2][:])
+                else:
+                    nc.vector.tensor_copy(out=yts[:], in_=xips[u % 2][:])
 
         def back_s(u):
             if tail(u):
@@ -434,7 +437,7 @@ def tile_involution2d_pa_kernel(tc, x_words, x_scales, Wi_words, Wi_scales, bi, 
                     )
 
         wshift(0)
-        for u in range(-2, nu + 4):
+        for u in range(-2, nu - 2):
             if u < 0:
                 load_chunk(u + 3)
             if u >= 0 and u % 2 == 0 and u // 2 + 3 < nbat:
@@ -480,5 +483,60 @@ def tile_involution2d_pa_kernel(tc, x_words, x_scales, Wi_words, Wi_scales, bi, 
                 xrcopy(1)
             evacy(u - 1)
             evacy_s(u - 1)
-            if u % 2 == 1 and u // 2 < nbat - 1:
+            if u % 2 == 1 and u // 2 < nbat - 2:
                 gadds(u // 2, 0, NB)
+            if u == nu - 4:
+                gadds(nbat - 2, 0, 2)
+
+        u = nu - 2
+        fwd(u - 1, 0)
+        bias(u + 1)
+        fwd(u - 1, 1)
+        fwd_s(u - 1)
+        fin_a(nbat - 3)
+        fin_b(nbat - 3)
+        vmult(u, (0, 1, 2, 3))
+        evact_s(u - 1)
+        vmult(u, (4, 5, 6, 7))
+        vreduce(u)
+        smult(u, 0)
+        xrcopy(u + 1)
+        evact(u - 1)
+        back(u - 1)
+        back_s(u - 1)
+        fwd_s(u, 0, 2)
+        fwd(u, 0)
+        fwd(u, 1)
+        smult(u, 1)
+        fwd_s(u, 2, 4)
+        evacy(u - 1)
+        evacy_s(u - 1)
+        u = nu - 1
+        fin_c(nbat - 3)
+        vmult(u, (0, 1, 2, 3))
+        evact_s(u - 1)
+        vmult(u, (4, 5, 6, 7))
+        vreduce(u)
+        smult(u, 0)
+        evact(u - 1)
+        back(u - 1)
+        fin_a(nbat - 2)
+        fin_b(nbat - 2)
+        fwd_s(u, 0, 2)
+        fwd(u, 0)
+        fwd(u, 1)
+        back_s(u - 1)
+        smult(u, 1)
+        fwd_s(u, 2, 4)
+        fin_c(nbat - 2)
+        evacy(u - 1)
+        evacy_s(u - 1)
+        evact(u)
+        evact_s(u, "S")
+        back(u)
+        back_s(u)
+        evacy(u)
+        evacy_s(u)
+        fin_a(nbat - 1)
+        fin_b(nbat - 1)
+        fin_c(nbat - 1)

@@ -20,6 +20,7 @@ PASSES = 8
 NB = 4
 XW = 530
 YW = 560
+XRW = 60
 RV = 7
 NWP = 252
 DELTA = [32 * (t // 3 - 1) + (t % 3 - 1) for t in range(9)]
@@ -56,7 +57,7 @@ def tile_involution2d_pa_kernel(tc, x_words, x_scales, Wi_words, Wi_scales, bi, 
         mask = sb.tile([P, 2], F32, name="mask")
         zt = sb.tile([P, 64], F32, name="zt")
         xps = [sb.tile([P, 2, XW], F32, name="xp%d" % i) for i in range(3)]
-        xrs = [sb.tile([P, 2, 9, 57], F32, name="xr%d" % i) for i in range(3)]
+        xrs = [sb.tile([P, 2, 9, XRW], F32, name="xr%d" % i) for i in range(3)]
         bias_r = sb.tile([P, 9, 56], BF16, name="bias_r")
         wss = [sb.tile([P, NB, 81], F32, name="wS%d" % i) for i in range(2)]
         pvs = [sb.tile([P, 2, 2376], F32, name="pv%d" % i) for i in range(2)]
@@ -204,7 +205,7 @@ def tile_involution2d_pa_kernel(tc, x_words, x_scales, Wi_words, Wi_scales, bi, 
             if not 0 <= u < nu:
                 return
             nc.scalar.copy(
-                out=xrs[u % 3][:, k0:k1, RV:9, :],
+                out=xrs[u % 3][:, k0:k1, RV:9, 0:57],
                 in_=xps[u % 3][:, k0:k1, 9:522].rearrange("p k (a r) -> p k r a", r=9)[:, :, RV:9, :])
             nc.scalar.copy(out=xrs[u % 3][:, k0:k1, 0:RV, 56], in_=xps[u % 3][:, k0:k1, 513:513 + RV])
 
@@ -416,7 +417,7 @@ def tile_involution2d_pa_kernel(tc, x_words, x_scales, Wi_words, Wi_scales, bi, 
                 if b == nbat - 1 and d > 1:
                     nc.sync.dma_start(out=out_flat[P * NT - d:P * NT, c0:c0 + wd], in_=y[0:d, NB, st:st + wd])
                 if b == nbat - 1 and d == 1:
-                    nc.sync.dma_start(
+                    nc.gpsimd.dma_start(
                         out=out_flat[P * NT - 1:P * NT, c0:c0 + wd].rearrange("o (a c) -> (o a) c", c=8),
                         in_=y[0:7, NB, st:st + 8],
                     )

@@ -217,7 +217,7 @@ def tile_involution2d_pa_kernel(tc, x_words, x_scales, Wi_words, Wi_scales, bi, 
             nc.scalar.copy(
                 out=wss[b % 2][:, :, 9:81].rearrange("p k (t c) -> p k t c", c=9), in_=wp4[:, :, 1:9, 9:18])
 
-        def vmult(u, order=(3, 4, 5, 6, 7, 0, 1, 2)):
+        def vmult(u, order=(0, 1, 2, 3, 4, 5, 6, 7)):
             if not 0 <= u < nu:
                 return
             xp = xps[u % 3]

@@ -448,10 +448,10 @@ def tile_involution2d_pa_kernel(tc, x_words, x_scales, Wi_words, Wi_scales, bi, 
             if u % 4 == 2 and (u + 2) // 4 + 1 < 8:
                 load_w((u + 2) // 4 + 1)
             fwd(u - 1, 0)
+            fwd(u - 1, 1)
             if u != 0:
                 bias(u + 1)
             mx(u + 2, 0, 0, 8)
-            fwd(u - 1, 1)
             fwd_s(u - 1)
             if u % 2 == 1:
                 wsevac((u + 1) // 2)

@@ -282,6 +282,11 @@ def tile_involution2d_pa_kernel(tc, x_words, x_scales, Wi_words, Wi_scales, bi, 
                         scale=ws[:, kk, 9 * t + m:9 * t + m + 1],
                     )
 
+        def keep():
+            nc.tensor.matmul(
+                out=wps[(nbat - 2) % 2][:].rearrange("p n c -> p (n c)")[:, 0:512], lhsT=ebf[1][:, 128:256], rhs=bias_bf[:],
+                start=True, stop=True)
+
         def fwd(u, k):
             if not 0 <= u < nu:
                 return
@@ -290,6 +295,8 @@ def tile_involution2d_pa_kernel(tc, x_words, x_scales, Wi_words, Wi_scales, bi, 
                 nc.tensor.matmul(
                     out=acct[:, k, :], lhsT=pv[:, k, m:1152:9], rhs=ident[:],
                     is_transpose=True, start=(m == 0), stop=(m == 8))
+                if u >= nu - 3 and m % 4 == 3:
+                    keep()
 
         def tail(u):
             return nu - 3 <= u < nu
@@ -301,6 +308,7 @@ def tile_involution2d_pa_kernel(tc, x_words, x_scales, Wi_words, Wi_scales, bi, 
                         nc.tensor.matmul(
                             out=xips[u % 2][:, P * c:P * (c + 1)], lhsT=pms[(u // 2) % 2][:, 2 * (u % 2) + c // 2, m, P * (c % 2):P * (c % 2 + 1)],
                             rhs=ident[:], is_transpose=True, start=(m == 0), stop=(m == 8))
+                    keep()
 
         def evact_s(u, eng=None):
             if tail(u):

@@ -103,16 +103,26 @@ def tile_involution2d_pa_kernel(tc, x_words, x_scales, Wi_words, Wi_scales, bi, 
         nc.scalar.dma_start(
             out=w_sb[:, 0:8, :], in_=w_flat[0:1024, :].rearrange("(n p) c -> p n c", p=P))
         nc.gpsimd.dma_start(out=bias_bf[:], in_=bi.partition_broadcast(P))
-        for q in range(4):
+        xc0 = xcs[0][:].rearrange("p g n -> p (g n)").rearrange("p (k g n) -> p k g n", k=NB, g=PASSES)
+
+        def load_first(kk):
             nc.sync.dma_start(
-                out=xcs[0][:, 2 * q:2 * q + 2, :].bitcast(I32),
-                in_=x_words[2 * q:2 * q + 2, :, 0:1024].rearrange("g p n -> p g n").bitcast(I32))
+                out=xc0[:, kk, :, :].bitcast(I32),
+                in_=x_words[:, :, 256 * kk:256 * (kk + 1)].rearrange("g p n -> p g n").bitcast(I32))
+
+        def load_wi(g0, g1):
             nc.sync.dma_start(
-                out=wic[:, 2 * q:2 * q + 2, :].bitcast(I32),
-                in_=Wi_words[2 * q:2 * q + 2, :, :].rearrange("g p n -> p g n").bitcast(I32))
-            if q == 0:
-                load_scales(wis, Wi_scales, 0, 512)
-                load_scales(xss[0], x_scales, 0, 512)
+                out=wic[:, g0:g1, :].bitcast(I32),
+                in_=Wi_words[g0:g1, :, :].rearrange("g p n -> p g n").bitcast(I32))
+
+        load_first(0)
+        load_wi(0, 2)
+        load_scales(wis, Wi_scales, 0, 512)
+        load_scales(xss[0], x_scales, 0, 512)
+        load_wi(2, 5)
+        load_wi(5, 8)
+        for kk in range(1, NB):
+            load_first(kk)
 
         make_identity(nc, ident[:])
         nc.vector.memset(e32[:], 0.0)
@@ -146,7 +156,7 @@ def tile_involution2d_pa_kernel(tc, x_words, x_scales, Wi_words, Wi_scales, bi, 
             for g in range(g0, g1):
                 nc.tensor.matmul_mx(
                     out=acc[:],
-                    lhsT=xc[:, g, 256 * kk:256 * (kk + 1)].bitcast(FP4),
+                    lhsT=(xc0[:, kk, g, :] if u < 2 else xc[:, g, 256 * kk:256 * (kk + 1)]).bitcast(FP4),
                     lhsT_scale=xs[:, g, 128 * kk:128 * (kk + 1)],
                     rhs=wic[:, g, :].bitcast(FP4),
                     rhs_scale=wis[:, g, :],
@@ -299,7 +309,7 @@ def tile_involution2d_pa_kernel(tc, x_words, x_scales, Wi_words, Wi_scales, bi, 
                     keep()
 
         def tail(u):
-            return nu - 3 <= u < nu
+            return u in (nu - 3, nu - 1)
 
         def fwd_s(u, c0=0, c1=4):
             if tail(u):
@@ -517,7 +527,7 @@ def tile_involution2d_pa_kernel(tc, x_words, x_scales, Wi_words, Wi_scales, bi, 
         fwd(u, 0)
         fwd(u, 1)
         smult(u, 1)
-        fwd_s(u, 2, 4)
+        gadds(nbat - 1, 0, 2)
         evacy(u - 1)
         evacy_s(u - 1)
         u = nu - 1
@@ -544,6 +554,8 @@ def tile_involution2d_pa_kernel(tc, x_words, x_scales, Wi_words, Wi_scales, bi, 
         evact_s(u, "S")
         back(u)
         back_s(u)
+        for i in range(4):
+            keep()
         evacy(u)
         evacy_s(u)
         fin_a(nbat - 1)

@@ -532,22 +532,22 @@ def tile_involution2d_pa_kernel(tc, x_words, x_scales, Wi_words, Wi_scales, bi, 
         evacy_s(u - 1)
         u = nu - 1
         fin_c(nbat - 3)
-        vmult(u, (0, 1, 2, 3))
-        evact_s(u - 1)
-        vmult(u, (4, 5, 6, 7))
-        vreduce(u)
-        smult(u, 0)
-        evact(u - 1)
-        back(u - 1)
         fin_a(nbat - 2)
         fin_b(nbat - 2)
+        vmult(u, (0, 1, 2, 3))
+        evact_s(u - 1)
+        smult(u, 0)
+        fin_c(nbat - 2)
+        vmult(u, (4, 5, 6, 7))
+        vreduce(u)
+        evact(u - 1)
+        back(u - 1)
         fwd_s(u, 0, 2)
         fwd(u, 0)
         fwd(u, 1)
         back_s(u - 1)
         smult(u, 1)
         fwd_s(u, 2, 4)
-        fin_c(nbat - 2)
         evacy(u - 1)
         evacy_s(u - 1)
         evact(u)

@@ -275,7 +275,7 @@ def tile_involution2d_pa_kernel(tc, x_words, x_scales, Wi_words, Wi_scales, bi, 
                 in_=pv[:, :, 9 * 165:9 * 264].rearrange("p k (q s m) -> p k q s m", q=3, m=9),
                 axis=AX.X, op=ALU.add)
 
-        def smult(u, k):
+        def smult(u, k, g0=0, g1=8):
             if not 0 <= u < nu:
                 return
             xr = xrs[u % 3]
@@ -283,6 +283,8 @@ def tile_involution2d_pa_kernel(tc, x_words, x_scales, Wi_words, Wi_scales, bi, 
             pm = pms[(u // 2) % 2]
             kk = 2 * (u % 2) + k
             for gi, (g, t) in enumerate(WHOLE):
+                if not g0 <= gi < g1:
+                    continue
                 c0 = 288 * g - 512 * t
                 for m in range(9):
                     nc.scalar.activation(
@@ -517,7 +519,6 @@ def tile_involution2d_pa_kernel(tc, x_words, x_scales, Wi_words, Wi_scales, bi, 
         vmult(u, (0, 1, 2, 3))
         evact_s(u - 1)
         vmult(u, (4, 5, 6, 7))
-        vreduce(u)
         smult(u, 0)
         xrcopy(u + 1)
         evact(u - 1)
@@ -527,7 +528,6 @@ def tile_involution2d_pa_kernel(tc, x_words, x_scales, Wi_words, Wi_scales, bi, 
         fwd(u, 0)
         fwd(u, 1)
         smult(u, 1)
-        gadds(nbat - 1, 0, 2)
         evacy(u - 1)
         evacy_s(u - 1)
         u = nu - 1
@@ -535,16 +535,19 @@ def tile_involution2d_pa_kernel(tc, x_words, x_scales, Wi_words, Wi_scales, bi, 
         fin_a(nbat - 2)
         fin_b(nbat - 2)
         vmult(u, (0, 1, 2, 3))
+        vreduce(u - 1)
+        gadds(nbat - 1, 0, 2)
         evact_s(u - 1)
-        smult(u, 0)
+        smult(u, 0, 0, 4)
+        evact(u - 1)
+        smult(u, 0, 4, 8)
         fin_c(nbat - 2)
         vmult(u, (4, 5, 6, 7))
         vreduce(u)
-        evact(u - 1)
         back(u - 1)
-        fwd_s(u, 0, 2)
         fwd(u, 0)
         fwd(u, 1)
+        fwd_s(u, 0, 2)
         back_s(u - 1)
         smult(u, 1)
         fwd_s(u, 2, 4)
@@ -554,7 +557,7 @@ def tile_involution2d_pa_kernel(tc, x_words, x_scales, Wi_words, Wi_scales, bi, 
         evact_s(u, "S")
         back(u)
         back_s(u)
-        for i in range(4):
+        for i in range(3):
             keep()
         evacy(u)
         evacy_s(u)

@@ -201,10 +201,10 @@ def tile_involution2d_pa_kernel(tc, x_words, x_scales, Wi_words, Wi_scales, bi, 
                         stop=True,
                     )
 
-        def bias(u):
+        def bias(u, k0=0, k1=2):
             if not 0 <= u < nu:
                 return
-            for k in range(2):
+            for k in range(k0, k1):
                 acc = xips[(2 * u + k) % 3]
                 nc.vector.tensor_tensor(out=xps[u % 3][:, k, 9:521], in0=acc[:], in1=bias_bf[:], op=ALU.add)
                 nc.vector.tensor_tensor(
@@ -227,12 +227,12 @@ def tile_involution2d_pa_kernel(tc, x_words, x_scales, Wi_words, Wi_scales, bi, 
             nc.scalar.copy(
                 out=wss[b % 2][:, :, 9:81].rearrange("p k (t c) -> p k t c", c=9), in_=wp4[:, :, 1:9, 9:18])
 
-        def vmult(u, order=(0, 1, 2, 3, 4, 5, 6, 7)):
+        def vmult(u, order=(0, 1, 2, 3, 4, 5, 6, 7), k0=0, k1=2):
             if not 0 <= u < nu:
                 return
-            xp = xps[u % 3]
-            wp = wps[(u // 2) % 2][:, 2 * (u % 2):2 * (u % 2) + 2, :]
-            pv = pvs[u % 2]
+            xp = xps[u % 3][:, k0:k1, :]
+            wp = wps[(u // 2) % 2][:, 2 * (u % 2) + k0:2 * (u % 2) + k1, :]
+            pv = pvs[u % 2][:, k0:k1, :]
             for b, (g, ta) in [(i, SPLIT[i]) for i in order]:
                 n1 = 57 * ta + 56 - 32 * g + 1
                 n2 = 33 - n1
@@ -246,11 +246,11 @@ def tile_involution2d_pa_kernel(tc, x_words, x_scales, Wi_words, Wi_scales, bi, 
                     nc.vector.tensor_tensor(
                         out=pv[:, :, 9 * o:9 * (o + n)].rearrange("p k (s m) -> p k s m", m=9),
                         in0=xp[:, :, a:a + 9 * n].rearrange("p k (s m) -> p k s m", m=9),
-                        in1=wp[:, :, cw:cw + 9].unsqueeze(2).to_broadcast([P, 2, n, 9]),
+                        in1=wp[:, :, cw:cw + 9].unsqueeze(2).to_broadcast([P, k1 - k0, n, 9]),
                         op=ALU.mult,
                     )
                 if g == 7:
-                    for k in range(2):
+                    for k in range(k1 - k0):
                         cw = COL[(4, 7)]
                         nc.vector.tensor_tensor(
                             out=pv[:, k, 9 * 103:9 * 161].rearrange("p (h s m) -> p h s m", h=2, m=9),
@@ -469,7 +469,9 @@ def tile_involution2d_pa_kernel(tc, x_words, x_scales, Wi_words, Wi_scales, bi, 
                 load_w((u + 2) // 4 + 1)
             fwd(u - 1, 0)
             fwd(u - 1, 1)
-            if u != 0:
+            if u == -1:
+                bias(0, 0, 1)
+            elif u != 0:
                 bias(u + 1)
             mx(u + 2, 0, 0, 8)
             fwd_s(u - 1)
@@ -480,9 +482,14 @@ def tile_involution2d_pa_kernel(tc, x_words, x_scales, Wi_words, Wi_scales, bi, 
                 fin_b((u - 4) // 2)
             else:
                 fin_c((u - 5) // 2)
-            vmult(u)
-            if u == 0:
+            if u == -1:
+                vmult(0, (0, 1, 2, 3, 4, 5, 6, 7), 0, 1)
+                bias(0, 1, 2)
+            elif u == 0:
+                vmult(0, (0, 1, 2, 3, 4, 5, 6, 7), 1, 2)
                 bias(u + 1)
+            else:
+                vmult(u)
             vreduce(u)
             smult(u, 0)
             if u == -1:

@@ -33,6 +33,12 @@ WHOLE = [(0, 0), (2, 1), (4, 2), (6, 3), (9, 5), (11, 6), (13, 7), (15, 8)]
 SPLIT = [(1, 0), (3, 1), (5, 2), (7, 3), (8, 4), (10, 5), (12, 6), (14, 7)]
 START = [57 * t + 1 for t in range(9)]
 WID = [56] * 8 + [64]
+GB = (0, 1, 2, 3, 4)
+VB = (5, 6, 7)
+NG = 33 * len(GB)
+NV = 33 * len(VB)
+GPL = 1
+EVT = "S"
 
 
 def tile_involution2d_pa_kernel(tc, x_words, x_scales, Wi_words, Wi_scales, bi, w_span, out):
@@ -60,19 +66,19 @@ def tile_involution2d_pa_kernel(tc, x_words, x_scales, Wi_words, Wi_scales, bi, 
         xrs = [sb.tile([P, 2, 9, XRW], F32, name="xr%d" % i) for i in range(3)]
         bias_r = sb.tile([P, 9, 56], BF16, name="bias_r")
         wss = [sb.tile([P, NB, 81], F32, name="wS%d" % i) for i in range(2)]
-        pvs = [sb.tile([P, 2, 2376], F32, name="pv%d" % i) for i in range(2)]
-        pms = [sb.tile([P, NB, 9, 256], F32, name="pm%d" % i) for i in range(2)]
+        wsb = [sb.tile([P, NB, NWP], BF16, name="wB%d" % i) for i in range(2)]
+        pvg = [sb.tile([P, 2, 9 * NG], F32, name="pg%d" % i) for i in range(2)]
+        pvv = [sb.tile([P, 2, 9 * NV], F32, name="pw%d" % i) for i in range(2)]
+        pms = [sb.tile([P, 2, 9, 256], F32, name="pm%d" % i) for i in range(2)]
         ys = [sb.tile([P, NB + 1, YW], F32, name="y%d" % i) for i in range(3)]
         lbs = [sb.tile([P, NB + 2, 72], F32, name="lb%d" % i) for i in range(2)]
-        gdep = sb.tile([P, 1], F32, name="gdep")
-        yt = sb.tile([P, 2, P], F32, name="yt")
         yts = sb.tile([P, 4 * P], F32, name="yts")
 
         xips = [ps.tile([P, 512], F32, name="xiP%d" % i) for i in range(3)]
         wps = [ps.tile([P, NB, NWP], BF16, name="wP%d" % i) for i in range(2)]
         lsh = ps.tile([P, NB + 1, 72], F32, name="lsh")
-        acct = ps.tile([P, 2, P], F32, name="acct")
-        yb = ps.tile([P, 2, P], F32, name="yb")
+        acct = ps.tile([P, 4 * P], F32, name="acct")
+        yb = ps.tile([P, 4 * P], F32, name="yb")
 
         def load_scales(dst, src, c0, c1):
             for q in range(4):
@@ -226,13 +232,24 @@ def tile_involution2d_pa_kernel(tc, x_words, x_scales, Wi_words, Wi_scales, bi, 
             nc.scalar.copy(out=wss[b % 2][:, :, 0:9], in_=wp4[:, :, 0, 0:9])
             nc.scalar.copy(
                 out=wss[b % 2][:, :, 9:81].rearrange("p k (t c) -> p k t c", c=9), in_=wp4[:, :, 1:9, 9:18])
+            wb4 = wsb[b % 2][:].rearrange("p k (t x) -> p k t x", x=WTP)
+            nc.scalar.copy(out=wb4[:, :, 0:6, 0:18], in_=wp4[:, :, 0:6, 0:18])
+            nc.scalar.copy(out=wb4[:, :, 1:4, 18:27], in_=wp4[:, :, 1:4, 18:27])
 
-        def vmult(u, order=(0, 1, 2, 3, 4, 5, 6, 7), k0=0, k1=2):
+        def nmult(eng, u, order, k0=0, k1=2):
             if not 0 <= u < nu:
                 return
             xp = xps[u % 3][:, k0:k1, :]
-            wp = wps[(u // 2) % 2][:, 2 * (u % 2) + k0:2 * (u % 2) + k1, :]
-            pv = pvs[u % 2][:, k0:k1, :]
+            if eng == "V":
+                e = nc.vector
+                wp = wps[(u // 2) % 2][:, 2 * (u % 2) + k0:2 * (u % 2) + k1, :]
+                pv = pvv[u % 2][:, k0:k1, :]
+                base = NG
+            else:
+                e = nc.gpsimd
+                wp = wsb[(u // 2) % 2][:, 2 * (u % 2) + k0:2 * (u % 2) + k1, :]
+                pv = pvg[u % 2][:, k0:k1, :]
+                base = 0
             for b, (g, ta) in [(i, SPLIT[i]) for i in order]:
                 n1 = 57 * ta + 56 - 32 * g + 1
                 n2 = 33 - n1
@@ -243,7 +260,8 @@ def tile_involution2d_pa_kernel(tc, x_words, x_scales, Wi_words, Wi_scales, bi, 
                     segs.append((ta + 1, ta + 1, n2, 33 * b + n1))
                 for (t, a, n, o) in segs:
                     cw = COL[(t, g)]
-                    nc.vector.tensor_tensor(
+                    o = o - base
+                    e.tensor_tensor(
                         out=pv[:, :, 9 * o:9 * (o + n)].rearrange("p k (s m) -> p k s m", m=9),
                         in0=xp[:, :, a:a + 9 * n].rearrange("p k (s m) -> p k s m", m=9),
                         in1=wp[:, :, cw:cw + 9].unsqueeze(2).to_broadcast([P, k1 - k0, n, 9]),
@@ -252,35 +270,50 @@ def tile_involution2d_pa_kernel(tc, x_words, x_scales, Wi_words, Wi_scales, bi, 
                 if g == 7:
                     for k in range(k1 - k0):
                         cw = COL[(4, 7)]
-                        nc.vector.tensor_tensor(
-                            out=pv[:, k, 9 * 103:9 * 161].rearrange("p (h s m) -> p h s m", h=2, m=9),
+                        e.tensor_tensor(
+                            out=pv[:, k, 9 * (103 - base):9 * (161 - base)].rearrange("p (h s m) -> p h s m", h=2, m=9),
                             in0=xp[:, k, 4:4 + 522].rearrange("p (h s m) -> p h s m", h=2, m=9),
                             in1=wp[:, k, cw:cw + 18].rearrange("p (h m) -> p h m", m=9).unsqueeze(2).to_broadcast(
                                 [P, 2, 29, 9]),
                             op=ALU.mult,
                         )
 
+        def gplane(u):
+            if not 0 <= u < nu or GPL == 0:
+                return
+            nc.gpsimd.tensor_tensor(
+                out=pms[u % 2][:, :, :, 0:32],
+                in0=xrs[u % 3][:, :, :, 0:32],
+                in1=wsb[(u // 2) % 2][:, 2 * (u % 2):2 * (u % 2) + 2, 0:9].unsqueeze(3).to_broadcast([P, 2, 9, 32]),
+                op=ALU.mult,
+            )
+
         def vreduce(u):
             if not 0 <= u < nu:
                 return
-            pv = pvs[u % 2]
             y = ys[(u // 2) % 3]
             s0 = 2 * (u % 2)
+            pg = pvg[u % 2]
+            pw = pvv[u % 2]
             nc.vector.tensor_reduce(
-                out=y[:, s0:s0 + 2, 257:294],
-                in_=pv[:, :, 9 * 128:9 * 165].rearrange("p k (s m) -> p k s m", m=9),
+                out=y[:, s0:s0 + 2, 33:33 + 195].rearrange("p k (q c) -> p k q c", c=65)[:, :, :, 0:33],
+                in_=pg[:, :, 0:9 * 99].rearrange("p k (q s m) -> p k q s m", q=3, m=9),
+                axis=AX.X, op=ALU.add)
+            nc.vector.tensor_reduce(
+                out=y[:, s0:s0 + 2, 228:294],
+                in_=pg[:, :, 9 * 99:9 * 165].rearrange("p k (s m) -> p k s m", m=9),
                 axis=AX.X, op=ALU.add)
             nc.vector.tensor_reduce(
                 out=y[:, s0:s0 + 2, 326:326 + 195].rearrange("p k (q c) -> p k q c", c=65)[:, :, :, 0:33],
-                in_=pv[:, :, 9 * 165:9 * 264].rearrange("p k (q s m) -> p k q s m", q=3, m=9),
+                in_=pw[:].rearrange("p k (q s m) -> p k q s m", q=3, m=9),
                 axis=AX.X, op=ALU.add)
 
-        def smult(u, k, g0=0, g1=8):
+        def smult(u, k, g0=GPL, g1=8):
             if not 0 <= u < nu:
                 return
             xr = xrs[u % 3]
             ws = wss[(u // 2) % 2]
-            pm = pms[(u // 2) % 2]
+            pm = pms[u % 2]
             kk = 2 * (u % 2) + k
             for gi, (g, t) in enumerate(WHOLE):
                 if not g0 <= gi < g1:
@@ -288,7 +321,7 @@ def tile_involution2d_pa_kernel(tc, x_words, x_scales, Wi_words, Wi_scales, bi, 
                 c0 = 288 * g - 512 * t
                 for m in range(9):
                     nc.scalar.activation(
-                        out=pm[:, kk, m, 32 * gi:32 * gi + 32],
+                        out=pm[:, k, m, 32 * gi:32 * gi + 32],
                         in_=xr[:, k, (c0 + m) % 9, (c0 + m) // 9:(c0 + m) // 9 + 32],
                         func=ACT.Copy,
                         scale=ws[:, kk, 9 * t + m:9 * t + m + 1],
@@ -299,88 +332,40 @@ def tile_involution2d_pa_kernel(tc, x_words, x_scales, Wi_words, Wi_scales, bi, 
                 out=wps[(nbat - 2) % 2][:].rearrange("p n c -> p (n c)")[:, 0:512], lhsT=ebf[1][:, 128:256], rhs=bias_bf[:],
                 start=True, stop=True)
 
-        def fwd(u, k):
+        def fwd_s(u, c0=0, c1=4):
             if not 0 <= u < nu:
                 return
-            pv = pvs[u % 2]
-            for m in range(9):
-                nc.tensor.matmul(
-                    out=acct[:, k, :], lhsT=pv[:, k, m:1152:9], rhs=ident[:],
-                    is_transpose=True, start=(m == 0), stop=(m == 8))
-                if u >= nu - 3 and m % 4 == 3:
+            for c in range(c0, c1):
+                for m in range(9):
+                    nc.tensor.matmul(
+                        out=acct[:, P * c:P * (c + 1)], lhsT=pms[u % 2][:, c // 2, m, P * (c % 2):P * (c % 2 + 1)],
+                        rhs=ident[:], is_transpose=True, start=(m == 0), stop=(m == 8))
+                if u >= nu - 2:
                     keep()
 
-        def tail(u):
-            return u in (nu - 3, nu - 1)
-
-        def fwd_s(u, c0=0, c1=4):
-            if tail(u):
-                for c in range(c0, c1):
-                    for m in range(9):
-                        nc.tensor.matmul(
-                            out=xips[u % 2][:, P * c:P * (c + 1)], lhsT=pms[(u // 2) % 2][:, 2 * (u % 2) + c // 2, m, P * (c % 2):P * (c % 2 + 1)],
-                            rhs=ident[:], is_transpose=True, start=(m == 0), stop=(m == 8))
-                    keep()
-
-        def evact_s(u, eng=None):
-            if tail(u):
-                if eng == "S":
-                    nc.scalar.copy(out=yts[:], in_=xips[u % 2][:])
-                else:
-                    nc.vector.tensor_copy(out=yts[:], in_=xips[u % 2][:])
+        def evact_s(u):
+            if not 0 <= u < nu:
+                return
+            if EVT == "S":
+                nc.scalar.copy(out=yts[:], in_=acct[:])
+            else:
+                nc.vector.tensor_copy(out=yts[:], in_=acct[:])
 
         def back_s(u):
-            if tail(u):
-                for c in range(4):
-                    nc.tensor.transpose(out=xips[2][:, P * c:P * (c + 1)], in_=yts[:, P * c:P * (c + 1)], identity=ident[:])
+            if not 0 <= u < nu:
+                return
+            for c in range(4):
+                nc.tensor.transpose(out=yb[:, P * c:P * (c + 1)], in_=yts[:, P * c:P * (c + 1)], identity=ident[:])
 
         def evacy_s(u):
-            if tail(u):
-                s0 = 2 * (u % 2)
-                for h in range(2):
-                    nc.scalar.copy(
-                        out=ys[(u // 2) % 3][:, s0:s0 + 2, 1 + 293 * h:1 + 293 * h + 260].rearrange(
-                            "p k (q c) -> p k q c", c=65)[:, :, :, 0:32],
-                        in_=xips[2][:].rearrange("p (k h q c) -> p k h q c", k=2, h=2, c=32)[:, :, h, :, :])
-
-        def evact(u):
             if not 0 <= u < nu:
                 return
-            nc.scalar.copy(out=yt[:], in_=acct[:])
-
-        def back(u):
-            if not 0 <= u < nu:
-                return
-            for k in range(2):
-                nc.tensor.transpose(out=yb[:, k, :], in_=yt[:, k, :], identity=ident[:])
-
-        def evacy(u):
-            if not 0 <= u < nu:
-                return
-            y = ys[(u // 2) % 3]
             s0 = 2 * (u % 2)
-            nc.scalar.copy(
-                out=y[:, s0:s0 + 2, 33:33 + 195].rearrange("p k (q c) -> p k q c", c=65)[:, :, :, 0:33],
-                in_=yb[:, :, 0:99].rearrange("p k (q c) -> p k q c", c=33))
-            nc.scalar.copy(out=y[:, s0:s0 + 2, 228:257], in_=yb[:, :, 99:128])
-
-        def gadds(b, n0, n1):
-            if not 0 <= b < nbat:
-                return
-            pm = pms[b % 2][:, n0:n1, :, :]
-            y = ys[b % 3]
-            nc.gpsimd.tensor_tensor(out=pm[:, :, 0:4, :], in0=pm[:, :, 0:4, :], in1=pm[:, :, 4:8, :], op=ALU.add)
-            nc.gpsimd.tensor_tensor(out=pm[:, :, 0:2, :], in0=pm[:, :, 0:2, :], in1=pm[:, :, 2:4, :], op=ALU.add)
-            nc.gpsimd.tensor_tensor(out=pm[:, :, 0, :], in0=pm[:, :, 0, :], in1=pm[:, :, 1, :], op=ALU.add)
-            nc.gpsimd.tensor_copy(out=gdep[:], in_=y[:, n1 - 1, 326:327])
-            for h in (1, 0):
-                nc.gpsimd.tensor_tensor(
-                    out=y[:, n0:n1, 1 + 293 * h:1 + 293 * h + 260].rearrange(
+            for h in range(2):
+                nc.scalar.copy(
+                    out=ys[(u // 2) % 3][:, s0:s0 + 2, 1 + 293 * h:1 + 293 * h + 260].rearrange(
                         "p k (q c) -> p k q c", c=65)[:, :, :, 0:32],
-                    in0=pm[:, :, 0, 128 * h:128 * (h + 1)].rearrange("p k (q c) -> p k q c", c=32),
-                    in1=pm[:, :, 8, 128 * h:128 * (h + 1)].rearrange("p k (q c) -> p k q c", c=32),
-                    op=ALU.add,
-                )
+                    in_=yb[:].rearrange("p (k h q c) -> p k h q c", k=2, h=2, c=32)[:, :, h, :, :])
 
         def fin_a(b):
             if not 0 <= b < nbat:
@@ -458,7 +443,7 @@ def tile_involution2d_pa_kernel(tc, x_words, x_scales, Wi_words, Wi_scales, bi, 
                     )
 
         wshift(0)
-        for u in range(-2, nu - 2):
+        for u in range(-2, nu + 1):
             if u < 0:
                 load_chunk(u + 3)
             if u >= 0 and u % 2 == 0 and u // 2 + 3 < nbat:
@@ -467,14 +452,11 @@ def tile_involution2d_pa_kernel(tc, x_words, x_scales, Wi_words, Wi_scales, bi, 
                 zero_rows()
             if u % 4 == 2 and (u + 2) // 4 + 1 < 8:
                 load_w((u + 2) // 4 + 1)
-            fwd(u - 1, 0)
-            fwd(u - 1, 1)
-            if u == -1:
-                bias(0, 0, 1)
-            elif u != 0:
-                bias(u + 1)
+            back_s(u - 2)
+            fwd_s(u - 1, 0, 2)
+            bias(u + 1)
             mx(u + 2, 0, 0, 8)
-            fwd_s(u - 1)
+            fwd_s(u - 1, 2, 4)
             if u % 2 == 1:
                 wsevac((u + 1) // 2)
             if u % 2 == 0:
@@ -482,92 +464,21 @@ def tile_involution2d_pa_kernel(tc, x_words, x_scales, Wi_words, Wi_scales, bi, 
                 fin_b((u - 4) // 2)
             else:
                 fin_c((u - 5) // 2)
-            if u == -1:
-                vmult(0, (0, 1, 2, 3, 4, 5, 6, 7), 0, 1)
-                bias(0, 1, 2)
-            elif u == 0:
-                vmult(0, (0, 1, 2, 3, 4, 5, 6, 7), 1, 2)
-                bias(u + 1)
-            else:
-                vmult(u)
-            vreduce(u)
-            smult(u, 0)
-            if u == -1:
-                xrcopy(0, 0, 1)
-            elif u == 0:
-                xrcopy(0, 1, 2)
-            else:
-                xrcopy(u + 1)
-            evact(u - 1)
-            evact_s(u - 1)
-            mx(u + 2, 1, 0, 4)
-            back(u - 1)
-            back_s(u - 1)
             if u % 2 == 0 and u >= 0:
                 wshift((u + 2) // 2)
-            mx(u + 2, 1, 4, 8)
+            mx(u + 2, 1, 0, 8)
+            nmult("V", u, VB)
+            gplane(u)
+            nmult("G", u, GB)
+            vreduce(u - 1)
+            smult(u, 0)
+            xrcopy(u + 1)
             smult(u, 1)
-            if u == 0:
-                xrcopy(1)
-            evacy(u - 1)
-            evacy_s(u - 1)
-            if u % 2 == 1 and u // 2 < nbat - 2:
-                gadds(u // 2, 0, NB)
-            if u == nu - 4:
-                gadds(nbat - 2, 0, 2)
-
-        u = nu - 2
-        fwd(u - 1, 0)
-        bias(u + 1)
-        fwd(u - 1, 1)
-        fwd_s(u - 1)
-        fin_a(nbat - 3)
-        fin_b(nbat - 3)
-        vmult(u, (0, 1, 2, 3))
-        evact_s(u - 1)
-        vmult(u, (4, 5, 6, 7))
-        smult(u, 0)
-        xrcopy(u + 1)
-        evact(u - 1)
-        back(u - 1)
-        back_s(u - 1)
-        fwd_s(u, 0, 2)
-        fwd(u, 0)
-        fwd(u, 1)
-        smult(u, 1)
-        evacy(u - 1)
-        evacy_s(u - 1)
-        u = nu - 1
-        fin_c(nbat - 3)
-        fin_a(nbat - 2)
-        fin_b(nbat - 2)
-        vmult(u, (0, 1, 2, 3))
-        vreduce(u - 1)
-        gadds(nbat - 1, 0, 2)
-        evact_s(u - 1)
-        smult(u, 0, 0, 4)
-        evact(u - 1)
-        smult(u, 0, 4, 8)
+            evacy_s(u - 2)
+            evact_s(u - 1)
+        back_s(nu - 1)
+        evacy_s(nu - 1)
         fin_c(nbat - 2)
-        vmult(u, (4, 5, 6, 7))
-        vreduce(u)
-        back(u - 1)
-        fwd(u, 0)
-        fwd(u, 1)
-        fwd_s(u, 0, 2)
-        back_s(u - 1)
-        smult(u, 1)
-        fwd_s(u, 2, 4)
-        evacy(u - 1)
-        evacy_s(u - 1)
-        evact(u)
-        evact_s(u, "S")
-        back(u)
-        back_s(u)
-        for i in range(3):
-            keep()
-        evacy(u)
-        evacy_s(u)
         fin_a(nbat - 1)
         fin_b(nbat - 1)
         fin_c(nbat - 1)

@@ -37,7 +37,9 @@ GB = (0, 1, 2, 3, 4)
 VB = (5, 6, 7)
 NG = 33 * len(GB)
 NV = 33 * len(VB)
-GPL = 1
+NPL = 8
+GW = (0,)
+VW = ()
 EVT = "S"
 
 
@@ -69,7 +71,7 @@ def tile_involution2d_pa_kernel(tc, x_words, x_scales, Wi_words, Wi_scales, bi, 
         wsb = [sb.tile([P, NB, NWP], BF16, name="wB%d" % i) for i in range(2)]
         pvg = [sb.tile([P, 2, 9 * NG], F32, name="pg%d" % i) for i in range(2)]
         pvv = [sb.tile([P, 2, 9 * NV], F32, name="pw%d" % i) for i in range(2)]
-        pms = [sb.tile([P, 2, 9, 256], F32, name="pm%d" % i) for i in range(2)]
+        pms = [sb.tile([P, 2, 9, 256], F32, name="pm%d" % i) for i in range(3)]
         ys = [sb.tile([P, NB + 1, YW], F32, name="y%d" % i) for i in range(3)]
         lbs = [sb.tile([P, NB + 2, 72], F32, name="lb%d" % i) for i in range(2)]
         yts = sb.tile([P, 4 * P], F32, name="yts")
@@ -278,15 +280,32 @@ def tile_involution2d_pa_kernel(tc, x_words, x_scales, Wi_words, Wi_scales, bi, 
                             op=ALU.mult,
                         )
 
-        def gplane(u):
-            if not 0 <= u < nu or GPL == 0:
+        def pmult(eng, u, gis, k0=0, k1=2):
+            if not 0 <= u < nu:
                 return
-            nc.gpsimd.tensor_tensor(
-                out=pms[u % 2][:, :, :, 0:32],
-                in0=xrs[u % 3][:, :, :, 0:32],
-                in1=wsb[(u // 2) % 2][:, 2 * (u % 2):2 * (u % 2) + 2, 0:9].unsqueeze(3).to_broadcast([P, 2, 9, 32]),
-                op=ALU.mult,
-            )
+            kk = 2 * (u % 2)
+            e = nc.vector if eng == "V" else nc.gpsimd
+            w = (wps if eng == "V" else wsb)[(u // 2) % 2][:, kk + k0:kk + k1, :]
+            for gi in gis:
+                g, t = WHOLE[gi]
+                c0 = 288 * g - 512 * t
+                r0 = c0 % 9
+                cw = COL[(t, g)]
+                for (m0, m1, r, a) in [(0, 9 - r0, r0, c0 // 9), (9 - r0, 9, 0, c0 // 9 + 1)]:
+                    if m1 > m0:
+                        e.tensor_tensor(
+                            out=pms[u % 3][:, k0:k1, m0:m1, 32 * gi:32 * gi + 32],
+                            in0=xrs[u % 3][:, k0:k1, r:r + m1 - m0, a:a + 32],
+                            in1=w[:, :, cw + m0:cw + m1].unsqueeze(3).to_broadcast([P, k1 - k0, m1 - m0, 32]),
+                            op=ALU.mult,
+                        )
+
+        def gpre(u):
+            if not 0 <= u < nu:
+                return
+            pm = pms[u % 3]
+            for m in range(NPL, 8):
+                nc.gpsimd.tensor_tensor(out=pm[:, :, 8, :], in0=pm[:, :, 8, :], in1=pm[:, :, m, :], op=ALU.add)
 
         def vreduce(u):
             if not 0 <= u < nu:
@@ -308,15 +327,15 @@ def tile_involution2d_pa_kernel(tc, x_words, x_scales, Wi_words, Wi_scales, bi, 
                 in_=pw[:].rearrange("p k (q s m) -> p k q s m", q=3, m=9),
                 axis=AX.X, op=ALU.add)
 
-        def smult(u, k, g0=GPL, g1=8):
+        def smult(u, k, g0=0, g1=8):
             if not 0 <= u < nu:
                 return
             xr = xrs[u % 3]
             ws = wss[(u // 2) % 2]
-            pm = pms[u % 2]
+            pm = pms[u % 3]
             kk = 2 * (u % 2) + k
             for gi, (g, t) in enumerate(WHOLE):
-                if not g0 <= gi < g1:
+                if not g0 <= gi < g1 or gi in GW or gi in VW:
                     continue
                 c0 = 288 * g - 512 * t
                 for m in range(9):
@@ -336,10 +355,10 @@ def tile_involution2d_pa_kernel(tc, x_words, x_scales, Wi_words, Wi_scales, bi, 
             if not 0 <= u < nu:
                 return
             for c in range(c0, c1):
-                for m in range(9):
+                for m in range(NPL):
                     nc.tensor.matmul(
-                        out=acct[:, P * c:P * (c + 1)], lhsT=pms[u % 2][:, c // 2, m, P * (c % 2):P * (c % 2 + 1)],
-                        rhs=ident[:], is_transpose=True, start=(m == 0), stop=(m == 8))
+                        out=acct[:, P * c:P * (c + 1)], lhsT=pms[u % 3][:, c // 2, m, P * (c % 2):P * (c % 2 + 1)],
+                        rhs=ident[:], is_transpose=True, start=(m == 0), stop=(m == NPL - 1))
                 if u >= nu - 2:
                     keep()
 
@@ -362,10 +381,12 @@ def tile_involution2d_pa_kernel(tc, x_words, x_scales, Wi_words, Wi_scales, bi, 
                 return
             s0 = 2 * (u % 2)
             for h in range(2):
-                nc.scalar.copy(
+                nc.vector.tensor_tensor(
                     out=ys[(u // 2) % 3][:, s0:s0 + 2, 1 + 293 * h:1 + 293 * h + 260].rearrange(
                         "p k (q c) -> p k q c", c=65)[:, :, :, 0:32],
-                    in_=yb[:].rearrange("p (k h q c) -> p k h q c", k=2, h=2, c=32)[:, :, h, :, :])
+                    in0=yb[:].rearrange("p (k h q c) -> p k h q c", k=2, h=2, c=32)[:, :, h, :, :],
+                    in1=pms[u % 3][:, :, 8, P * h:P * (h + 1)].rearrange("p k (q c) -> p k q c", c=32),
+                    op=ALU.add)
 
         def fin_a(b):
             if not 0 <= b < nbat:
@@ -459,6 +480,7 @@ def tile_involution2d_pa_kernel(tc, x_words, x_scales, Wi_words, Wi_scales, bi, 
             fwd_s(u - 1, 2, 4)
             if u % 2 == 1:
                 wsevac((u + 1) // 2)
+            evacy_s(u - 2)
             if u % 2 == 0:
                 fin_a((u - 4) // 2)
                 fin_b((u - 4) // 2)
@@ -467,14 +489,15 @@ def tile_involution2d_pa_kernel(tc, x_words, x_scales, Wi_words, Wi_scales, bi, 
             if u % 2 == 0 and u >= 0:
                 wshift((u + 2) // 2)
             mx(u + 2, 1, 0, 8)
-            nmult("V", u, VB)
-            gplane(u)
+            gpre(u - 1)
+            pmult("G", u, GW)
             nmult("G", u, GB)
+            nmult("V", u, VB)
+            pmult("V", u, VW)
             vreduce(u - 1)
             smult(u, 0)
             xrcopy(u + 1)
             smult(u, 1)
-            evacy_s(u - 2)
             evact_s(u - 1)
         back_s(nu - 1)
         evacy_s(nu - 1)

@@ -39,6 +39,7 @@ NG = 33 * len(GB)
 NV = 33 * len(VB)
 NPL = 8
 GW = (0,)
+GK = 1
 VW = ()
 EVT = "S"
 
@@ -335,7 +336,7 @@ def tile_involution2d_pa_kernel(tc, x_words, x_scales, Wi_words, Wi_scales, bi, 
             pm = pms[u % 3]
             kk = 2 * (u % 2) + k
             for gi, (g, t) in enumerate(WHOLE):
-                if not g0 <= gi < g1 or gi in GW or gi in VW:
+                if not g0 <= gi < g1 or (gi in GW and k < GK) or gi in VW:
                     continue
                 c0 = 288 * g - 512 * t
                 for m in range(9):
@@ -490,7 +491,7 @@ def tile_involution2d_pa_kernel(tc, x_words, x_scales, Wi_words, Wi_scales, bi, 
                 wshift((u + 2) // 2)
             mx(u + 2, 1, 0, 8)
             gpre(u - 1)
-            pmult("G", u, GW)
+            pmult("G", u, GW, 0, GK)
             nmult("G", u, GB)
             nmult("V", u, VB)
             pmult("V", u, VW)

@@ -39,6 +39,7 @@ NG = 33 * len(GB)
 NV = 33 * len(VB)
 NPL = 8
 GW = (0,)
+NTL = 1
 GK = 1
 VW = ()
 EVT = "S"
@@ -71,11 +72,13 @@ def tile_involution2d_pa_kernel(tc, x_words, x_scales, Wi_words, Wi_scales, bi, 
         wss = [sb.tile([P, NB, 81], F32, name="wS%d" % i) for i in range(2)]
         wsb = [sb.tile([P, NB, NWP], BF16, name="wB%d" % i) for i in range(2)]
         pvg = [sb.tile([P, 2, 9 * NG], F32, name="pg%d" % i) for i in range(2)]
-        pvv = [sb.tile([P, 2, 9 * NV], F32, name="pw%d" % i) for i in range(2)]
+        pvv = [sb.tile([P, 2, 9 * NV], F32, name="pw%d" % i) for i in range(3)]
+        pvx = sb.tile([P, 2, 9 * 66], F32, name="px")
         pms = [sb.tile([P, 2, 9, 256], F32, name="pm%d" % i) for i in range(3)]
         ys = [sb.tile([P, NB + 1, YW], F32, name="y%d" % i) for i in range(3)]
         lbs = [sb.tile([P, NB + 2, 72], F32, name="lb%d" % i) for i in range(2)]
         yts = sb.tile([P, 4 * P], F32, name="yts")
+        ytn = sb.tile([P, 2 * P], F32, name="ytn")
 
         xips = [ps.tile([P, 512], F32, name="xiP%d" % i) for i in range(3)]
         wps = [ps.tile([P, NB, NWP], BF16, name="wP%d" % i) for i in range(2)]
@@ -239,15 +242,15 @@ def tile_involution2d_pa_kernel(tc, x_words, x_scales, Wi_words, Wi_scales, bi, 
             nc.scalar.copy(out=wb4[:, :, 0:6, 0:18], in_=wp4[:, :, 0:6, 0:18])
             nc.scalar.copy(out=wb4[:, :, 1:4, 18:27], in_=wp4[:, :, 1:4, 18:27])
 
-        def nmult(eng, u, order, k0=0, k1=2):
+        def nmult(eng, u, order, k0=0, k1=2, extra=False):
             if not 0 <= u < nu:
                 return
             xp = xps[u % 3][:, k0:k1, :]
             if eng == "V":
                 e = nc.vector
                 wp = wps[(u // 2) % 2][:, 2 * (u % 2) + k0:2 * (u % 2) + k1, :]
-                pv = pvv[u % 2][:, k0:k1, :]
-                base = NG
+                pv = (pvx if extra else pvv[u % 3])[:, k0:k1, :]
+                base = 99 if extra else NG
             else:
                 e = nc.gpsimd
                 wp = wsb[(u // 2) % 2][:, 2 * (u % 2) + k0:2 * (u % 2) + k1, :]
@@ -308,25 +311,58 @@ def tile_involution2d_pa_kernel(tc, x_words, x_scales, Wi_words, Wi_scales, bi, 
             for m in range(NPL, 8):
                 nc.gpsimd.tensor_tensor(out=pm[:, :, 8, :], in0=pm[:, :, 8, :], in1=pm[:, :, m, :], op=ALU.add)
 
-        def vreduce(u):
+        def tailn(u):
+            return nu - 2 - NTL <= u < nu - 2
+
+        def fwd_n(u):
+            for k in range(2):
+                for m in range(9):
+                    nc.tensor.matmul(
+                        out=xips[u % 2][:, P * k:P * (k + 1)], lhsT=pvg[u % 2][:, k, m:1152:9], rhs=ident[:],
+                        is_transpose=True, start=(m == 0), stop=(m == 8))
+                    if m % 4 == 3:
+                        keep()
+
+        def evact_n(u):
+            nc.scalar.copy(out=ytn[:], in_=xips[u % 2][:, 0:2 * P])
+
+        def back_n(u):
+            for k in range(2):
+                nc.tensor.transpose(out=xips[2][:, P * k:P * (k + 1)], in_=ytn[:, P * k:P * (k + 1)], identity=ident[:])
+
+        def evacy_n(u):
+            y = ys[(u // 2) % 3]
+            s0 = 2 * (u % 2)
+            yn = xips[2][:, 0:2 * P].rearrange("p (k c) -> p k c", k=2)
+            nc.scalar.copy(
+                out=y[:, s0:s0 + 2, 33:33 + 195].rearrange("p k (q c) -> p k q c", c=65)[:, :, :, 0:33],
+                in_=yn[:, :, 0:99].rearrange("p k (q c) -> p k q c", c=33))
+            nc.scalar.copy(out=y[:, s0:s0 + 2, 228:257], in_=yn[:, :, 99:128])
+
+        def vreduce(u, parts="abc"):
             if not 0 <= u < nu:
                 return
             y = ys[(u // 2) % 3]
             s0 = 2 * (u % 2)
             pg = pvg[u % 2]
-            pw = pvv[u % 2]
-            nc.vector.tensor_reduce(
-                out=y[:, s0:s0 + 2, 33:33 + 195].rearrange("p k (q c) -> p k q c", c=65)[:, :, :, 0:33],
-                in_=pg[:, :, 0:9 * 99].rearrange("p k (q s m) -> p k q s m", q=3, m=9),
-                axis=AX.X, op=ALU.add)
-            nc.vector.tensor_reduce(
-                out=y[:, s0:s0 + 2, 228:294],
-                in_=pg[:, :, 9 * 99:9 * 165].rearrange("p k (s m) -> p k s m", m=9),
-                axis=AX.X, op=ALU.add)
-            nc.vector.tensor_reduce(
-                out=y[:, s0:s0 + 2, 326:326 + 195].rearrange("p k (q c) -> p k q c", c=65)[:, :, :, 0:33],
-                in_=pw[:].rearrange("p k (q s m) -> p k q s m", q=3, m=9),
-                axis=AX.X, op=ALU.add)
+            pw = pvv[u % 3]
+            for part in parts:
+                if part == "a" and not tailn(u):
+                    nc.vector.tensor_reduce(
+                        out=y[:, s0:s0 + 2, 33:33 + 195].rearrange("p k (q c) -> p k q c", c=65)[:, :, :, 0:33],
+                        in_=pg[:, :, 0:9 * 99].rearrange("p k (q s m) -> p k q s m", q=3, m=9),
+                        axis=AX.X, op=ALU.add)
+                if part == "b":
+                    f = 128 if tailn(u) else 99
+                    nc.vector.tensor_reduce(
+                        out=y[:, s0:s0 + 2, 228 + f - 99:294],
+                        in_=(pvx[:] if u == nu - 1 else pg[:, :, 9 * f:9 * 165]).rearrange("p k (s m) -> p k s m", m=9),
+                        axis=AX.X, op=ALU.add)
+                if part == "c":
+                    nc.vector.tensor_reduce(
+                        out=y[:, s0:s0 + 2, 326:326 + 195].rearrange("p k (q c) -> p k q c", c=65)[:, :, :, 0:33],
+                        in_=pw[:].rearrange("p k (q s m) -> p k q s m", q=3, m=9),
+                        axis=AX.X, op=ALU.add)
 
         def smult(u, k, g0=0, g1=8):
             if not 0 <= u < nu:
@@ -360,7 +396,7 @@ def tile_involution2d_pa_kernel(tc, x_words, x_scales, Wi_words, Wi_scales, bi, 
                     nc.tensor.matmul(
                         out=acct[:, P * c:P * (c + 1)], lhsT=pms[u % 3][:, c // 2, m, P * (c % 2):P * (c % 2 + 1)],
                         rhs=ident[:], is_transpose=True, start=(m == 0), stop=(m == NPL - 1))
-                if u >= nu - 2:
+                if u >= nu - 3:
                     keep()
 
         def evact_s(u):
@@ -389,12 +425,12 @@ def tile_involution2d_pa_kernel(tc, x_words, x_scales, Wi_words, Wi_scales, bi, 
                     in1=pms[u % 3][:, :, 8, P * h:P * (h + 1)].rearrange("p k (q c) -> p k q c", c=32),
                     op=ALU.add)
 
-        def fin_a(b):
+        def fin_a(b, j0=0, j1=NB):
             if not 0 <= b < nbat:
                 return
             nc.scalar.copy(
-                out=lbs[b % 2][:, 1:1 + NB, 0:64].rearrange("p n (t c) -> p n t c", c=8),
-                in_=ys[b % 3][:, 0:NB, 50:514].rearrange("p n (t c) -> p n t c", c=58)[:, :, :, 0:8],
+                out=lbs[b % 2][:, 1 + j0:1 + j1, 0:64].rearrange("p n (t c) -> p n t c", c=8),
+                in_=ys[b % 3][:, j0:j1, 50:514].rearrange("p n (t c) -> p n t c", c=58)[:, :, :, 0:8],
             )
             if b + 1 < nbat:
                 nc.scalar.copy(
@@ -402,48 +438,48 @@ def tile_involution2d_pa_kernel(tc, x_words, x_scales, Wi_words, Wi_scales, bi, 
                     in_=ys[b % 3][:, NB - 1, 50:514].rearrange("p (t c) -> p t c", c=58)[:, :, 0:8],
                 )
 
-        def fin_b(b):
+        def fin_b(b, j0=0, j1=NB):
             if not 0 <= b < nbat:
                 return
-            t0 = NB * b
-            n = NB + (1 if b == nbat - 1 else 0)
-            cur = lbs[b % 2][:, 1:1 + n, :].rearrange("p n (a b) -> p n a b", b=24)
-            prv = lbs[b % 2][:, 0:n, :].rearrange("p n (a b) -> p n a b", b=24)
-            l4 = lsh[:, 0:n, :].rearrange("p n (a b) -> p n a b", b=24)
+            cur = lbs[b % 2][:, 1 + j0:1 + j1, :].rearrange("p n (a b) -> p n a b", b=24)
+            prv = lbs[b % 2][:, j0:j1, :].rearrange("p n (a b) -> p n a b", b=24)
+            l4 = lsh[:, j0:j1, :].rearrange("p n (a b) -> p n a b", b=24)
             nc.tensor.matmul(out=l4[:, :, :, 0:16], lhsT=e32[:, 127:255], rhs=cur[:, :, :, 0:16], start=True, stop=False)
             nc.tensor.matmul(out=l4[:, :, :, 0:16], lhsT=e32[:, 255:383], rhs=prv[:, :, :, 0:16], start=False, stop=True)
             nc.tensor.matmul(out=l4[:, :, 0:2, 16:24], lhsT=e32[:, 98:226], rhs=cur[:, :, 0:2, 16:24], start=True, stop=False)
             nc.tensor.matmul(out=l4[:, :, 0:2, 16:24], lhsT=e32[:, 226:354], rhs=prv[:, :, 0:2, 16:24], start=False, stop=True)
 
-        def fin_c(b):
+        def fin_c(b, j0=0, j1=NB, s0=None):
             if not 0 <= b < nbat:
                 return
             t0 = NB * b
-            n = NB + (1 if b == nbat - 1 else 0)
             y = ys[b % 3]
+            last = b == nbat - 1 and j1 > NB
             for t in range(2, 9):
                 nc.scalar.copy(
-                    out=y[:, 0:n, 57 * t + 1:58 * t],
-                    in_=lsh[:, 0:n, 8 * (t - 1) + 8 - t:8 * (t - 1) + 7],
+                    out=y[:, j0:j1, 57 * t + 1:58 * t],
+                    in_=lsh[:, j0:j1, 8 * (t - 1) + 8 - t:8 * (t - 1) + 7],
                 )
             nc.vector.tensor_tensor(
-                out=y[:, 0:n, 58:465:58], in0=lsh[:, 0:n, 7:64:8], in1=y[:, 0:n, 58:465:58], op=ALU.add)
-            for t in range(9):
+                out=y[:, j0:j1, 58:465:58], in0=lsh[:, j0:j1, 7:64:8], in1=y[:, j0:j1, 58:465:58], op=ALU.add)
+            if s0 is None:
+                s0 = j0
+            for t in range(9 if s0 >= 0 else 0):
                 d = DELTA[t]
                 c0 = 56 * t
                 wd = WID[t]
                 st = START[t]
-                k0, k1 = 0, NB
+                k0, k1 = s0, min(j1, NB)
                 if b == 0 and d > 0:
                     nc.sync.dma_start(out=out_flat[0:P - d, c0:c0 + wd], in_=y[d:P, 0, st:st + wd])
                     k0 = 1
-                if b == nbat - 1 and d < 0:
+                if last and d < 0:
                     r0 = P * (NT - 1) - d
                     nc.sync.dma_start(out=out_flat[r0:P * NT, c0:c0 + wd], in_=y[0:P + d, NB - 1, st:st + wd])
                     k1 = NB - 1
-                if b == nbat - 1 and d > 1:
+                if last and d > 1:
                     nc.sync.dma_start(out=out_flat[P * NT - d:P * NT, c0:c0 + wd], in_=y[0:d, NB, st:st + wd])
-                if b == nbat - 1 and d == 1:
+                if last and d == 1:
                     nc.gpsimd.dma_start(
                         out=out_flat[P * NT - 1:P * NT, c0:c0 + wd].rearrange("o (a c) -> (o a) c", c=8),
                         in_=y[0:7, NB, st:st + 8],
@@ -465,7 +501,8 @@ def tile_involution2d_pa_kernel(tc, x_words, x_scales, Wi_words, Wi_scales, bi, 
                     )
 
         wshift(0)
-        for u in range(-2, nu + 1):
+        wsevac(0)
+        for u in range(-2, nu - 2):
             if u < 0:
                 load_chunk(u + 3)
             if u >= 0 and u % 2 == 0 and u // 2 + 3 < nbat:
@@ -476,10 +513,20 @@ def tile_involution2d_pa_kernel(tc, x_words, x_scales, Wi_words, Wi_scales, bi, 
                 load_w((u + 2) // 4 + 1)
             back_s(u - 2)
             fwd_s(u - 1, 0, 2)
-            bias(u + 1)
+            head = u < 2
+            if head:
+                for k in range(2):
+                    bias(u + 1, k, k + 1)
+                    nmult("V", u + 1, VB, k, k + 1)
+                    if u == -1:
+                        xrcopy(0, k, k + 1)
+                        nmult("G", 0, GB, k, k + 1)
+                        smult(0, k)
+            else:
+                bias(u + 1)
             mx(u + 2, 0, 0, 8)
             fwd_s(u - 1, 2, 4)
-            if u % 2 == 1:
+            if u % 2 == 1 and u > 0:
                 wsevac((u + 1) // 2)
             evacy_s(u - 2)
             if u % 2 == 0:
@@ -492,17 +539,64 @@ def tile_involution2d_pa_kernel(tc, x_words, x_scales, Wi_words, Wi_scales, bi, 
             mx(u + 2, 1, 0, 8)
             gpre(u - 1)
             pmult("G", u, GW, 0, GK)
-            nmult("G", u, GB)
-            nmult("V", u, VB)
-            pmult("V", u, VW)
+            if u > 0:
+                nmult("G", u, GB)
+            if not head:
+                nmult("V", u + 1, VB)
             vreduce(u - 1)
-            smult(u, 0)
-            xrcopy(u + 1)
-            smult(u, 1)
+            if u > 0:
+                smult(u, 0)
+            if u >= 0:
+                xrcopy(u + 1)
+            if u > 0:
+                smult(u, 1)
             evact_s(u - 1)
-        back_s(nu - 1)
-        evacy_s(nu - 1)
+        a, b, c = nu - 3, nu - 2, nu - 1
+        back_s(a - 1)
+        fwd_s(a)
+        bias(c)
+        evacy_s(a - 1)
+        fin_a(nbat - 3)
+        fin_b(nbat - 3)
+        pmult("G", b, GW, 0, GK)
+        nmult("G", b, GB)
+        fwd_n(a)
+        nmult("V", c, VB)
+        nmult("V", c, (3, 4), extra=True)
+        vreduce(a)
+        smult(b, 0)
+        xrcopy(c)
+        smult(b, 1)
+        evact_s(a)
+        evact_n(a)
+
+        back_s(a)
+        back_n(a)
+        evacy_s(a)
+        fin_c(nbat - 3)
+        pmult("G", c, GW, 0, 2)
+        nmult("G", c, (0, 1, 2))
+        fwd_s(b)
+        vreduce(b)
+        smult(c, 0, 1)
+        evact_s(b)
+        evacy_n(a)
+        fin_a(nbat - 2)
+        fin_b(nbat - 2)
+        back_s(b)
+        fwd_s(c, 0, 2)
+        smult(c, 1, 1)
+        vreduce(c, "cb")
+        evacy_s(b)
         fin_c(nbat - 2)
-        fin_a(nbat - 1)
-        fin_b(nbat - 1)
-        fin_c(nbat - 1)
+        fwd_s(c, 2, 4)
+        vreduce(c, "a")
+        fin_a(nbat - 1, 0, 2)
+        fin_b(nbat - 1, 0, 2)
+        evact_s(c)
+        back_s(c)
+        fin_c(nbat - 1, 0, 2, -1)
+        evacy_s(c)
+        fin_a(nbat - 1, 2, NB)
+        fin_b(nbat - 1, 2, NB + 1)
+        fin_c(nbat - 1, 2, NB + 1, 0)

@@ -538,19 +538,22 @@ def tile_involution2d_pa_kernel(tc, x_words, x_scales, Wi_words, Wi_scales, bi, 
                 wshift((u + 2) // 2)
             mx(u + 2, 1, 0, 8)
             gpre(u - 1)
+            if u > 0:
+                nmult("G", u, GB[0:2])
             pmult("G", u, GW, 0, GK)
             if u > 0:
-                nmult("G", u, GB)
+                nmult("G", u, GB[2:])
             if not head:
                 nmult("V", u + 1, VB)
             vreduce(u - 1)
             if u > 0:
                 smult(u, 0)
+                smult(u, 1, 0, 4)
+            evact_s(u - 1)
+            if u > 0:
+                smult(u, 1, 4, 8)
             if u >= 0:
                 xrcopy(u + 1)
-            if u > 0:
-                smult(u, 1)
-            evact_s(u - 1)
         a, b, c = nu - 3, nu - 2, nu - 1
         back_s(a - 1)
         fwd_s(a)

@@ -73,6 +73,7 @@ def tile_involution2d_pa_kernel(tc, x_words, x_scales, Wi_words, Wi_scales, bi, 
         wsb = [sb.tile([P, NB, NWP], BF16, name="wB%d" % i) for i in range(2)]
         pvg = [sb.tile([P, 2, 9 * NG], F32, name="pg%d" % i) for i in range(2)]
         pvv = [sb.tile([P, 2, 9 * NV], F32, name="pw%d" % i) for i in range(3)]
+        px4 = sb.tile([P, 2, 36], F32, name="px4")
         pvx = sb.tile([P, 2, 9 * 66], F32, name="px")
         pms = [sb.tile([P, 2, 9, 256], F32, name="pm%d" % i) for i in range(3)]
         ys = [sb.tile([P, NB + 1, YW], F32, name="y%d" % i) for i in range(3)]
@@ -82,7 +83,7 @@ def tile_involution2d_pa_kernel(tc, x_words, x_scales, Wi_words, Wi_scales, bi, 
 
         xips = [ps.tile([P, 512], F32, name="xiP%d" % i) for i in range(3)]
         wps = [ps.tile([P, NB, NWP], BF16, name="wP%d" % i) for i in range(2)]
-        lsh = ps.tile([P, NB + 1, 72], F32, name="lsh")
+        lsh0 = ps.tile([P, NB + 1, 72], F32, name="lsh")
         acct = ps.tile([P, 4 * P], F32, name="acct")
         yb = ps.tile([P, 4 * P], F32, name="yb")
 
@@ -425,10 +426,10 @@ def tile_involution2d_pa_kernel(tc, x_words, x_scales, Wi_words, Wi_scales, bi, 
                     in1=pms[u % 3][:, :, 8, P * h:P * (h + 1)].rearrange("p k (q c) -> p k q c", c=32),
                     op=ALU.add)
 
-        def fin_a(b, j0=0, j1=NB):
+        def fin_a(b, j0=0, j1=NB, eng="S"):
             if not 0 <= b < nbat:
                 return
-            nc.scalar.copy(
+            (nc.scalar.copy if eng == "S" else nc.vector.tensor_copy)(
                 out=lbs[b % 2][:, 1 + j0:1 + j1, 0:64].rearrange("p n (t c) -> p n t c", c=8),
                 in_=ys[b % 3][:, j0:j1, 50:514].rearrange("p n (t c) -> p n t c", c=58)[:, :, :, 0:8],
             )
@@ -438,9 +439,10 @@ def tile_involution2d_pa_kernel(tc, x_words, x_scales, Wi_words, Wi_scales, bi, 
                     in_=ys[b % 3][:, NB - 1, 50:514].rearrange("p (t c) -> p t c", c=58)[:, :, 0:8],
                 )
 
-        def fin_b(b, j0=0, j1=NB):
+        def fin_b(b, j0=0, j1=NB, bank=None):
             if not 0 <= b < nbat:
                 return
+            lsh = lsh0 if bank is None else bank
             cur = lbs[b % 2][:, 1 + j0:1 + j1, :].rearrange("p n (a b) -> p n a b", b=24)
             prv = lbs[b % 2][:, j0:j1, :].rearrange("p n (a b) -> p n a b", b=24)
             l4 = lsh[:, j0:j1, :].rearrange("p n (a b) -> p n a b", b=24)
@@ -449,19 +451,27 @@ def tile_involution2d_pa_kernel(tc, x_words, x_scales, Wi_words, Wi_scales, bi, 
             nc.tensor.matmul(out=l4[:, :, 0:2, 16:24], lhsT=e32[:, 98:226], rhs=cur[:, :, 0:2, 16:24], start=True, stop=False)
             nc.tensor.matmul(out=l4[:, :, 0:2, 16:24], lhsT=e32[:, 226:354], rhs=prv[:, :, 0:2, 16:24], start=False, stop=True)
 
-        def fin_c(b, j0=0, j1=NB, s0=None):
+        def fin_c(b, j0=0, j1=NB, s0=None, fix=True, eng="S", bank=None):
             if not 0 <= b < nbat:
                 return
             t0 = NB * b
             y = ys[b % 3]
+            lsh = lsh0 if bank is None else bank
             last = b == nbat - 1 and j1 > NB
-            for t in range(2, 9):
-                nc.scalar.copy(
-                    out=y[:, j0:j1, 57 * t + 1:58 * t],
-                    in_=lsh[:, j0:j1, 8 * (t - 1) + 8 - t:8 * (t - 1) + 7],
-                )
-            nc.vector.tensor_tensor(
-                out=y[:, j0:j1, 58:465:58], in0=lsh[:, j0:j1, 7:64:8], in1=y[:, j0:j1, 58:465:58], op=ALU.add)
+            for t in range(2, 9 if fix else 2):
+                if eng == "S":
+                    nc.scalar.copy(
+                        out=y[:, j0:j1, 57 * t + 1:58 * t],
+                        in_=lsh[:, j0:j1, 8 * (t - 1) + 8 - t:8 * (t - 1) + 7],
+                    )
+                else:
+                    nc.vector.tensor_copy(
+                        out=y[:, j0:j1, 57 * t + 1:58 * t],
+                        in_=lsh[:, j0:j1, 8 * (t - 1) + 8 - t:8 * (t - 1) + 7],
+                    )
+            if fix:
+                nc.vector.tensor_tensor(
+                    out=y[:, j0:j1, 58:465:58], in0=lsh[:, j0:j1, 7:64:8], in1=y[:, j0:j1, 58:465:58], op=ALU.add)
             if s0 is None:
                 s0 = j0
             for t in range(9 if s0 >= 0 else 0):
@@ -489,6 +499,23 @@ def tile_involution2d_pa_kernel(tc, x_words, x_scales, Wi_words, Wi_scales, bi, 
                     out=out_flat[r0:r0 + P * (k1 - k0), c0:c0 + wd].rearrange("(n p) c -> p n c", p=P),
                     in_=y[:, k0:k1, st:st + wd],
                 )
+
+        def early4_m(u):
+            g, t = WHOLE[3]
+            a0 = 9 + 288 * g - 512 * t + 9 * 28
+            cw = COL[(t, g)]
+            kk = 2 * (u % 2)
+            nc.vector.tensor_tensor(
+                out=px4[:].rearrange("p k (s m) -> p k s m", m=9),
+                in0=xps[u % 3][:, :, a0:a0 + 36].rearrange("p k (s m) -> p k s m", m=9),
+                in1=wps[(u // 2) % 2][:, kk:kk + 2, cw:cw + 9].unsqueeze(2).to_broadcast([P, 2, 4, 9]),
+                op=ALU.mult)
+
+        def early4_r(u):
+            kk = 2 * (u % 2)
+            nc.vector.tensor_reduce(
+                out=ys[(u // 2) % 3][:, kk:kk + 2, 224:228], in_=px4[:].rearrange("p k (s m) -> p k s m", m=9),
+                axis=AX.X, op=ALU.add)
 
         def zero_rows():
             for t in range(9):
@@ -555,6 +582,7 @@ def tile_involution2d_pa_kernel(tc, x_words, x_scales, Wi_words, Wi_scales, bi, 
             if u >= 0:
                 xrcopy(u + 1)
         a, b, c = nu - 3, nu - 2, nu - 1
+        lsh1 = xips[0][:, 0:(NB + 1) * 72].rearrange("p (n c) -> p n c", c=72)
         back_s(a - 1)
         fwd_s(a)
         bias(c)
@@ -566,6 +594,7 @@ def tile_involution2d_pa_kernel(tc, x_words, x_scales, Wi_words, Wi_scales, bi, 
         fwd_n(a)
         nmult("V", c, VB)
         nmult("V", c, (3, 4), extra=True)
+        early4_m(c)
         vreduce(a)
         smult(b, 0)
         xrcopy(c)
@@ -590,16 +619,18 @@ def tile_involution2d_pa_kernel(tc, x_words, x_scales, Wi_words, Wi_scales, bi, 
         fwd_s(c, 0, 2)
         smult(c, 1, 1)
         vreduce(c, "cb")
+        early4_r(c)
         evacy_s(b)
         fin_c(nbat - 2)
         fwd_s(c, 2, 4)
         vreduce(c, "a")
         fin_a(nbat - 1, 0, 2)
         fin_b(nbat - 1, 0, 2)
+        fin_a(nbat - 1, 2, NB, eng="V")
         evact_s(c)
+        fin_b(nbat - 1, 2, NB + 1, bank=lsh1)
         back_s(c)
         fin_c(nbat - 1, 0, 2, -1)
+        fin_c(nbat - 1, 2, NB + 1, -1, eng="V", bank=lsh1)
         evacy_s(c)
-        fin_a(nbat - 1, 2, NB)
-        fin_b(nbat - 1, 2, NB + 1)
-        fin_c(nbat - 1, 2, NB + 1, 0)
+        fin_c(nbat - 1, 2, NB + 1, 0, fix=False)

@@ -40,6 +40,7 @@ NV = 33 * len(VB)
 NPL = 8
 GW = (0,)
 NTL = 1
+GT = 6
 GK = 1
 VW = ()
 EVT = "S"
@@ -187,7 +188,7 @@ def tile_involution2d_pa_kernel(tc, x_words, x_scales, Wi_words, Wi_scales, bi, 
                 d = DELTA[t]
                 e = ebf[t % 3]
                 c0 = COL[(t, GLO[t])]
-                ncol = 9 * (GHI[t] - GLO[t] + 1)
+                ncol = WTP if t < GT else 9 * (GHI[t] - GLO[t] + 1)
                 w0 = 9 * GLO[t]
                 if t // 3 == 0:
                     ks = [k for k in range(NB) if (t0 + k) % 8 != 7]
@@ -239,9 +240,7 @@ def tile_involution2d_pa_kernel(tc, x_words, x_scales, Wi_words, Wi_scales, bi, 
             nc.scalar.copy(out=wss[b % 2][:, :, 0:9], in_=wp4[:, :, 0, 0:9])
             nc.scalar.copy(
                 out=wss[b % 2][:, :, 9:81].rearrange("p k (t c) -> p k t c", c=9), in_=wp4[:, :, 1:9, 9:18])
-            wb4 = wsb[b % 2][:].rearrange("p k (t x) -> p k t x", x=WTP)
-            nc.scalar.copy(out=wb4[:, :, 0:6, 0:18], in_=wp4[:, :, 0:6, 0:18])
-            nc.scalar.copy(out=wb4[:, :, 1:4, 18:27], in_=wp4[:, :, 1:4, 18:27])
+            nc.scalar.copy(out=wsb[b % 2][:, :, 0:WTP * GT], in_=wps[b % 2][:, :, 0:WTP * GT])
 
         def nmult(eng, u, order, k0=0, k1=2, extra=False):
             if not 0 <= u < nu:

@@ -61,6 +61,8 @@ def tile_involution2d_pa_kernel(tc, x_words, x_scales, Wi_words, Wi_scales, bi, 
         xss = [sb.tile([P, PASSES, 512], U8, name="xs%d" % i, align_bytes=64) for i in range(3)]
         w_sb = sb.tile([P, 3 * 8, 144], BF16, name="w_sb")
         bias_bf = sb.tile([P, 512], BF16, name="bias_bf")
+        brow = sb.tile([P, 512], BF16, name="brow")
+        ones = sb.tile([P, P], BF16, name="ones")
         ident = sb.tile([P, P], F32, name="ident")
         e32 = sb.tile([P, 384], F32, name="e32")
         ebf = [sb.tile([P, 384], BF16, name="ebf%d" % j) for j in range(3)]
@@ -112,11 +114,16 @@ def tile_involution2d_pa_kernel(tc, x_words, x_scales, Wi_words, Wi_scales, bi, 
 
         ctx.enter_context(tc.manual_schedule())
 
+        nc.vector.memset(brow[:], 0.0)
         nc.vector.memset(wis[:].bitcast(I32), 0)
         nc.vector.memset(xss[0][:].bitcast(I32), 0)
+        nc.vector.memset(ones[:], 1.0)
         nc.scalar.dma_start(
             out=w_sb[:, 0:8, :], in_=w_flat[0:1024, :].rearrange("(n p) c -> p n c", p=P))
-        nc.gpsimd.dma_start(out=bias_bf[:], in_=bi.partition_broadcast(P))
+        nc.gpsimd.dma_start(out=brow[0:1, :], in_=bi.rearrange("(o n) -> o n", o=1))
+        for i in range(3):
+            nc.tensor.matmul(out=acct[:], lhsT=ones[:], rhs=brow[:], start=True, stop=True)
+        nc.scalar.copy(out=bias_bf[:], in_=acct[:])
         xc0 = xcs[0][:].rearrange("p g n -> p (g n)").rearrange("p (k g n) -> p k g n", k=NB, g=PASSES)
 
         def load_first(kk):
@@ -160,12 +167,15 @@ def tile_involution2d_pa_kernel(tc, x_words, x_scales, Wi_words, Wi_scales, bi, 
         nu = NT // 2
         nbat = NT // NB
 
+        def pos(u):
+            return 2 * (u % 2) if u < nu - 2 else 2 * ((u + 1) % 2)
+
         def mx(u, k, g0, g1):
             if not 0 <= u < nu:
                 return
             xc = xcs[(u // 2) % 3]
             xs = xss[(u // 2) % 3]
-            kk = 2 * (u % 2) + k
+            kk = pos(u) + k
             acc = xips[(2 * u + k) % 3]
             for g in range(g0, g1):
                 nc.tensor.matmul_mx(
@@ -248,12 +258,12 @@ def tile_involution2d_pa_kernel(tc, x_words, x_scales, Wi_words, Wi_scales, bi, 
             xp = xps[u % 3][:, k0:k1, :]
             if eng == "V":
                 e = nc.vector
-                wp = wps[(u // 2) % 2][:, 2 * (u % 2) + k0:2 * (u % 2) + k1, :]
+                wp = wps[(u // 2) % 2][:, pos(u) + k0:pos(u) + k1, :]
                 pv = (pvx if extra else pvv[u % 3])[:, k0:k1, :]
                 base = 99 if extra else NG
             else:
                 e = nc.gpsimd
-                wp = wsb[(u // 2) % 2][:, 2 * (u % 2) + k0:2 * (u % 2) + k1, :]
+                wp = wsb[(u // 2) % 2][:, pos(u) + k0:pos(u) + k1, :]
                 pv = pvg[u % 2][:, k0:k1, :]
                 base = 0
             for b, (g, ta) in [(i, SPLIT[i]) for i in order]:
@@ -287,7 +297,7 @@ def tile_involution2d_pa_kernel(tc, x_words, x_scales, Wi_words, Wi_scales, bi, 
         def pmult(eng, u, gis, k0=0, k1=2):
             if not 0 <= u < nu:
                 return
-            kk = 2 * (u % 2)
+            kk = pos(u)
             e = nc.vector if eng == "V" else nc.gpsimd
             w = (wps if eng == "V" else wsb)[(u // 2) % 2][:, kk + k0:kk + k1, :]
             for gi in gis:
@@ -332,7 +342,7 @@ def tile_involution2d_pa_kernel(tc, x_words, x_scales, Wi_words, Wi_scales, bi, 
 
         def evacy_n(u):
             y = ys[(u // 2) % 3]
-            s0 = 2 * (u % 2)
+            s0 = pos(u)
             yn = xips[2][:, 0:2 * P].rearrange("p (k c) -> p k c", k=2)
             nc.scalar.copy(
                 out=y[:, s0:s0 + 2, 33:33 + 195].rearrange("p k (q c) -> p k q c", c=65)[:, :, :, 0:33],
@@ -343,7 +353,7 @@ def tile_involution2d_pa_kernel(tc, x_words, x_scales, Wi_words, Wi_scales, bi, 
             if not 0 <= u < nu:
                 return
             y = ys[(u // 2) % 3]
-            s0 = 2 * (u % 2)
+            s0 = pos(u)
             pg = pvg[u % 2]
             pw = pvv[u % 3]
             for part in parts:
@@ -370,7 +380,7 @@ def tile_involution2d_pa_kernel(tc, x_words, x_scales, Wi_words, Wi_scales, bi, 
             xr = xrs[u % 3]
             ws = wss[(u // 2) % 2]
             pm = pms[u % 3]
-            kk = 2 * (u % 2) + k
+            kk = pos(u) + k
             for gi, (g, t) in enumerate(WHOLE):
                 if not g0 <= gi < g1 or (gi in GW and k < GK) or gi in VW:
                     continue
@@ -416,7 +426,7 @@ def tile_involution2d_pa_kernel(tc, x_words, x_scales, Wi_words, Wi_scales, bi, 
         def evacy_s(u):
             if not 0 <= u < nu:
                 return
-            s0 = 2 * (u % 2)
+            s0 = pos(u)
             for h in range(2):
                 nc.vector.tensor_tensor(
                     out=ys[(u // 2) % 3][:, s0:s0 + 2, 1 + 293 * h:1 + 293 * h + 260].rearrange(
@@ -450,7 +460,7 @@ def tile_involution2d_pa_kernel(tc, x_words, x_scales, Wi_words, Wi_scales, bi, 
             nc.tensor.matmul(out=l4[:, :, 0:2, 16:24], lhsT=e32[:, 98:226], rhs=cur[:, :, 0:2, 16:24], start=True, stop=False)
             nc.tensor.matmul(out=l4[:, :, 0:2, 16:24], lhsT=e32[:, 226:354], rhs=prv[:, :, 0:2, 16:24], start=False, stop=True)
 
-        def fin_c(b, j0=0, j1=NB, s0=None, fix=True, eng="S", bank=None):
+        def fin_c(b, j0=0, j1=NB, s0=None, fix=True, eng="S", bank=None, gq=(), taps=tuple(range(9))):
             if not 0 <= b < nbat:
                 return
             t0 = NB * b
@@ -473,7 +483,7 @@ def tile_involution2d_pa_kernel(tc, x_words, x_scales, Wi_words, Wi_scales, bi, 
                     out=y[:, j0:j1, 58:465:58], in0=lsh[:, j0:j1, 7:64:8], in1=y[:, j0:j1, 58:465:58], op=ALU.add)
             if s0 is None:
                 s0 = j0
-            for t in range(9 if s0 >= 0 else 0):
+            for t in (taps if s0 >= 0 else ()):
                 d = DELTA[t]
                 c0 = 56 * t
                 wd = WID[t]
@@ -494,16 +504,17 @@ def tile_involution2d_pa_kernel(tc, x_words, x_scales, Wi_words, Wi_scales, bi, 
                         in_=y[0:7, NB, st:st + 8],
                     )
                 r0 = P * (t0 + k0) - d
-                nc.sync.dma_start(
-                    out=out_flat[r0:r0 + P * (k1 - k0), c0:c0 + wd].rearrange("(n p) c -> p n c", p=P),
-                    in_=y[:, k0:k1, st:st + wd],
-                )
+                if k1 > k0:
+                    (nc.gpsimd if t in gq else nc.sync).dma_start(
+                        out=out_flat[r0:r0 + P * (k1 - k0), c0:c0 + wd].rearrange("(n p) c -> p n c", p=P),
+                        in_=y[:, k0:k1, st:st + wd],
+                    )
 
         def early4_m(u):
             g, t = WHOLE[3]
             a0 = 9 + 288 * g - 512 * t + 9 * 28
             cw = COL[(t, g)]
-            kk = 2 * (u % 2)
+            kk = pos(u)
             nc.vector.tensor_tensor(
                 out=px4[:].rearrange("p k (s m) -> p k s m", m=9),
                 in0=xps[u % 3][:, :, a0:a0 + 36].rearrange("p k (s m) -> p k s m", m=9),
@@ -511,7 +522,7 @@ def tile_involution2d_pa_kernel(tc, x_words, x_scales, Wi_words, Wi_scales, bi, 
                 op=ALU.mult)
 
         def early4_r(u):
-            kk = 2 * (u % 2)
+            kk = pos(u)
             nc.vector.tensor_reduce(
                 out=ys[(u // 2) % 3][:, kk:kk + 2, 224:228], in_=px4[:].rearrange("p k (s m) -> p k s m", m=9),
                 axis=AX.X, op=ALU.add)
@@ -582,6 +593,7 @@ def tile_involution2d_pa_kernel(tc, x_words, x_scales, Wi_words, Wi_scales, bi, 
                 xrcopy(u + 1)
         a, b, c = nu - 3, nu - 2, nu - 1
         lsh1 = xips[0][:, 0:(NB + 1) * 72].rearrange("p (n c) -> p n c", c=72)
+        lsh2 = xips[2][:, 0:(NB + 1) * 72].rearrange("p (n c) -> p n c", c=72)
         back_s(a - 1)
         fwd_s(a)
         bias(c)
@@ -616,20 +628,23 @@ def tile_involution2d_pa_kernel(tc, x_words, x_scales, Wi_words, Wi_scales, bi, 
         fin_b(nbat - 2)
         back_s(b)
         fwd_s(c, 0, 2)
-        smult(c, 1, 1)
-        vreduce(c, "cb")
-        early4_r(c)
+        smult(c, 1, 1, 4)
+        vreduce(c, "c")
         evacy_s(b)
-        fin_c(nbat - 2)
-        fwd_s(c, 2, 4)
-        vreduce(c, "a")
-        fin_a(nbat - 1, 0, 2)
-        fin_b(nbat - 1, 0, 2)
         fin_a(nbat - 1, 2, NB, eng="V")
+        fin_c(nbat - 2)
+        smult(c, 1, 4, 8)
+        fin_b(nbat - 1, 3, NB + 1, bank=lsh2)
+        fwd_s(c, 2, 4)
+        vreduce(c, "b")
+        early4_r(c)
+        fin_c(nbat - 1, 3, NB + 1, 3, eng="V", bank=lsh2)
+        vreduce(c, "a")
+        fin_a(nbat - 1, 0, 2, eng="V")
         evact_s(c)
-        fin_b(nbat - 1, 2, NB + 1, bank=lsh1)
+        fin_b(nbat - 1, 0, 3, bank=lsh1)
         back_s(c)
-        fin_c(nbat - 1, 0, 2, -1)
-        fin_c(nbat - 1, 2, NB + 1, -1, eng="V", bank=lsh1)
+        fin_c(nbat - 1, 0, 3, -1, eng="V", bank=lsh1)
+        fin_c(nbat - 1, 0, 3, 0, fix=False, taps=(4,))
         evacy_s(c)
-        fin_c(nbat - 1, 2, NB + 1, 0, fix=False)
+        fin_c(nbat - 1, 0, 3, 0, fix=False, taps=(0, 1, 2, 3, 5, 6, 7, 8))

@@ -40,6 +40,7 @@ NV = 33 * len(VB)
 NPL = 8
 GW = (0,)
 NTL = 1
+WA = 5
 GT = 6
 GK = 1
 VW = ()
@@ -188,13 +189,13 @@ def tile_involution2d_pa_kernel(tc, x_words, x_scales, Wi_words, Wi_scales, bi, 
                     stop=(g == PASSES - 1),
                 )
 
-        def wshift(b):
+        def wshift(b, ta=0, tb=9):
             if not 0 <= b < nbat:
                 return
             wp = wps[b % 2]
             t0 = NB * b
             w0t = 8 * ((t0 // 8) % 3) + t0 % 8
-            for t in range(9):
+            for t in range(ta, tb):
                 d = DELTA[t]
                 e = ebf[t % 3]
                 c0 = COL[(t, GLO[t])]
@@ -549,7 +550,14 @@ def tile_involution2d_pa_kernel(tc, x_words, x_scales, Wi_words, Wi_scales, bi, 
             if u % 4 == 2 and (u + 2) // 4 + 1 < 8:
                 load_w((u + 2) // 4 + 1)
             back_s(u - 2)
-            fwd_s(u - 1, 0, 2)
+            fwd_s(u - 1, 0, 1)
+            if u == 0:
+                wshift(1)
+            if u % 2 == 1 and u > 0:
+                wshift((u + 3) // 2, WA, 9)
+            if u % 2 == 0 and u > 0:
+                wshift((u + 2) // 2, 0, WA)
+            fwd_s(u - 1, 1, 2)
             head = u < 2
             if head:
                 for k in range(2):
@@ -562,7 +570,7 @@ def tile_involution2d_pa_kernel(tc, x_words, x_scales, Wi_words, Wi_scales, bi, 
             else:
                 bias(u + 1)
             mx(u + 2, 0, 0, 8)
-            fwd_s(u - 1, 2, 4)
+            fwd_s(u - 1, 2, 3)
             if u % 2 == 1 and u > 0:
                 wsevac((u + 1) // 2)
             evacy_s(u - 2)
@@ -571,8 +579,7 @@ def tile_involution2d_pa_kernel(tc, x_words, x_scales, Wi_words, Wi_scales, bi, 
                 fin_b((u - 4) // 2)
             else:
                 fin_c((u - 5) // 2)
-            if u % 2 == 0 and u >= 0:
-                wshift((u + 2) // 2)
+            fwd_s(u - 1, 3, 4)
             mx(u + 2, 1, 0, 8)
             gpre(u - 1)
             if u > 0:

@@ -40,9 +40,11 @@ NV = 33 * len(VB)
 NPL = 8
 GW = (0,)
 NTL = 1
-WA = 5
-GT = 6
-GK = 1
+WA = 4
+GT = 7
+GK = 2
+GBN = (0, 1, 2, 3, 4, 5)
+VBN = (6, 7)
 VW = ()
 EVT = "S"
 
@@ -58,8 +60,10 @@ def tile_involution2d_pa_kernel(tc, x_words, x_scales, Wi_words, Wi_scales, bi, 
 
         wic = sb.tile([P, PASSES, 1024], U8, name="wic", align_bytes=64)
         wis = sb.tile([P, PASSES, 512], U8, name="wis", align_bytes=64)
-        xcs = [sb.tile([P, PASSES, 1024], U8, name="xc%d" % i, align_bytes=64) for i in range(3)]
-        xss = [sb.tile([P, PASSES, 512], U8, name="xs%d" % i, align_bytes=64) for i in range(3)]
+        xcs = [sb.tile([P, PASSES, 1024], U8, name="xc%d" % i, align_bytes=64) for i in range(2)]
+        xss = [sb.tile([P, PASSES, 512], U8, name="xs%d" % i, align_bytes=64) for i in range(2)]
+        pm5s = [sb.tile([P, 9, P], F32, name="pf%d" % i) for i in range(2)]
+        yt5 = sb.tile([P, P], F32, name="yt5")
         w_sb = sb.tile([P, 3 * 8, 144], BF16, name="w_sb")
         bias_bf = sb.tile([P, 512], BF16, name="bias_bf")
         brow = sb.tile([P, 512], BF16, name="brow")
@@ -99,8 +103,8 @@ def tile_involution2d_pa_kernel(tc, x_words, x_scales, Wi_words, Wi_scales, bi, 
                 )
 
         def load_chunk(c):
-            xc = xcs[c % 3]
-            xs = xss[c % 3]
+            xc = xcs[c % 2]
+            xs = xss[c % 2]
             nc.sync.dma_start(
                 out=xc[:].bitcast(I32),
                 in_=x_words[:, :, 1024 * c:1024 * (c + 1)].rearrange("g p n -> p g n").bitcast(I32),
@@ -156,9 +160,11 @@ def tile_involution2d_pa_kernel(tc, x_words, x_scales, Wi_words, Wi_scales, bi, 
         nc.vector.tensor_scalar(out=ebf[0][:], in0=e32[:], scalar1=mask[:, 0:1], scalar2=None, op0=ALU.mult)
         nc.vector.tensor_copy(out=ebf[1][:], in_=e32[:])
         nc.vector.tensor_scalar(out=ebf[2][:], in0=e32[:], scalar1=mask[:, 1:2], scalar2=None, op0=ALU.mult)
+        nc.vector.memset(xss[1][:].bitcast(I32), 0)
         for i in range(1, 3):
-            nc.vector.memset(xss[i][:].bitcast(I32), 0)
             nc.vector.memset(xps[i][:], 0.0)
+        for i in range(2):
+            nc.gpsimd.memset(pm5s[i][:], 0.0)
         nc.vector.memset(zt[:], 0.0)
         nc.vector.memset(lbs[0][:, 0, :], 0.0)
         nc.vector.memset(lbs[(NT // NB - 1) % 2][:, NB + 1, :], 0.0)
@@ -171,11 +177,14 @@ def tile_involution2d_pa_kernel(tc, x_words, x_scales, Wi_words, Wi_scales, bi, 
         def pos(u):
             return 2 * (u % 2) if u < nu - 2 else 2 * ((u + 1) % 2)
 
+        def newdiv(u):
+            return u < nu - 3
+
         def mx(u, k, g0, g1):
             if not 0 <= u < nu:
                 return
-            xc = xcs[(u // 2) % 3]
-            xs = xss[(u // 2) % 3]
+            xc = xcs[(u // 2) % 2]
+            xs = xss[(u // 2) % 2]
             kk = pos(u) + k
             acc = xips[(2 * u + k) % 3]
             for g in range(g0, g1):
@@ -257,6 +266,7 @@ def tile_involution2d_pa_kernel(tc, x_words, x_scales, Wi_words, Wi_scales, bi, 
             if not 0 <= u < nu:
                 return
             xp = xps[u % 3][:, k0:k1, :]
+            new = newdiv(u) and eng == "G"
             if eng == "V":
                 e = nc.vector
                 wp = wps[(u // 2) % 2][:, pos(u) + k0:pos(u) + k1, :]
@@ -277,14 +287,22 @@ def tile_involution2d_pa_kernel(tc, x_words, x_scales, Wi_words, Wi_scales, bi, 
                     segs.append((ta + 1, ta + 1, n2, 33 * b + n1))
                 for (t, a, n, o) in segs:
                     cw = COL[(t, g)]
-                    o = o - base
+                    o = o - base - (56 if new and b >= 4 else 0)
                     e.tensor_tensor(
                         out=pv[:, :, 9 * o:9 * (o + n)].rearrange("p k (s m) -> p k s m", m=9),
                         in0=xp[:, :, a:a + 9 * n].rearrange("p k (s m) -> p k s m", m=9),
                         in1=wp[:, :, cw:cw + 9].unsqueeze(2).to_broadcast([P, k1 - k0, n, 9]),
                         op=ALU.mult,
                     )
-                if g == 7:
+                if g == 7 and new:
+                    cw = COL[(4, 7)]
+                    e.tensor_tensor(
+                        out=pv[:, :, 9 * 103:9 * 105].rearrange("p k (h m) -> p k h m", m=9),
+                        in0=xp[:, :, 4:4 + 522].rearrange("p k (s m) -> p k s m", m=9)[:, :, 0:58:57, :],
+                        in1=wp[:, :, cw:cw + 18].rearrange("p k (h m) -> p k h m", m=9),
+                        op=ALU.mult,
+                    )
+                if g == 7 and not new:
                     for k in range(k1 - k0):
                         cw = COL[(4, 7)]
                         e.tensor_tensor(
@@ -357,6 +375,24 @@ def tile_involution2d_pa_kernel(tc, x_words, x_scales, Wi_words, Wi_scales, bi, 
             s0 = pos(u)
             pg = pvg[u % 2]
             pw = pvv[u % 3]
+            if newdiv(u):
+                nc.vector.tensor_reduce(
+                    out=y[:, s0:s0 + 2, 33:33 + 195].rearrange("p k (q c) -> p k q c", c=65)[:, :, :, 0:33],
+                    in_=pg[:, :, 0:9 * 99].rearrange("p k (q s m) -> p k q s m", q=3, m=9),
+                    axis=AX.X, op=ALU.add)
+                nc.vector.tensor_reduce(
+                    out=y[:, s0:s0 + 2, 228:228 + 122].rearrange("p k (q c) -> p k q c", c=61)[:, :, :, 0:5],
+                    in_=pg[:, :, 9 * 99:9 * 109].rearrange("p k (q s m) -> p k q s m", q=2, m=9),
+                    axis=AX.X, op=ALU.add)
+                nc.vector.tensor_reduce(
+                    out=y[:, s0:s0 + 2, 326:359],
+                    in_=pg[:, :, 9 * 109:9 * 142].rearrange("p k (s m) -> p k s m", m=9),
+                    axis=AX.X, op=ALU.add)
+                nc.vector.tensor_reduce(
+                    out=y[:, s0:s0 + 2, 391:391 + 130].rearrange("p k (q c) -> p k q c", c=65)[:, :, :, 0:33],
+                    in_=pw[:, :, 9 * 33:9 * 99].rearrange("p k (q s m) -> p k q s m", q=2, m=9),
+                    axis=AX.X, op=ALU.add)
+                return
             for part in parts:
                 if part == "a" and not tailn(u):
                     nc.vector.tensor_reduce(
@@ -374,6 +410,51 @@ def tile_involution2d_pa_kernel(tc, x_words, x_scales, Wi_words, Wi_scales, bi, 
                         out=y[:, s0:s0 + 2, 326:326 + 195].rearrange("p k (q c) -> p k q c", c=65)[:, :, :, 0:33],
                         in_=pw[:].rearrange("p k (q s m) -> p k q s m", q=3, m=9),
                         axis=AX.X, op=ALU.add)
+
+        def five(u):
+            return xips[(2 * (u + 1)) % 3]
+
+        def tmult(u):
+            if not (0 <= u and newdiv(u)):
+                return
+            kk = pos(u)
+            w = wps[(u // 2) % 2][:, kk:kk + 2, :]
+            cw = COL[(4, 7)]
+            pm = pm5s[u % 2][:].rearrange("p m (k c) -> p k m c", k=2)
+            for h in range(2):
+                for (m0, m1, r, a) in [(0, 5, 4, 28 * h), (5, 9, 0, 28 * h + 1)]:
+                    nc.vector.tensor_tensor(
+                        out=pm[:, :, m0:m1, 28 * h:28 * h + 28],
+                        in0=xrs[u % 3][:, :, r:r + m1 - m0, a:a + 28],
+                        in1=w[:, :, cw + 9 * h + m0:cw + 9 * h + m1].unsqueeze(3).to_broadcast([P, 2, m1 - m0, 28]),
+                        op=ALU.mult,
+                    )
+
+        def fwd5(u):
+            if not (0 <= u and newdiv(u)):
+                return
+            for m in range(9):
+                nc.tensor.matmul(
+                    out=five(u)[:, 0:P], lhsT=pm5s[u % 2][:, m, :], rhs=ident[:],
+                    is_transpose=True, start=(m == 0), stop=(m == 8))
+
+        def evact5(u):
+            if not (0 <= u and newdiv(u)):
+                return
+            nc.scalar.copy(out=yt5[:], in_=five(u)[:, 0:P])
+
+        def back5(u):
+            if not (0 <= u and newdiv(u)):
+                return
+            nc.tensor.transpose(out=five(u)[:, P:2 * P], in_=yt5[:], identity=ident[:])
+
+        def evacy5(u):
+            if not (0 <= u and newdiv(u)):
+                return
+            s0 = pos(u)
+            nc.vector.tensor_copy(
+                out=ys[(u // 2) % 3][:, s0:s0 + 2, 233:289],
+                in_=five(u)[:, P:2 * P].rearrange("p (k c) -> p k c", k=2)[:, :, 0:56])
 
         def smult(u, k, g0=0, g1=8):
             if not 0 <= u < nu:
@@ -541,34 +622,35 @@ def tile_involution2d_pa_kernel(tc, x_words, x_scales, Wi_words, Wi_scales, bi, 
         wshift(0)
         wsevac(0)
         for u in range(-2, nu - 2):
-            if u < 0:
-                load_chunk(u + 3)
-            if u >= 0 and u % 2 == 0 and u // 2 + 3 < nbat:
-                load_chunk(u // 2 + 3)
+            if u == -2:
+                load_chunk(1)
+            if u >= 0 and u % 2 == 0 and u // 2 + 2 < nbat:
+                load_chunk(u // 2 + 2)
             if u == 0:
                 zero_rows()
             if u % 4 == 2 and (u + 2) // 4 + 1 < 8:
                 load_w((u + 2) // 4 + 1)
             back_s(u - 2)
+            back5(u - 2)
             fwd_s(u - 1, 0, 1)
             if u == 0:
                 wshift(1)
-            if u % 2 == 1 and u > 0:
-                wshift((u + 3) // 2, WA, 9)
             if u % 2 == 0 and u > 0:
-                wshift((u + 2) // 2, 0, WA)
+                wshift((u + 2) // 2, WA, 9)
             fwd_s(u - 1, 1, 2)
             head = u < 2
             if head:
                 for k in range(2):
                     bias(u + 1, k, k + 1)
-                    nmult("V", u + 1, VB, k, k + 1)
+                    nmult("V", u + 1, VBN, k, k + 1)
                     if u == -1:
                         xrcopy(0, k, k + 1)
-                        nmult("G", 0, GB, k, k + 1)
+                        nmult("G", 0, GBN, k, k + 1)
                         smult(0, k)
             else:
-                bias(u + 1)
+                bias(u + 1, 0, 1)
+                evacy5(u - 2)
+                bias(u + 1, 1, 2)
             mx(u + 2, 0, 0, 8)
             fwd_s(u - 1, 2, 3)
             if u % 2 == 1 and u > 0:
@@ -579,21 +661,27 @@ def tile_involution2d_pa_kernel(tc, x_words, x_scales, Wi_words, Wi_scales, bi, 
                 fin_b((u - 4) // 2)
             else:
                 fin_c((u - 5) // 2)
+            fwd5(u - 1)
+            if u % 2 == 0 and u > 0:
+                wshift((u + 2) // 2, 0, WA)
             fwd_s(u - 1, 3, 4)
             mx(u + 2, 1, 0, 8)
             gpre(u - 1)
+            gl = GBN if newdiv(u) else GB
             if u > 0:
-                nmult("G", u, GB[0:2])
+                nmult("G", u, gl[0:2])
             pmult("G", u, GW, 0, GK)
             if u > 0:
-                nmult("G", u, GB[2:])
+                nmult("G", u, gl[2:])
             if not head:
-                nmult("V", u + 1, VB)
+                nmult("V", u + 1, VBN if newdiv(u + 1) else VB)
+            tmult(u)
             vreduce(u - 1)
             if u > 0:
                 smult(u, 0)
                 smult(u, 1, 0, 4)
             evact_s(u - 1)
+            evact5(u - 1)
             if u > 0:
                 smult(u, 1, 4, 8)
             if u >= 0:
@@ -602,8 +690,10 @@ def tile_involution2d_pa_kernel(tc, x_words, x_scales, Wi_words, Wi_scales, bi, 
         lsh1 = xips[0][:, 0:(NB + 1) * 72].rearrange("p (n c) -> p n c", c=72)
         lsh2 = xips[2][:, 0:(NB + 1) * 72].rearrange("p (n c) -> p n c", c=72)
         back_s(a - 1)
+        back5(a - 1)
         fwd_s(a)
         bias(c)
+        evacy5(a - 1)
         evacy_s(a - 1)
         fin_a(nbat - 3)
         fin_b(nbat - 3)

@@ -43,8 +43,8 @@ NTL = 1
 WA = 4
 GT = 7
 GK = 2
-GBN = (0, 1, 2, 3, 4, 5)
-VBN = (6, 7)
+GBN = (0, 1, 2, 5)
+VBN = (3, 4, 6, 7)
 VW = ()
 EVT = "S"
 
@@ -266,7 +266,7 @@ def tile_involution2d_pa_kernel(tc, x_words, x_scales, Wi_words, Wi_scales, bi, 
             if not 0 <= u < nu:
                 return
             xp = xps[u % 3][:, k0:k1, :]
-            new = newdiv(u) and eng == "G"
+            new = newdiv(u) and not extra
             if eng == "V":
                 e = nc.vector
                 wp = wps[(u // 2) % 2][:, pos(u) + k0:pos(u) + k1, :]
@@ -280,6 +280,13 @@ def tile_involution2d_pa_kernel(tc, x_words, x_scales, Wi_words, Wi_scales, bi, 
             for b, (g, ta) in [(i, SPLIT[i]) for i in order]:
                 n1 = 57 * ta + 56 - 32 * g + 1
                 n2 = 33 - n1
+                shift = base
+                if new and eng == "G" and b >= 4:
+                    shift = 56
+                if new and eng == "V" and b == 3:
+                    shift = 99
+                if new and eng == "V" and b == 4:
+                    shift = 155
                 segs = []
                 if not (g == 8):
                     segs.append((ta, ta + 9 * (32 * g - 57 * ta + 1), n1, 33 * b))
@@ -287,7 +294,7 @@ def tile_involution2d_pa_kernel(tc, x_words, x_scales, Wi_words, Wi_scales, bi, 
                     segs.append((ta + 1, ta + 1, n2, 33 * b + n1))
                 for (t, a, n, o) in segs:
                     cw = COL[(t, g)]
-                    o = o - base - (56 if new and b >= 4 else 0)
+                    o = o - shift
                     e.tensor_tensor(
                         out=pv[:, :, 9 * o:9 * (o + n)].rearrange("p k (s m) -> p k s m", m=9),
                         in0=xp[:, :, a:a + 9 * n].rearrange("p k (s m) -> p k s m", m=9),
@@ -297,7 +304,7 @@ def tile_involution2d_pa_kernel(tc, x_words, x_scales, Wi_words, Wi_scales, bi, 
                 if g == 7 and new:
                     cw = COL[(4, 7)]
                     e.tensor_tensor(
-                        out=pv[:, :, 9 * 103:9 * 105].rearrange("p k (h m) -> p k h m", m=9),
+                        out=pv[:, :, 9 * (103 - shift):9 * (105 - shift)].rearrange("p k (h m) -> p k h m", m=9),
                         in0=xp[:, :, 4:4 + 522].rearrange("p k (s m) -> p k s m", m=9)[:, :, 0:58:57, :],
                         in1=wp[:, :, cw:cw + 18].rearrange("p k (h m) -> p k h m", m=9),
                         op=ALU.mult,
@@ -382,7 +389,7 @@ def tile_involution2d_pa_kernel(tc, x_words, x_scales, Wi_words, Wi_scales, bi, 
                     axis=AX.X, op=ALU.add)
                 nc.vector.tensor_reduce(
                     out=y[:, s0:s0 + 2, 228:228 + 122].rearrange("p k (q c) -> p k q c", c=61)[:, :, :, 0:5],
-                    in_=pg[:, :, 9 * 99:9 * 109].rearrange("p k (q s m) -> p k q s m", q=2, m=9),
+                    in_=pw[:, :, 0:9 * 10].rearrange("p k (q s m) -> p k q s m", q=2, m=9),
                     axis=AX.X, op=ALU.add)
                 nc.vector.tensor_reduce(
                     out=y[:, s0:s0 + 2, 326:359],

@@ -643,7 +643,7 @@ def tile_involution2d_pa_kernel(tc, x_words, x_scales, Wi_words, Wi_scales, bi, 
             if u == 0:
                 wshift(1)
             if u % 2 == 0 and u > 0:
-                wshift((u + 2) // 2, WA, 9)
+                wshift((u + 2) // 2, 0, WA)
             fwd_s(u - 1, 1, 2)
             head = u < 2
             if head:
@@ -658,6 +658,7 @@ def tile_involution2d_pa_kernel(tc, x_words, x_scales, Wi_words, Wi_scales, bi, 
                 bias(u + 1, 0, 1)
                 evacy5(u - 2)
                 bias(u + 1, 1, 2)
+            tmult(u)
             mx(u + 2, 0, 0, 8)
             fwd_s(u - 1, 2, 3)
             if u % 2 == 1 and u > 0:
@@ -669,8 +670,8 @@ def tile_involution2d_pa_kernel(tc, x_words, x_scales, Wi_words, Wi_scales, bi, 
             else:
                 fin_c((u - 5) // 2)
             fwd5(u - 1)
-            if u % 2 == 0 and u > 0:
-                wshift((u + 2) // 2, 0, WA)
+            if u % 2 == 1 and u > 0:
+                wshift((u + 3) // 2, WA, 9)
             fwd_s(u - 1, 3, 4)
             mx(u + 2, 1, 0, 8)
             gpre(u - 1)
@@ -682,7 +683,6 @@ def tile_involution2d_pa_kernel(tc, x_words, x_scales, Wi_words, Wi_scales, bi, 
                 nmult("G", u, gl[2:])
             if not head:
                 nmult("V", u + 1, VBN if newdiv(u + 1) else VB)
-            tmult(u)
             vreduce(u - 1)
             if u > 0:
                 smult(u, 0)

@@ -437,10 +437,16 @@ def tile_involution2d_pa_kernel(tc, x_words, x_scales, Wi_words, Wi_scales, bi, 
                         op=ALU.mult,
                     )
 
+        def gadd5(u):
+            if not (0 <= u and newdiv(u)):
+                return
+            pm = pm5s[u % 2]
+            nc.gpsimd.tensor_tensor(out=pm[:, 0:4, :], in0=pm[:, 0:4, :], in1=pm[:, 4:8, :], op=ALU.add)
+
         def fwd5(u):
             if not (0 <= u and newdiv(u)):
                 return
-            for m in range(9):
+            for m in (0, 1, 2, 3, 8):
                 nc.tensor.matmul(
                     out=five(u)[:, 0:P], lhsT=pm5s[u % 2][:, m, :], rhs=ident[:],
                     is_transpose=True, start=(m == 0), stop=(m == 8))
@@ -681,6 +687,7 @@ def tile_involution2d_pa_kernel(tc, x_words, x_scales, Wi_words, Wi_scales, bi, 
             pmult("G", u, GW, 0, GK)
             if u > 0:
                 nmult("G", u, gl[2:])
+            gadd5(u)
             if not head:
                 nmult("V", u + 1, VBN if newdiv(u + 1) else VB)
             vreduce(u - 1)

@@ -645,12 +645,11 @@ def tile_involution2d_pa_kernel(tc, x_words, x_scales, Wi_words, Wi_scales, bi, 
                 load_w((u + 2) // 4 + 1)
             back_s(u - 2)
             back5(u - 2)
-            fwd_s(u - 1, 0, 1)
+            fwd_s(u - 1, 0, 2)
             if u == 0:
                 wshift(1)
             if u % 2 == 0 and u > 0:
                 wshift((u + 2) // 2, 0, WA)
-            fwd_s(u - 1, 1, 2)
             head = u < 2
             if head:
                 for k in range(2):
@@ -670,15 +669,15 @@ def tile_involution2d_pa_kernel(tc, x_words, x_scales, Wi_words, Wi_scales, bi, 
             if u % 2 == 1 and u > 0:
                 wsevac((u + 1) // 2)
             evacy_s(u - 2)
+            fwd5(u - 1)
+            fwd_s(u - 1, 3, 4)
             if u % 2 == 0:
                 fin_a((u - 4) // 2)
                 fin_b((u - 4) // 2)
             else:
                 fin_c((u - 5) // 2)
-            fwd5(u - 1)
             if u % 2 == 1 and u > 0:
                 wshift((u + 3) // 2, WA, 9)
-            fwd_s(u - 1, 3, 4)
             mx(u + 2, 1, 0, 8)
             gpre(u - 1)
             gl = GBN if newdiv(u) else GB

@@ -427,7 +427,7 @@ def tile_involution2d_pa_kernel(tc, x_words, x_scales, Wi_words, Wi_scales, bi, 
             kk = pos(u)
             w = wps[(u // 2) % 2][:, kk:kk + 2, :]
             cw = COL[(4, 7)]
-            pm = pm5s[u % 2][:].rearrange("p m (k c) -> p k m c", k=2)
+            pm = pm5s[u % 2][:, :, 0:112].rearrange("p m (k c) -> p k m c", k=2)
             for h in range(2):
                 for (m0, m1, r, a) in [(0, 5, 4, 28 * h), (5, 9, 0, 28 * h + 1)]:
                     nc.vector.tensor_tensor(
@@ -441,7 +441,7 @@ def tile_involution2d_pa_kernel(tc, x_words, x_scales, Wi_words, Wi_scales, bi, 
             if not (0 <= u and newdiv(u)):
                 return
             pm = pm5s[u % 2]
-            nc.gpsimd.tensor_tensor(out=pm[:, 0:4, :], in0=pm[:, 0:4, :], in1=pm[:, 4:8, :], op=ALU.add)
+            nc.gpsimd.tensor_tensor(out=pm[:, 0:4, 0:112], in0=pm[:, 0:4, 0:112], in1=pm[:, 4:8, 0:112], op=ALU.add)
 
         def fwd5(u):
             if not (0 <= u and newdiv(u)):
@@ -467,7 +467,7 @@ def tile_involution2d_pa_kernel(tc, x_words, x_scales, Wi_words, Wi_scales, bi, 
             s0 = pos(u)
             nc.vector.tensor_copy(
                 out=ys[(u // 2) % 3][:, s0:s0 + 2, 233:289],
-                in_=five(u)[:, P:2 * P].rearrange("p (k c) -> p k c", k=2)[:, :, 0:56])
+                in_=five(u)[:, P:P + 112].rearrange("p (k c) -> p k c", k=2))
 
         def smult(u, k, g0=0, g1=8):
             if not 0 <= u < nu:

@@ -62,7 +62,7 @@ def tile_involution2d_pa_kernel(tc, x_words, x_scales, Wi_words, Wi_scales, bi, 
         wis = sb.tile([P, PASSES, 512], U8, name="wis", align_bytes=64)
         xcs = [sb.tile([P, PASSES, 1024], U8, name="xc%d" % i, align_bytes=64) for i in range(2)]
         xss = [sb.tile([P, PASSES, 512], U8, name="xs%d" % i, align_bytes=64) for i in range(2)]
-        pm5s = [sb.tile([P, 9, P], F32, name="pf%d" % i) for i in range(2)]
+        pm5s = [sb.tile([P, 9, P], F32, name="pf%d" % i) for i in range(3)]
         yt5 = sb.tile([P, P], F32, name="yt5")
         w_sb = sb.tile([P, 3 * 8, 144], BF16, name="w_sb")
         bias_bf = sb.tile([P, 512], BF16, name="bias_bf")
@@ -163,7 +163,7 @@ def tile_involution2d_pa_kernel(tc, x_words, x_scales, Wi_words, Wi_scales, bi, 
         nc.vector.memset(xss[1][:].bitcast(I32), 0)
         for i in range(1, 3):
             nc.vector.memset(xps[i][:], 0.0)
-        for i in range(2):
+        for i in range(3):
             nc.gpsimd.memset(pm5s[i][:], 0.0)
         nc.vector.memset(zt[:], 0.0)
         nc.vector.memset(lbs[0][:, 0, :], 0.0)
@@ -427,7 +427,7 @@ def tile_involution2d_pa_kernel(tc, x_words, x_scales, Wi_words, Wi_scales, bi, 
             kk = pos(u)
             w = wps[(u // 2) % 2][:, kk:kk + 2, :]
             cw = COL[(4, 7)]
-            pm = pm5s[u % 2][:, :, 0:112].rearrange("p m (k c) -> p k m c", k=2)
+            pm = pm5s[u % 3][:, :, 0:112].rearrange("p m (k c) -> p k m c", k=2)
             for h in range(2):
                 for (m0, m1, r, a) in [(0, 5, 4, 28 * h), (5, 9, 0, 28 * h + 1)]:
                     nc.vector.tensor_tensor(
@@ -440,16 +440,16 @@ def tile_involution2d_pa_kernel(tc, x_words, x_scales, Wi_words, Wi_scales, bi, 
         def gadd5(u):
             if not (0 <= u and newdiv(u)):
                 return
-            pm = pm5s[u % 2]
-            nc.gpsimd.tensor_tensor(out=pm[:, 0:4, 0:112], in0=pm[:, 0:4, 0:112], in1=pm[:, 4:8, 0:112], op=ALU.add)
+            pm = pm5s[u % 3]
+            nc.gpsimd.tensor_tensor(out=pm[:, 0:2, 0:112], in0=pm[:, 0:2, 0:112], in1=pm[:, 6:8, 0:112], op=ALU.add)
 
         def fwd5(u):
             if not (0 <= u and newdiv(u)):
                 return
-            for m in (0, 1, 2, 3, 8):
+            for m in range(6):
                 nc.tensor.matmul(
-                    out=five(u)[:, 0:P], lhsT=pm5s[u % 2][:, m, :], rhs=ident[:],
-                    is_transpose=True, start=(m == 0), stop=(m == 8))
+                    out=five(u)[:, 0:P], lhsT=pm5s[u % 3][:, m, :], rhs=ident[:],
+                    is_transpose=True, start=(m == 0), stop=(m == 5))
 
         def evact5(u):
             if not (0 <= u and newdiv(u)):
@@ -465,9 +465,11 @@ def tile_involution2d_pa_kernel(tc, x_words, x_scales, Wi_words, Wi_scales, bi, 
             if not (0 <= u and newdiv(u)):
                 return
             s0 = pos(u)
-            nc.vector.tensor_copy(
+            nc.vector.tensor_tensor(
                 out=ys[(u // 2) % 3][:, s0:s0 + 2, 233:289],
-                in_=five(u)[:, P:P + 112].rearrange("p (k c) -> p k c", k=2))
+                in0=five(u)[:, P:P + 112].rearrange("p (k c) -> p k c", k=2),
+                in1=pm5s[u % 3][:, 8, 0:112].rearrange("p (k c) -> p k c", k=2),
+                op=ALU.add)
 
         def smult(u, k, g0=0, g1=8):
             if not 0 <= u < nu:

@@ -441,15 +441,15 @@ def tile_involution2d_pa_kernel(tc, x_words, x_scales, Wi_words, Wi_scales, bi, 
             if not (0 <= u and newdiv(u)):
                 return
             pm = pm5s[u % 3]
-            nc.gpsimd.tensor_tensor(out=pm[:, 0:2, 0:112], in0=pm[:, 0:2, 0:112], in1=pm[:, 6:8, 0:112], op=ALU.add)
+            nc.gpsimd.tensor_tensor(out=pm[:, 0:4, 0:112], in0=pm[:, 0:4, 0:112], in1=pm[:, 4:8, 0:112], op=ALU.add)
 
         def fwd5(u):
             if not (0 <= u and newdiv(u)):
                 return
-            for m in range(6):
+            for m in range(4):
                 nc.tensor.matmul(
                     out=five(u)[:, 0:P], lhsT=pm5s[u % 3][:, m, :], rhs=ident[:],
-                    is_transpose=True, start=(m == 0), stop=(m == 5))
+                    is_transpose=True, start=(m == 0), stop=(m == 3))
 
         def evact5(u):
             if not (0 <= u and newdiv(u)):

@@ -20,8 +20,6 @@ PASSES = 8
 NB = 4
 XW = 530
 YW = 560
-XRW = 60
-RV = 7
 NWP = 252
 DELTA = [32 * (t // 3 - 1) + (t % 3 - 1) for t in range(9)]
 GLO = [max(57 * t - 1, 0) // 32 for t in range(9)]
@@ -38,15 +36,8 @@ VB = (5, 6, 7)
 NG = 33 * len(GB)
 NV = 33 * len(VB)
 NPL = 8
-GW = (0,)
-NTL = 1
+GT = 6
 WA = 4
-GT = 7
-GK = 2
-GBN = (0, 1, 2, 5)
-VBN = (3, 4, 6, 7)
-VW = ()
-EVT = "S"
 
 
 def tile_involution2d_pa_kernel(tc, x_words, x_scales, Wi_words, Wi_scales, bi, w_span, out):
@@ -62,8 +53,6 @@ def tile_involution2d_pa_kernel(tc, x_words, x_scales, Wi_words, Wi_scales, bi, 
         wis = sb.tile([P, PASSES, 512], U8, name="wis", align_bytes=64)
         xcs = [sb.tile([P, PASSES, 1024], U8, name="xc%d" % i, align_bytes=64) for i in range(2)]
         xss = [sb.tile([P, PASSES, 512], U8, name="xs%d" % i, align_bytes=64) for i in range(2)]
-        pm5s = [sb.tile([P, 9, P], F32, name="pf%d" % i) for i in range(3)]
-        yt5 = sb.tile([P, P], F32, name="yt5")
         w_sb = sb.tile([P, 3 * 8, 144], BF16, name="w_sb")
         bias_bf = sb.tile([P, 512], BF16, name="bias_bf")
         brow = sb.tile([P, 512], BF16, name="brow")
@@ -73,11 +62,11 @@ def tile_involution2d_pa_kernel(tc, x_words, x_scales, Wi_words, Wi_scales, bi, 
         ebf = [sb.tile([P, 384], BF16, name="ebf%d" % j) for j in range(3)]
         edge = sb.tile([P, 2], F32, name="edge")
         mask = sb.tile([P, 2], F32, name="mask")
+        bm = sb.tile([P, 256], BF16, name="bm")
         zt = sb.tile([P, 64], F32, name="zt")
         xps = [sb.tile([P, 2, XW], F32, name="xp%d" % i) for i in range(3)]
-        xrs = [sb.tile([P, 2, 9, XRW], F32, name="xr%d" % i) for i in range(3)]
-        bias_r = sb.tile([P, 9, 56], BF16, name="bias_r")
-        wss = [sb.tile([P, NB, 81], F32, name="wS%d" % i) for i in range(2)]
+        wss = [sb.tile([P, NB, P], F32, name="wS%d" % i) for i in range(2)]
+        wts = [sb.tile([P, NB * P], BF16, name="wT%d" % i) for i in range(2)]
         wsb = [sb.tile([P, NB, NWP], BF16, name="wB%d" % i) for i in range(2)]
         pvg = [sb.tile([P, 2, 9 * NG], F32, name="pg%d" % i) for i in range(2)]
         pvv = [sb.tile([P, 2, 9 * NV], F32, name="pw%d" % i) for i in range(3)]
@@ -87,11 +76,11 @@ def tile_involution2d_pa_kernel(tc, x_words, x_scales, Wi_words, Wi_scales, bi, 
         ys = [sb.tile([P, NB + 1, YW], F32, name="y%d" % i) for i in range(3)]
         lbs = [sb.tile([P, NB + 2, 72], F32, name="lb%d" % i) for i in range(2)]
         yts = sb.tile([P, 4 * P], F32, name="yts")
-        ytn = sb.tile([P, 2 * P], F32, name="ytn")
 
         xips = [ps.tile([P, 512], F32, name="xiP%d" % i) for i in range(3)]
         wps = [ps.tile([P, NB, NWP], BF16, name="wP%d" % i) for i in range(2)]
-        lsh0 = ps.tile([P, NB + 1, 72], F32, name="lsh")
+        misc = ps.tile([P, 512], F32, name="misc")
+        lsh0 = misc[:, 0:(NB + 1) * 72].rearrange("p (n c) -> p n c", c=72)
         acct = ps.tile([P, 4 * P], F32, name="acct")
         yb = ps.tile([P, 4 * P], F32, name="yb")
 
@@ -152,7 +141,6 @@ def tile_involution2d_pa_kernel(tc, x_words, x_scales, Wi_words, Wi_scales, bi, 
 
         make_identity(nc, ident[:])
         nc.vector.memset(e32[:], 0.0)
-        nc.vector.memset(xps[0][:], 0.0)
         nc.vector.tensor_copy(out=e32[:, 128:256], in_=ident[:])
         nc.vector.tensor_reduce(out=edge[:, 0:1], in_=ident[:, 0:128:32], axis=AX.X, op=ALU.add)
         nc.vector.tensor_reduce(out=edge[:, 1:2], in_=ident[:, 31:128:32], axis=AX.X, op=ALU.add)
@@ -160,16 +148,16 @@ def tile_involution2d_pa_kernel(tc, x_words, x_scales, Wi_words, Wi_scales, bi, 
         nc.vector.tensor_scalar(out=ebf[0][:], in0=e32[:], scalar1=mask[:, 0:1], scalar2=None, op0=ALU.mult)
         nc.vector.tensor_copy(out=ebf[1][:], in_=e32[:])
         nc.vector.tensor_scalar(out=ebf[2][:], in0=e32[:], scalar1=mask[:, 1:2], scalar2=None, op0=ALU.mult)
-        nc.vector.memset(xss[1][:].bitcast(I32), 0)
-        for i in range(1, 3):
-            nc.vector.memset(xps[i][:], 0.0)
+        for i in range(2):
+            nc.gpsimd.memset(wss[i][:], 0.0)
         for i in range(3):
-            nc.gpsimd.memset(pm5s[i][:], 0.0)
+            nc.vector.memset(xps[i][:, :, 0:9], 0.0)
+            nc.vector.memset(xps[i][:, :, 521:XW], 0.0)
+        nc.vector.memset(xss[1][:].bitcast(I32), 0)
         nc.vector.memset(zt[:], 0.0)
         nc.vector.memset(lbs[0][:, 0, :], 0.0)
         nc.vector.memset(lbs[(NT // NB - 1) % 2][:, NB + 1, :], 0.0)
         nc.vector.memset(ys[(NT // NB - 1) % 3][:, NB, :], 0.0)
-        nc.vector.tensor_copy(out=bias_r[:], in_=bias_bf[:, 0:504].rearrange("p (a r) -> p r a", r=9))
 
         nu = NT // 2
         nbat = NT // NB
@@ -177,17 +165,14 @@ def tile_involution2d_pa_kernel(tc, x_words, x_scales, Wi_words, Wi_scales, bi, 
         def pos(u):
             return 2 * (u % 2) if u < nu - 2 else 2 * ((u + 1) % 2)
 
-        def newdiv(u):
-            return u < nu - 3
-
-        def mx(u, k, g0, g1):
+        def mx(u, k):
             if not 0 <= u < nu:
                 return
             xc = xcs[(u // 2) % 2]
             xs = xss[(u // 2) % 2]
             kk = pos(u) + k
             acc = xips[(2 * u + k) % 3]
-            for g in range(g0, g1):
+            for g in range(PASSES):
                 nc.tensor.matmul_mx(
                     out=acc[:],
                     lhsT=(xc0[:, kk, g, :] if u < 2 else xc[:, g, 256 * kk:256 * (kk + 1)]).bitcast(FP4),
@@ -235,23 +220,27 @@ def tile_involution2d_pa_kernel(tc, x_words, x_scales, Wi_words, Wi_scales, bi, 
                         stop=True,
                     )
 
-        def bias(u, k0=0, k1=2):
+        def bias(u, k):
             if not 0 <= u < nu:
                 return
-            for k in range(k0, k1):
-                acc = xips[(2 * u + k) % 3]
-                nc.vector.tensor_tensor(out=xps[u % 3][:, k, 9:521], in0=acc[:], in1=bias_bf[:], op=ALU.add)
-                nc.vector.tensor_tensor(
-                    out=xrs[u % 3][:, k, 0:RV, 0:56], in0=acc[:, 0:504].rearrange("p (a r) -> p r a", r=9)[:, 0:RV, :],
-                    in1=bias_r[:, 0:RV, :], op=ALU.add)
+            nc.vector.tensor_tensor(
+                out=xps[u % 3][:, k, 9:521], in0=xips[(2 * u + k) % 3][:], in1=bias_bf[:], op=ALU.add)
 
-        def xrcopy(u, k0=0, k1=2):
-            if not 0 <= u < nu:
-                return
-            nc.scalar.copy(
-                out=xrs[u % 3][:, k0:k1, RV:9, 0:57],
-                in_=xps[u % 3][:, k0:k1, 9:522].rearrange("p k (a r) -> p k r a", r=9)[:, :, RV:9, :])
-            nc.scalar.copy(out=xrs[u % 3][:, k0:k1, 0:RV, 56], in_=xps[u % 3][:, k0:k1, 513:513 + RV])
+        def biasmap():
+            for gi, (g, t) in enumerate(WHOLE):
+                c0 = 288 * g - 512 * t
+                for m in range(9):
+                    d = 9 * t + m
+                    nc.tensor.matmul(
+                        out=yb[:, 32 * gi:32 * gi + 32], lhsT=ebf[1][:, 128 - d:256 - d], rhs=brow[:, c0 + m:c0 + m + 280:9],
+                        start=(m == 0), stop=(m == 8))
+
+        def wtrans(b):
+            for k in range(NB):
+                nc.tensor.transpose(out=misc[:, P * k:P * (k + 1)], in_=wss[b % 2][:, k, :], identity=ident[:])
+
+        def wtevac(b):
+            nc.scalar.copy(out=wts[b % 2][:], in_=misc[:])
 
         def wsevac(b):
             if not 0 <= b < nbat:
@@ -266,7 +255,6 @@ def tile_involution2d_pa_kernel(tc, x_words, x_scales, Wi_words, Wi_scales, bi, 
             if not 0 <= u < nu:
                 return
             xp = xps[u % 3][:, k0:k1, :]
-            new = newdiv(u) and not extra
             if eng == "V":
                 e = nc.vector
                 wp = wps[(u // 2) % 2][:, pos(u) + k0:pos(u) + k1, :]
@@ -280,13 +268,6 @@ def tile_involution2d_pa_kernel(tc, x_words, x_scales, Wi_words, Wi_scales, bi, 
             for b, (g, ta) in [(i, SPLIT[i]) for i in order]:
                 n1 = 57 * ta + 56 - 32 * g + 1
                 n2 = 33 - n1
-                shift = base
-                if new and eng == "G" and b >= 4:
-                    shift = 56
-                if new and eng == "V" and b == 3:
-                    shift = 99
-                if new and eng == "V" and b == 4:
-                    shift = 155
                 segs = []
                 if not (g == 8):
                     segs.append((ta, ta + 9 * (32 * g - 57 * ta + 1), n1, 33 * b))
@@ -294,22 +275,14 @@ def tile_involution2d_pa_kernel(tc, x_words, x_scales, Wi_words, Wi_scales, bi, 
                     segs.append((ta + 1, ta + 1, n2, 33 * b + n1))
                 for (t, a, n, o) in segs:
                     cw = COL[(t, g)]
-                    o = o - shift
+                    o = o - base
                     e.tensor_tensor(
                         out=pv[:, :, 9 * o:9 * (o + n)].rearrange("p k (s m) -> p k s m", m=9),
                         in0=xp[:, :, a:a + 9 * n].rearrange("p k (s m) -> p k s m", m=9),
                         in1=wp[:, :, cw:cw + 9].unsqueeze(2).to_broadcast([P, k1 - k0, n, 9]),
                         op=ALU.mult,
                     )
-                if g == 7 and new:
-                    cw = COL[(4, 7)]
-                    e.tensor_tensor(
-                        out=pv[:, :, 9 * (103 - shift):9 * (105 - shift)].rearrange("p k (h m) -> p k h m", m=9),
-                        in0=xp[:, :, 4:4 + 522].rearrange("p k (s m) -> p k s m", m=9)[:, :, 0:58:57, :],
-                        in1=wp[:, :, cw:cw + 18].rearrange("p k (h m) -> p k h m", m=9),
-                        op=ALU.mult,
-                    )
-                if g == 7 and not new:
+                if g == 7:
                     for k in range(k1 - k0):
                         cw = COL[(4, 7)]
                         e.tensor_tensor(
@@ -320,61 +293,6 @@ def tile_involution2d_pa_kernel(tc, x_words, x_scales, Wi_words, Wi_scales, bi, 
                             op=ALU.mult,
                         )
 
-        def pmult(eng, u, gis, k0=0, k1=2):
-            if not 0 <= u < nu:
-                return
-            kk = pos(u)
-            e = nc.vector if eng == "V" else nc.gpsimd
-            w = (wps if eng == "V" else wsb)[(u // 2) % 2][:, kk + k0:kk + k1, :]
-            for gi in gis:
-                g, t = WHOLE[gi]
-                c0 = 288 * g - 512 * t
-                r0 = c0 % 9
-                cw = COL[(t, g)]
-                for (m0, m1, r, a) in [(0, 9 - r0, r0, c0 // 9), (9 - r0, 9, 0, c0 // 9 + 1)]:
-                    if m1 > m0:
-                        e.tensor_tensor(
-                            out=pms[u % 3][:, k0:k1, m0:m1, 32 * gi:32 * gi + 32],
-                            in0=xrs[u % 3][:, k0:k1, r:r + m1 - m0, a:a + 32],
-                            in1=w[:, :, cw + m0:cw + m1].unsqueeze(3).to_broadcast([P, k1 - k0, m1 - m0, 32]),
-                            op=ALU.mult,
-                        )
-
-        def gpre(u):
-            if not 0 <= u < nu:
-                return
-            pm = pms[u % 3]
-            for m in range(NPL, 8):
-                nc.gpsimd.tensor_tensor(out=pm[:, :, 8, :], in0=pm[:, :, 8, :], in1=pm[:, :, m, :], op=ALU.add)
-
-        def tailn(u):
-            return nu - 2 - NTL <= u < nu - 2
-
-        def fwd_n(u):
-            for k in range(2):
-                for m in range(9):
-                    nc.tensor.matmul(
-                        out=xips[u % 2][:, P * k:P * (k + 1)], lhsT=pvg[u % 2][:, k, m:1152:9], rhs=ident[:],
-                        is_transpose=True, start=(m == 0), stop=(m == 8))
-                    if m % 4 == 3:
-                        keep()
-
-        def evact_n(u):
-            nc.scalar.copy(out=ytn[:], in_=xips[u % 2][:, 0:2 * P])
-
-        def back_n(u):
-            for k in range(2):
-                nc.tensor.transpose(out=xips[2][:, P * k:P * (k + 1)], in_=ytn[:, P * k:P * (k + 1)], identity=ident[:])
-
-        def evacy_n(u):
-            y = ys[(u // 2) % 3]
-            s0 = pos(u)
-            yn = xips[2][:, 0:2 * P].rearrange("p (k c) -> p k c", k=2)
-            nc.scalar.copy(
-                out=y[:, s0:s0 + 2, 33:33 + 195].rearrange("p k (q c) -> p k q c", c=65)[:, :, :, 0:33],
-                in_=yn[:, :, 0:99].rearrange("p k (q c) -> p k q c", c=33))
-            nc.scalar.copy(out=y[:, s0:s0 + 2, 228:257], in_=yn[:, :, 99:128])
-
         def vreduce(u, parts="abc"):
             if not 0 <= u < nu:
                 return
@@ -382,35 +300,16 @@ def tile_involution2d_pa_kernel(tc, x_words, x_scales, Wi_words, Wi_scales, bi, 
             s0 = pos(u)
             pg = pvg[u % 2]
             pw = pvv[u % 3]
-            if newdiv(u):
-                nc.vector.tensor_reduce(
-                    out=y[:, s0:s0 + 2, 33:33 + 195].rearrange("p k (q c) -> p k q c", c=65)[:, :, :, 0:33],
-                    in_=pg[:, :, 0:9 * 99].rearrange("p k (q s m) -> p k q s m", q=3, m=9),
-                    axis=AX.X, op=ALU.add)
-                nc.vector.tensor_reduce(
-                    out=y[:, s0:s0 + 2, 228:228 + 122].rearrange("p k (q c) -> p k q c", c=61)[:, :, :, 0:5],
-                    in_=pw[:, :, 0:9 * 10].rearrange("p k (q s m) -> p k q s m", q=2, m=9),
-                    axis=AX.X, op=ALU.add)
-                nc.vector.tensor_reduce(
-                    out=y[:, s0:s0 + 2, 326:359],
-                    in_=pg[:, :, 9 * 109:9 * 142].rearrange("p k (s m) -> p k s m", m=9),
-                    axis=AX.X, op=ALU.add)
-                nc.vector.tensor_reduce(
-                    out=y[:, s0:s0 + 2, 391:391 + 130].rearrange("p k (q c) -> p k q c", c=65)[:, :, :, 0:33],
-                    in_=pw[:, :, 9 * 33:9 * 99].rearrange("p k (q s m) -> p k q s m", q=2, m=9),
-                    axis=AX.X, op=ALU.add)
-                return
             for part in parts:
-                if part == "a" and not tailn(u):
+                if part == "a":
                     nc.vector.tensor_reduce(
                         out=y[:, s0:s0 + 2, 33:33 + 195].rearrange("p k (q c) -> p k q c", c=65)[:, :, :, 0:33],
                         in_=pg[:, :, 0:9 * 99].rearrange("p k (q s m) -> p k q s m", q=3, m=9),
                         axis=AX.X, op=ALU.add)
                 if part == "b":
-                    f = 128 if tailn(u) else 99
                     nc.vector.tensor_reduce(
-                        out=y[:, s0:s0 + 2, 228 + f - 99:294],
-                        in_=(pvx[:] if u == nu - 1 else pg[:, :, 9 * f:9 * 165]).rearrange("p k (s m) -> p k s m", m=9),
+                        out=y[:, s0:s0 + 2, 228:294],
+                        in_=(pvx[:] if u == nu - 1 else pg[:, :, 9 * 99:9 * 165]).rearrange("p k (s m) -> p k s m", m=9),
                         axis=AX.X, op=ALU.add)
                 if part == "c":
                     nc.vector.tensor_reduce(
@@ -418,74 +317,20 @@ def tile_involution2d_pa_kernel(tc, x_words, x_scales, Wi_words, Wi_scales, bi, 
                         in_=pw[:].rearrange("p k (q s m) -> p k q s m", q=3, m=9),
                         axis=AX.X, op=ALU.add)
 
-        def five(u):
-            return xips[(2 * (u + 1)) % 3]
-
-        def tmult(u):
-            if not (0 <= u and newdiv(u)):
-                return
-            kk = pos(u)
-            w = wps[(u // 2) % 2][:, kk:kk + 2, :]
-            cw = COL[(4, 7)]
-            pm = pm5s[u % 3][:, :, 0:112].rearrange("p m (k c) -> p k m c", k=2)
-            for h in range(2):
-                for (m0, m1, r, a) in [(0, 5, 4, 28 * h), (5, 9, 0, 28 * h + 1)]:
-                    nc.vector.tensor_tensor(
-                        out=pm[:, :, m0:m1, 28 * h:28 * h + 28],
-                        in0=xrs[u % 3][:, :, r:r + m1 - m0, a:a + 28],
-                        in1=w[:, :, cw + 9 * h + m0:cw + 9 * h + m1].unsqueeze(3).to_broadcast([P, 2, m1 - m0, 28]),
-                        op=ALU.mult,
-                    )
-
-        def gadd5(u):
-            if not (0 <= u and newdiv(u)):
-                return
-            pm = pm5s[u % 3]
-            nc.gpsimd.tensor_tensor(out=pm[:, 0:4, 0:112], in0=pm[:, 0:4, 0:112], in1=pm[:, 4:8, 0:112], op=ALU.add)
-
-        def fwd5(u):
-            if not (0 <= u and newdiv(u)):
-                return
-            for m in range(4):
-                nc.tensor.matmul(
-                    out=five(u)[:, 0:P], lhsT=pm5s[u % 3][:, m, :], rhs=ident[:],
-                    is_transpose=True, start=(m == 0), stop=(m == 3))
-
-        def evact5(u):
-            if not (0 <= u and newdiv(u)):
-                return
-            nc.scalar.copy(out=yt5[:], in_=five(u)[:, 0:P])
-
-        def back5(u):
-            if not (0 <= u and newdiv(u)):
-                return
-            nc.tensor.transpose(out=five(u)[:, P:2 * P], in_=yt5[:], identity=ident[:])
-
-        def evacy5(u):
-            if not (0 <= u and newdiv(u)):
-                return
-            s0 = pos(u)
-            nc.vector.tensor_tensor(
-                out=ys[(u // 2) % 3][:, s0:s0 + 2, 233:289],
-                in0=five(u)[:, P:P + 112].rearrange("p (k c) -> p k c", k=2),
-                in1=pm5s[u % 3][:, 8, 0:112].rearrange("p (k c) -> p k c", k=2),
-                op=ALU.add)
-
         def smult(u, k, g0=0, g1=8):
             if not 0 <= u < nu:
                 return
-            xr = xrs[u % 3]
+            acc = xips[(2 * u + k) % 3]
             ws = wss[(u // 2) % 2]
             pm = pms[u % 3]
             kk = pos(u) + k
-            for gi, (g, t) in enumerate(WHOLE):
-                if not g0 <= gi < g1 or (gi in GW and k < GK) or gi in VW:
-                    continue
+            for gi in range(g0, g1):
+                g, t = WHOLE[gi]
                 c0 = 288 * g - 512 * t
                 for m in range(9):
                     nc.scalar.activation(
                         out=pm[:, k, m, 32 * gi:32 * gi + 32],
-                        in_=xr[:, k, (c0 + m) % 9, (c0 + m) // 9:(c0 + m) // 9 + 32],
+                        in_=acc[:, c0 + m:c0 + m + 280:9],
                         func=ACT.Copy,
                         scale=ws[:, kk, 9 * t + m:9 * t + m + 1],
                     )
@@ -509,16 +354,19 @@ def tile_involution2d_pa_kernel(tc, x_words, x_scales, Wi_words, Wi_scales, bi, 
         def evact_s(u):
             if not 0 <= u < nu:
                 return
-            if EVT == "S":
-                nc.scalar.copy(out=yts[:], in_=acct[:])
-            else:
-                nc.vector.tensor_copy(out=yts[:], in_=acct[:])
+            nc.scalar.copy(out=yts[:], in_=acct[:])
 
         def back_s(u):
             if not 0 <= u < nu:
                 return
-            for c in range(4):
-                nc.tensor.transpose(out=yb[:, P * c:P * (c + 1)], in_=yts[:, P * c:P * (c + 1)], identity=ident[:])
+            for k in range(2):
+                nc.tensor.matmul(
+                    out=yb[:, 2 * P * k:2 * P * (k + 1)], lhsT=wts[(u // 2) % 2][:, P * (pos(u) + k):P * (pos(u) + k + 1)],
+                    rhs=bm[:], start=True, stop=False)
+                for c in (2 * k, 2 * k + 1):
+                    nc.tensor.matmul(
+                        out=yb[:, P * c:P * (c + 1)], lhsT=yts[:, P * c:P * (c + 1)], rhs=ident[:],
+                        is_transpose=True, start=False, stop=(c % 2 == 1))
 
         def evacy_s(u):
             if not 0 <= u < nu:
@@ -636,111 +484,77 @@ def tile_involution2d_pa_kernel(tc, x_words, x_scales, Wi_words, Wi_scales, bi, 
 
         wshift(0)
         wsevac(0)
-        for u in range(-2, nu - 2):
-            if u == -2:
+        for u in range(-1, nu - 1):
+            if u == -1:
                 load_chunk(1)
-            if u >= 0 and u % 2 == 0 and u // 2 + 2 < nbat:
-                load_chunk(u // 2 + 2)
+                load_w(1)
+            if u > 0 and u % 2 == 1 and (u + 3) // 2 < nbat:
+                load_chunk((u + 3) // 2)
             if u == 0:
                 zero_rows()
             if u % 4 == 2 and (u + 2) // 4 + 1 < 8:
                 load_w((u + 2) // 4 + 1)
+            odd = u % 2 == 1 and u > 0
+            even = u % 2 == 0
             back_s(u - 2)
-            back5(u - 2)
-            fwd_s(u - 1, 0, 2)
+            bias(u, 1)
             if u == 0:
-                wshift(1)
-            if u % 2 == 0 and u > 0:
+                nmult("G", 0, GB, 1, 2)
+            fwd_s(u - 1, 0, 2)
+            if even:
                 wshift((u + 2) // 2, 0, WA)
-            head = u < 2
-            if head:
-                for k in range(2):
-                    bias(u + 1, k, k + 1)
-                    nmult("V", u + 1, VBN, k, k + 1)
-                    if u == -1:
-                        xrcopy(0, k, k + 1)
-                        nmult("G", 0, GBN, k, k + 1)
-                        smult(0, k)
-            else:
-                bias(u + 1, 0, 1)
-                evacy5(u - 2)
-                bias(u + 1, 1, 2)
-            tmult(u)
-            mx(u + 2, 0, 0, 8)
-            fwd_s(u - 1, 2, 3)
-            if u % 2 == 1 and u > 0:
-                wsevac((u + 1) // 2)
+            if odd:
+                wshift((u + 1) // 2, WA, 9)
+            smult(u, 0)
+            mx(u + 1, 0)
             evacy_s(u - 2)
-            fwd5(u - 1)
-            fwd_s(u - 1, 3, 4)
-            if u % 2 == 0:
-                fin_a((u - 4) // 2)
-                fin_b((u - 4) // 2)
-            else:
-                fin_c((u - 5) // 2)
-            if u % 2 == 1 and u > 0:
-                wshift((u + 3) // 2, WA, 9)
-            mx(u + 2, 1, 0, 8)
-            gpre(u - 1)
-            gl = GBN if newdiv(u) else GB
+            fwd_s(u - 1, 2, 4)
+            if odd:
+                fin_a((u - 3) // 2)
+                fin_b((u - 3) // 2)
+            if even:
+                fin_c((u - 4) // 2)
+                wtrans(u // 2)
+            if u == 0:
+                biasmap()
+            mx(u + 1, 1)
             if u > 0:
-                nmult("G", u, gl[0:2])
-            pmult("G", u, GW, 0, GK)
-            if u > 0:
-                nmult("G", u, gl[2:])
-            gadd5(u)
-            if not head:
-                nmult("V", u + 1, VBN if newdiv(u + 1) else VB)
-            vreduce(u - 1)
-            if u > 0:
-                smult(u, 0)
-                smult(u, 1, 0, 4)
+                nmult("G", u, GB)
+            nmult("V", u, VB)
+            vreduce(u - 1, "ca")
+            bias(u + 1, 0)
+            if u == -1:
+                nmult("G", 0, GB, 0, 1)
+            vreduce(u - 1, "b")
+            smult(u, 1, 0, 5)
             evact_s(u - 1)
-            evact5(u - 1)
-            if u > 0:
-                smult(u, 1, 4, 8)
-            if u >= 0:
-                xrcopy(u + 1)
+            if odd:
+                wsevac((u + 1) // 2)
+            if even:
+                wtevac(u // 2)
+            if u == 0:
+                nc.scalar.copy(out=bm[:], in_=yb[:, 0:256])
+            smult(u, 1, 5, 8)
         a, b, c = nu - 3, nu - 2, nu - 1
-        lsh1 = xips[0][:, 0:(NB + 1) * 72].rearrange("p (n c) -> p n c", c=72)
-        lsh2 = xips[2][:, 0:(NB + 1) * 72].rearrange("p (n c) -> p n c", c=72)
-        back_s(a - 1)
-        back5(a - 1)
-        fwd_s(a)
-        bias(c)
-        evacy5(a - 1)
-        evacy_s(a - 1)
-        fin_a(nbat - 3)
-        fin_b(nbat - 3)
-        pmult("G", b, GW, 0, GK)
-        nmult("G", b, GB)
-        fwd_n(a)
+        lsh1 = xips[(2 * c + 1) % 3][:, 0:(NB + 1) * 72].rearrange("p (n c) -> p n c", c=72)
+        lsh2 = xips[(2 * c) % 3][:, 0:(NB + 1) * 72].rearrange("p (n c) -> p n c", c=72)
+        back_s(a)
+        bias(c, 1)
+        fwd_s(b)
+        evacy_s(a)
+        nmult("G", c, (0, 1, 2))
+        smult(c, 0)
+        fin_a(nbat - 2)
+        fin_b(nbat - 2)
         nmult("V", c, VB)
         nmult("V", c, (3, 4), extra=True)
         early4_m(c)
-        vreduce(a)
-        smult(b, 0)
-        xrcopy(c)
-        smult(b, 1)
-        evact_s(a)
-        evact_n(a)
-
-        back_s(a)
-        back_n(a)
-        evacy_s(a)
-        fin_c(nbat - 3)
-        pmult("G", c, GW, 0, 2)
-        nmult("G", c, (0, 1, 2))
-        fwd_s(b)
-        vreduce(b)
-        smult(c, 0, 1)
+        vreduce(b, "cab")
+        smult(c, 1, 0, 2)
         evact_s(b)
-        evacy_n(a)
-        fin_a(nbat - 2)
-        fin_b(nbat - 2)
+        smult(c, 1, 2, 4)
         back_s(b)
         fwd_s(c, 0, 2)
-        smult(c, 1, 1, 4)
         vreduce(c, "c")
         evacy_s(b)
         fin_a(nbat - 1, 2, NB, eng="V")

@@ -412,6 +412,9 @@ def tile_involution2d_pa_kernel(tc, x_words, x_scales, Wi_words, Wi_scales, bi, 
             y = ys[b % 3]
             lsh = lsh0 if bank is None else bank
             last = b == nbat - 1 and j1 > NB
+            if fix:
+                nc.vector.tensor_tensor(
+                    out=y[:, j0:j1, 58:465:58], in0=lsh[:, j0:j1, 7:64:8], in1=y[:, j0:j1, 58:465:58], op=ALU.add)
             for t in range(2, 9 if fix else 2):
                 if eng == "S":
                     nc.scalar.copy(
@@ -423,9 +426,6 @@ def tile_involution2d_pa_kernel(tc, x_words, x_scales, Wi_words, Wi_scales, bi, 
                         out=y[:, j0:j1, 57 * t + 1:58 * t],
                         in_=lsh[:, j0:j1, 8 * (t - 1) + 8 - t:8 * (t - 1) + 7],
                     )
-            if fix:
-                nc.vector.tensor_tensor(
-                    out=y[:, j0:j1, 58:465:58], in0=lsh[:, j0:j1, 7:64:8], in1=y[:, j0:j1, 58:465:58], op=ALU.add)
             if s0 is None:
                 s0 = j0
             for t in (taps if s0 >= 0 else ()):

@@ -31,10 +31,16 @@ WHOLE = [(0, 0), (2, 1), (4, 2), (6, 3), (9, 5), (11, 6), (13, 7), (15, 8)]
 SPLIT = [(1, 0), (3, 1), (5, 2), (7, 3), (8, 4), (10, 5), (12, 6), (14, 7)]
 START = [57 * t + 1 for t in range(9)]
 WID = [56] * 8 + [64]
-GB = (0, 1, 2, 3, 4)
-VB = (5, 6, 7)
-NG = 33 * len(GB)
-NV = 33 * len(VB)
+SEGS = [s for (g, ta) in SPLIT for s in (
+    (ta, ta + 9 * (32 * g - 57 * ta + 1), 57 * ta + 57 - 32 * g, g, 32 * g + ta + 1),
+    (ta + 1, ta + 1, 32 * g - 57 * ta - 24, g, 58 * (ta + 1)))]
+VB = (6, 9, 11, 12, 13, 14, 15)
+GB = tuple(i for i in range(16) if i not in VB)
+VBL = VB
+GBL = GB
+VPL = ((0, 1),)
+NG = sum(SEGS[i][2] for i in GB)
+NV = sum(SEGS[i][2] for i in VBL)
 NPL = 8
 GT = 6
 WA = 4
@@ -69,9 +75,8 @@ def tile_involution2d_pa_kernel(tc, x_words, x_scales, Wi_words, Wi_scales, bi, 
         wts = [sb.tile([P, NB * P], BF16, name="wT%d" % i) for i in range(2)]
         wsb = [sb.tile([P, NB, NWP], BF16, name="wB%d" % i) for i in range(2)]
         pvg = [sb.tile([P, 2, 9 * NG], F32, name="pg%d" % i) for i in range(2)]
-        pvv = [sb.tile([P, 2, 9 * NV], F32, name="pw%d" % i) for i in range(3)]
+        pvv = [sb.tile([P, 2, 9 * NV], F32, name="pw%d" % i) for i in range(2)]
         px4 = sb.tile([P, 2, 36], F32, name="px4")
-        pvx = sb.tile([P, 2, 9 * 66], F32, name="px")
         pms = [sb.tile([P, 2, 9, 256], F32, name="pm%d" % i) for i in range(3)]
         ys = [sb.tile([P, NB + 1, YW], F32, name="y%d" % i) for i in range(3)]
         lbs = [sb.tile([P, NB + 2, 72], F32, name="lb%d" % i) for i in range(2)]
@@ -251,71 +256,79 @@ def tile_involution2d_pa_kernel(tc, x_words, x_scales, Wi_words, Wi_scales, bi, 
                 out=wss[b % 2][:, :, 9:81].rearrange("p k (t c) -> p k t c", c=9), in_=wp4[:, :, 1:9, 9:18])
             nc.scalar.copy(out=wsb[b % 2][:, :, 0:WTP * GT], in_=wps[b % 2][:, :, 0:WTP * GT])
 
-        def nmult(eng, u, order, k0=0, k1=2, extra=False):
+        def pieces(eng, u):
+            if u == nu - 1:
+                return VBL if eng == "V" else GBL
+            return VB if eng == "V" else GB
+
+        def nmult(eng, u, k0=0, k1=2, some=None):
             if not 0 <= u < nu:
                 return
             xp = xps[u % 3][:, k0:k1, :]
-            if eng == "V":
-                e = nc.vector
-                wp = wps[(u // 2) % 2][:, pos(u) + k0:pos(u) + k1, :]
-                pv = (pvx if extra else pvv[u % 3])[:, k0:k1, :]
-                base = 99 if extra else NG
-            else:
-                e = nc.gpsimd
-                wp = wsb[(u // 2) % 2][:, pos(u) + k0:pos(u) + k1, :]
-                pv = pvg[u % 2][:, k0:k1, :]
-                base = 0
-            for b, (g, ta) in [(i, SPLIT[i]) for i in order]:
-                n1 = 57 * ta + 56 - 32 * g + 1
-                n2 = 33 - n1
-                segs = []
-                if not (g == 8):
-                    segs.append((ta, ta + 9 * (32 * g - 57 * ta + 1), n1, 33 * b))
-                if not (g == 7):
-                    segs.append((ta + 1, ta + 1, n2, 33 * b + n1))
-                for (t, a, n, o) in segs:
+            e = nc.vector if eng == "V" else nc.gpsimd
+            wp = (wps if eng == "V" else wsb)[(u // 2) % 2][:, pos(u) + k0:pos(u) + k1, :]
+            pv = (pvv if eng == "V" else pvg)[u % 2][:, k0:k1, :]
+            o = 0
+            for i in pieces(eng, u):
+                t, a, n, g, yc = SEGS[i]
+                if some is None or i in some:
                     cw = COL[(t, g)]
-                    o = o - base
                     e.tensor_tensor(
                         out=pv[:, :, 9 * o:9 * (o + n)].rearrange("p k (s m) -> p k s m", m=9),
                         in0=xp[:, :, a:a + 9 * n].rearrange("p k (s m) -> p k s m", m=9),
                         in1=wp[:, :, cw:cw + 9].unsqueeze(2).to_broadcast([P, k1 - k0, n, 9]),
                         op=ALU.mult,
                     )
-                if g == 7:
-                    for k in range(k1 - k0):
-                        cw = COL[(4, 7)]
-                        e.tensor_tensor(
-                            out=pv[:, k, 9 * (103 - base):9 * (161 - base)].rearrange("p (h s m) -> p h s m", h=2, m=9),
-                            in0=xp[:, k, 4:4 + 522].rearrange("p (h s m) -> p h s m", h=2, m=9),
-                            in1=wp[:, k, cw:cw + 18].rearrange("p (h m) -> p h m", m=9).unsqueeze(2).to_broadcast(
-                                [P, 2, 29, 9]),
-                            op=ALU.mult,
-                        )
+                o += n
 
-        def vreduce(u, parts="abc"):
+        def runs(eng, u):
+            out_runs = []
+            o = 0
+            for i in pieces(eng, u):
+                n, yc = SEGS[i][2], SEGS[i][4]
+                if out_runs and out_runs[-1][2] + out_runs[-1][0] == yc:
+                    out_runs[-1][0] += n
+                else:
+                    out_runs.append([n, o, yc, 1])
+                o += n
+            merged = []
+            for r in out_runs:
+                if merged and merged[-1][0] == r[0] and merged[-1][2] + 65 * merged[-1][3] == r[2]:
+                    merged[-1][3] += 1
+                else:
+                    merged.append(r)
+            return merged
+
+        def vreduce(u, eng, lo=0, hi=99):
             if not 0 <= u < nu:
                 return
             y = ys[(u // 2) % 3]
             s0 = pos(u)
-            pg = pvg[u % 2]
-            pw = pvv[u % 3]
-            for part in parts:
-                if part == "a":
+            pv = (pvv if eng == "V" else pvg)[u % 2]
+            for n, o, yc, q in runs(eng, u)[lo:hi]:
+                if q == 1:
                     nc.vector.tensor_reduce(
-                        out=y[:, s0:s0 + 2, 33:33 + 195].rearrange("p k (q c) -> p k q c", c=65)[:, :, :, 0:33],
-                        in_=pg[:, :, 0:9 * 99].rearrange("p k (q s m) -> p k q s m", q=3, m=9),
+                        out=y[:, s0:s0 + 2, yc:yc + n],
+                        in_=pv[:, :, 9 * o:9 * (o + n)].rearrange("p k (s m) -> p k s m", m=9),
                         axis=AX.X, op=ALU.add)
-                if part == "b":
+                else:
                     nc.vector.tensor_reduce(
-                        out=y[:, s0:s0 + 2, 228:294],
-                        in_=(pvx[:] if u == nu - 1 else pg[:, :, 9 * 99:9 * 165]).rearrange("p k (s m) -> p k s m", m=9),
+                        out=y[:, s0:s0 + 2, yc:yc + 65 * q].rearrange("p k (q c) -> p k q c", c=65)[:, :, :, 0:n],
+                        in_=pv[:, :, 9 * o:9 * (o + n * q)].rearrange("p k (q s m) -> p k q s m", q=q, m=9),
                         axis=AX.X, op=ALU.add)
-                if part == "c":
-                    nc.vector.tensor_reduce(
-                        out=y[:, s0:s0 + 2, 326:326 + 195].rearrange("p k (q c) -> p k q c", c=65)[:, :, :, 0:33],
-                        in_=pw[:].rearrange("p k (q s m) -> p k q s m", q=3, m=9),
-                        axis=AX.X, op=ALU.add)
+
+        def vplane(u, k):
+            if not 0 <= u < nu:
+                return
+            for gi, kk in VPL:
+                if kk == k:
+                    g, t = WHOLE[gi]
+                    c0 = 288 * g - 512 * t
+                    nc.vector.tensor_tensor(
+                        out=pms[u % 3][:, k, :, 32 * gi:32 * gi + 32],
+                        in0=xips[(2 * u + k) % 3][:, c0:c0 + 288].rearrange("p (j m) -> p m j", m=9),
+                        in1=wss[(u // 2) % 2][:, pos(u) + k, 9 * t:9 * t + 9].unsqueeze(2).to_broadcast([P, 9, 32]),
+                        op=ALU.mult)
 
         def smult(u, k, g0=0, g1=8):
             if not 0 <= u < nu:
@@ -326,6 +339,8 @@ def tile_involution2d_pa_kernel(tc, x_words, x_scales, Wi_words, Wi_scales, bi, 
             kk = pos(u) + k
             for gi in range(g0, g1):
                 g, t = WHOLE[gi]
+                if (gi, k) in VPL:
+                    continue
                 c0 = 288 * g - 512 * t
                 for m in range(9):
                     nc.scalar.activation(
@@ -499,14 +514,19 @@ def tile_involution2d_pa_kernel(tc, x_words, x_scales, Wi_words, Wi_scales, bi, 
             back_s(u - 2)
             bias(u, 1)
             if u == 0:
-                nmult("G", 0, GB, 1, 2)
+                nmult("G", 0, 1, 2)
             fwd_s(u - 1, 0, 2)
             if even:
                 wshift((u + 2) // 2, 0, WA)
             if odd:
                 wshift((u + 1) // 2, WA, 9)
             smult(u, 0)
+            vplane(u, 1)
             mx(u + 1, 0)
+            if u == -1:
+                biasmap()
+            if u == 0:
+                nc.scalar.copy(out=bm[:], in_=yb[:, 0:256])
             evacy_s(u - 2)
             fwd_s(u - 1, 2, 4)
             if odd:
@@ -515,62 +535,60 @@ def tile_involution2d_pa_kernel(tc, x_words, x_scales, Wi_words, Wi_scales, bi, 
             if even:
                 fin_c((u - 4) // 2)
                 wtrans(u // 2)
-            if u == 0:
-                biasmap()
             mx(u + 1, 1)
             if u > 0:
-                nmult("G", u, GB)
-            nmult("V", u, VB)
-            vreduce(u - 1, "ca")
+                nmult("G", u)
+            nmult("V", u)
+            vreduce(u - 1, "V")
+            vreduce(u - 1, "G", 0, 2)
             bias(u + 1, 0)
+            vplane(u + 1, 0)
             if u == -1:
-                nmult("G", 0, GB, 0, 1)
-            vreduce(u - 1, "b")
+                nmult("G", 0, 0, 1)
+            vreduce(u - 1, "G", 2)
             smult(u, 1, 0, 5)
             evact_s(u - 1)
             if odd:
                 wsevac((u + 1) // 2)
             if even:
                 wtevac(u // 2)
-            if u == 0:
-                nc.scalar.copy(out=bm[:], in_=yb[:, 0:256])
             smult(u, 1, 5, 8)
         a, b, c = nu - 3, nu - 2, nu - 1
         lsh1 = xips[(2 * c + 1) % 3][:, 0:(NB + 1) * 72].rearrange("p (n c) -> p n c", c=72)
         lsh2 = xips[(2 * c) % 3][:, 0:(NB + 1) * 72].rearrange("p (n c) -> p n c", c=72)
         back_s(a)
         bias(c, 1)
+        vplane(c, 1)
         fwd_s(b)
         evacy_s(a)
-        nmult("G", c, (0, 1, 2))
-        smult(c, 0)
+        nmult("G", c)
+        smult(c, 0, 0, 4)
         fin_a(nbat - 2)
         fin_b(nbat - 2)
-        nmult("V", c, VB)
-        nmult("V", c, (3, 4), extra=True)
+        smult(c, 0, 4, 8)
+        nmult("V", c)
         early4_m(c)
-        vreduce(b, "cab")
-        smult(c, 1, 0, 2)
+        vreduce(b, "V")
+        fin_c(nbat - 2)
+        smult(c, 1, 0, 3)
         evact_s(b)
-        smult(c, 1, 2, 4)
+        vreduce(b, "G")
+        smult(c, 1, 3, 4)
         back_s(b)
         fwd_s(c, 0, 2)
-        vreduce(c, "c")
         evacy_s(b)
         fin_a(nbat - 1, 2, NB, eng="V")
-        fin_c(nbat - 2)
+        vreduce(c, "V")
         smult(c, 1, 4, 8)
         fin_b(nbat - 1, 3, NB + 1, bank=lsh2)
         fwd_s(c, 2, 4)
-        vreduce(c, "b")
-        early4_r(c)
         fin_c(nbat - 1, 3, NB + 1, 3, eng="V", bank=lsh2)
-        vreduce(c, "a")
+        vreduce(c, "G")
+        early4_r(c)
         fin_a(nbat - 1, 0, 2, eng="V")
         evact_s(c)
         fin_b(nbat - 1, 0, 3, bank=lsh1)
         back_s(c)
         fin_c(nbat - 1, 0, 3, -1, eng="V", bank=lsh1)
-        fin_c(nbat - 1, 0, 3, 0, fix=False, taps=(4,))
         evacy_s(c)
-        fin_c(nbat - 1, 0, 3, 0, fix=False, taps=(0, 1, 2, 3, 5, 6, 7, 8))
+        fin_c(nbat - 1, 0, 3, 0, fix=False)

@@ -513,6 +513,8 @@ def tile_involution2d_pa_kernel(tc, x_words, x_scales, Wi_words, Wi_scales, bi, 
             even = u % 2 == 0
             back_s(u - 2)
             bias(u, 1)
+            vplane(u, 1)
+            evacy_s(u - 2)
             if u == 0:
                 nmult("G", 0, 1, 2)
             fwd_s(u - 1, 0, 2)
@@ -520,21 +522,20 @@ def tile_involution2d_pa_kernel(tc, x_words, x_scales, Wi_words, Wi_scales, bi, 
                 wshift((u + 2) // 2, 0, WA)
             if odd:
                 wshift((u + 1) // 2, WA, 9)
-            smult(u, 0)
-            vplane(u, 1)
-            mx(u + 1, 0)
-            if u == -1:
-                biasmap()
-            if u == 0:
-                nc.scalar.copy(out=bm[:], in_=yb[:, 0:256])
-            evacy_s(u - 2)
             fwd_s(u - 1, 2, 4)
+            smult(u, 0, 0, 4)
             if odd:
                 fin_a((u - 3) // 2)
                 fin_b((u - 3) // 2)
             if even:
                 fin_c((u - 4) // 2)
                 wtrans(u // 2)
+            smult(u, 0, 4, 8)
+            mx(u + 1, 0)
+            if u == -1:
+                biasmap()
+            if u == 0:
+                nc.scalar.copy(out=bm[:], in_=yb[:, 0:256])
             mx(u + 1, 1)
             if u > 0:
                 nmult("G", u)

@@ -34,15 +34,14 @@ WID = [56] * 8 + [64]
 SEGS = [s for (g, ta) in SPLIT for s in (
     (ta, ta + 9 * (32 * g - 57 * ta + 1), 57 * ta + 57 - 32 * g, g, 32 * g + ta + 1),
     (ta + 1, ta + 1, 32 * g - 57 * ta - 24, g, 58 * (ta + 1)))]
-VB = (6, 9, 11, 12, 13, 14, 15)
+VB = (10, 12, 13, 14, 15)
 GB = tuple(i for i in range(16) if i not in VB)
-VBL = VB
-GBL = GB
-VPL = ((0, 1),)
+VPL = ((0, 1), (1, 1))
+VN = (1, 1)
 NG = sum(SEGS[i][2] for i in GB)
-NV = sum(SEGS[i][2] for i in VBL)
+NV = sum(SEGS[i][2] for i in VB)
 NPL = 8
-GT = 6
+GT = 7
 WA = 4
 
 
@@ -59,7 +58,7 @@ def tile_involution2d_pa_kernel(tc, x_words, x_scales, Wi_words, Wi_scales, bi, 
         wis = sb.tile([P, PASSES, 512], U8, name="wis", align_bytes=64)
         xcs = [sb.tile([P, PASSES, 1024], U8, name="xc%d" % i, align_bytes=64) for i in range(2)]
         xss = [sb.tile([P, PASSES, 512], U8, name="xs%d" % i, align_bytes=64) for i in range(2)]
-        w_sb = sb.tile([P, 3 * 8, 144], BF16, name="w_sb")
+        wrs = [[sb.tile([P, 8, 144], BF16, name="wr%d%d" % (i, r)) for r in range(3)] for i in range(2)]
         bias_bf = sb.tile([P, 512], BF16, name="bias_bf")
         brow = sb.tile([P, 512], BF16, name="brow")
         ones = sb.tile([P, P], BF16, name="ones")
@@ -105,11 +104,18 @@ def tile_involution2d_pa_kernel(tc, x_words, x_scales, Wi_words, Wi_scales, bi, 
             )
             load_scales(xs, x_scales, 512 * c, 512 * (c + 1))
 
-        def load_w(q):
-            nc.sync.dma_start(
-                out=w_sb[:, 8 * (q % 3):8 * (q % 3) + 8, :],
-                in_=w_flat[1024 * q:1024 * (q + 1), :].rearrange("(n p) c -> p n c", p=P),
-            )
+        def load_w(q, rows=(1, 0, 2)):
+            src = w_flat[1024 * q:1024 * (q + 1), :].rearrange("(n p) c -> p n c", p=P)
+            for r in rows:
+                dst = wrs[q % 2][r]
+                if r == 0:
+                    nc.sync.dma_start(out=dst[0:96, :, :], in_=src[32:P, :, :])
+                    nc.sync.dma_start(out=dst[96:P, 0:7, :], in_=src[0:32, 1:8, :])
+                if r == 1:
+                    nc.sync.dma_start(out=dst[:], in_=src)
+                if r == 2:
+                    nc.sync.dma_start(out=dst[32:P, :, :], in_=src[0:96, :, :])
+                    nc.sync.dma_start(out=dst[0:32, 1:8, :], in_=src[96:P, 0:7, :])
 
         ctx.enter_context(tc.manual_schedule())
 
@@ -118,7 +124,7 @@ def tile_involution2d_pa_kernel(tc, x_words, x_scales, Wi_words, Wi_scales, bi, 
         nc.vector.memset(xss[0][:].bitcast(I32), 0)
         nc.vector.memset(ones[:], 1.0)
         nc.scalar.dma_start(
-            out=w_sb[:, 0:8, :], in_=w_flat[0:1024, :].rearrange("(n p) c -> p n c", p=P))
+            out=wrs[0][1][:], in_=w_flat[0:1024, :].rearrange("(n p) c -> p n c", p=P))
         nc.gpsimd.dma_start(out=brow[0:1, :], in_=bi.rearrange("(o n) -> o n", o=1))
         for i in range(3):
             nc.tensor.matmul(out=acct[:], lhsT=ones[:], rhs=brow[:], start=True, stop=True)
@@ -159,6 +165,9 @@ def tile_involution2d_pa_kernel(tc, x_words, x_scales, Wi_words, Wi_scales, bi, 
             nc.vector.memset(xps[i][:, :, 0:9], 0.0)
             nc.vector.memset(xps[i][:, :, 521:XW], 0.0)
         nc.vector.memset(xss[1][:].bitcast(I32), 0)
+        for i in range(2):
+            nc.vector.memset(wrs[i][0][96:P, 7, :], 0.0)
+            nc.vector.memset(wrs[i][2][0:32, 0, :], 0.0)
         nc.vector.memset(zt[:], 0.0)
         nc.vector.memset(lbs[0][:, 0, :], 0.0)
         nc.vector.memset(lbs[(NT // NB - 1) % 2][:, NB + 1, :], 0.0)
@@ -192,35 +201,28 @@ def tile_involution2d_pa_kernel(tc, x_words, x_scales, Wi_words, Wi_scales, bi, 
             if not 0 <= b < nbat:
                 return
             wp = wps[b % 2]
-            t0 = NB * b
-            w0t = 8 * ((t0 // 8) % 3) + t0 % 8
+            n0 = NB * b % 8
+            wr = wrs[(b // 2) % 2]
             for t in range(ta, tb):
-                d = DELTA[t]
                 e = ebf[t % 3]
                 c0 = COL[(t, GLO[t])]
                 ncol = WTP if t < GT else 9 * (GHI[t] - GLO[t] + 1)
                 w0 = 9 * GLO[t]
-                if t // 3 == 0:
-                    ks = [k for k in range(NB) if (t0 + k) % 8 != 7]
-                    off, step = -d, 1
-                elif t // 3 == 2:
-                    ks = [k for k in range(NB) if (t0 + k) % 8 != 0]
-                    off, step = 256 - d, -1
-                else:
-                    ks = []
-                    off, step = 0, 0
+                d = DELTA[t] if b == 0 else t % 3 - 1
+                over = b == 0 and t // 3 != 1
                 nc.tensor.matmul(
                     out=wp[:, :, c0:c0 + ncol],
                     lhsT=e[:, 128 - d:256 - d],
-                    rhs=w_sb[:, w0t:w0t + NB, w0:w0 + ncol],
+                    rhs=wr[1 if b == 0 else t // 3][:, n0:n0 + NB, w0:w0 + ncol],
                     start=True,
-                    stop=(len(ks) == 0),
+                    stop=not over,
                 )
-                if ks:
+                if over:
+                    k0, step, off = (0, 1, -d) if t // 3 == 0 else (1, -1, 256 - d)
                     nc.tensor.matmul(
-                        out=wp[:, ks[0]:ks[-1] + 1, c0:c0 + ncol],
+                        out=wp[:, k0:NB, c0:c0 + ncol],
                         lhsT=e[:, off:off + 128],
-                        rhs=w_sb[:, w0t + ks[0] + step:w0t + ks[-1] + 1 + step, w0:w0 + ncol],
+                        rhs=wr[1][:, k0 + step:NB + step, w0:w0 + ncol],
                         start=False,
                         stop=True,
                     )
@@ -258,7 +260,7 @@ def tile_involution2d_pa_kernel(tc, x_words, x_scales, Wi_words, Wi_scales, bi, 
 
         def pieces(eng, u):
             if u == nu - 1:
-                return VBL if eng == "V" else GBL
+                return VB if eng == "V" else GB
             return VB if eng == "V" else GB
 
         def nmult(eng, u, k0=0, k1=2, some=None):
@@ -320,7 +322,7 @@ def tile_involution2d_pa_kernel(tc, x_words, x_scales, Wi_words, Wi_scales, bi, 
         def vplane(u, k):
             if not 0 <= u < nu:
                 return
-            for gi, kk in VPL:
+            for gi, kk in VPL[:VN[u % 2]]:
                 if kk == k:
                     g, t = WHOLE[gi]
                     c0 = 288 * g - 512 * t
@@ -339,7 +341,7 @@ def tile_involution2d_pa_kernel(tc, x_words, x_scales, Wi_words, Wi_scales, bi, 
             kk = pos(u) + k
             for gi in range(g0, g1):
                 g, t = WHOLE[gi]
-                if (gi, k) in VPL:
+                if (gi, k) in VPL[:VN[u % 2]]:
                     continue
                 c0 = 288 * g - 512 * t
                 for m in range(9):
@@ -416,7 +418,7 @@ def tile_involution2d_pa_kernel(tc, x_words, x_scales, Wi_words, Wi_scales, bi, 
             prv = lbs[b % 2][:, j0:j1, :].rearrange("p n (a b) -> p n a b", b=24)
             l4 = lsh[:, j0:j1, :].rearrange("p n (a b) -> p n a b", b=24)
             nc.tensor.matmul(out=l4[:, :, :, 0:16], lhsT=e32[:, 127:255], rhs=cur[:, :, :, 0:16], start=True, stop=False)
-            nc.tensor.matmul(out=l4[:, :, :, 0:16], lhsT=e32[:, 255:383], rhs=prv[:, :, :, 0:16], start=False, stop=True)
+            nc.tensor.matmul(out=l4[:, :, :, 8:16], lhsT=e32[:, 255:383], rhs=prv[:, :, :, 8:16], start=False, stop=True)
             nc.tensor.matmul(out=l4[:, :, 0:2, 16:24], lhsT=e32[:, 98:226], rhs=cur[:, :, 0:2, 16:24], start=True, stop=False)
             nc.tensor.matmul(out=l4[:, :, 0:2, 16:24], lhsT=e32[:, 226:354], rhs=prv[:, :, 0:2, 16:24], start=False, stop=True)
 
@@ -502,6 +504,9 @@ def tile_involution2d_pa_kernel(tc, x_words, x_scales, Wi_words, Wi_scales, bi, 
         for u in range(-1, nu - 1):
             if u == -1:
                 load_chunk(1)
+            if u == 0:
+                load_w(0, (0, 2))
+            if u == 1:
                 load_w(1)
             if u > 0 and u % 2 == 1 and (u + 3) // 2 < nbat:
                 load_chunk((u + 3) // 2)
@@ -518,10 +523,15 @@ def tile_involution2d_pa_kernel(tc, x_words, x_scales, Wi_words, Wi_scales, bi, 
             if u == 0:
                 nmult("G", 0, 1, 2)
             fwd_s(u - 1, 0, 2)
-            if even:
+            if even and u > 0:
                 wshift((u + 2) // 2, 0, WA)
             if odd:
-                wshift((u + 1) // 2, WA, 9)
+                wshift((u + 1) // 2, WA if u > 1 else 0, 9)
+            mx(u + 1, 0)
+            if u == -1:
+                biasmap()
+            if u == 0:
+                nc.scalar.copy(out=bm[:], in_=yb[:, 0:256])
             fwd_s(u - 1, 2, 4)
             smult(u, 0, 0, 4)
             if odd:
@@ -531,11 +541,6 @@ def tile_involution2d_pa_kernel(tc, x_words, x_scales, Wi_words, Wi_scales, bi, 
                 fin_c((u - 4) // 2)
                 wtrans(u // 2)
             smult(u, 0, 4, 8)
-            mx(u + 1, 0)
-            if u == -1:
-                biasmap()
-            if u == 0:
-                nc.scalar.copy(out=bm[:], in_=yb[:, 0:256])
             mx(u + 1, 1)
             if u > 0:
                 nmult("G", u)
@@ -547,8 +552,9 @@ def tile_involution2d_pa_kernel(tc, x_words, x_scales, Wi_words, Wi_scales, bi, 
             if u == -1:
                 nmult("G", 0, 0, 1)
             vreduce(u - 1, "G", 2)
-            smult(u, 1, 0, 5)
+            smult(u, 1, 0, 4)
             evact_s(u - 1)
+            smult(u, 1, 4, 5)
             if odd:
                 wsevac((u + 1) // 2)
             if even:

from contextlib import ExitStack

import concourse.mybir as mybir
from concourse.masks import make_identity

FLOPS = 2 * 8192 * 4096 * 512

F32 = mybir.dt.float32
BF16 = mybir.dt.bfloat16
U8 = mybir.dt.uint8
I32 = mybir.dt.int32
FP4 = mybir.dt.float4_e2m1fn_x4
ALU = mybir.AluOpType
ACT = mybir.ActivationFunctionType
AX = mybir.AxisListType

P = 128
NT = 64
PASSES = 8
NB = 4
XW = 530
YW = 560
NWP = 252
DELTA = [32 * (t // 3 - 1) + (t % 3 - 1) for t in range(9)]
GLO = [max(57 * t - 1, 0) // 32 for t in range(9)]
GHI = [min(57 * t + 56, 511) // 32 for t in range(9)]
PAIRS = [(t, g) for t in range(9) for g in range(GLO[t], GHI[t] + 1)]
WTP = 28
COL = dict(((t, g), WTP * t + 9 * (g - GLO[t])) for (t, g) in PAIRS)
WHOLE = [(0, 0), (2, 1), (4, 2), (6, 3), (9, 5), (11, 6), (13, 7), (15, 8)]
SPLIT = [(1, 0), (3, 1), (5, 2), (7, 3), (8, 4), (10, 5), (12, 6), (14, 7)]
START = [57 * t + 1 for t in range(9)]
WID = [56] * 8 + [64]
SEGS = [s for (g, ta) in SPLIT for s in (
    (ta, ta + 9 * (32 * g - 57 * ta + 1), 57 * ta + 57 - 32 * g, g, 32 * g + ta + 1),
    (ta + 1, ta + 1, 32 * g - 57 * ta - 24, g, 58 * (ta + 1)))]
VB = (10, 12, 13, 14, 15)
GB = tuple(i for i in range(16) if i not in VB)
VPL = ((0, 1), (1, 1))
VN = (1, 1)
NG = sum(SEGS[i][2] for i in GB)
NV = sum(SEGS[i][2] for i in VB)
NPL = 8
GT = 7
WA = 4


def tile_involution2d_pa_kernel(tc, x_words, x_scales, Wi_words, Wi_scales, bi, w_span, out):
    nc = tc.nc
    out_flat = out.flatten_outer_dims()
    w_flat = w_span.flatten_outer_dims()

    with ExitStack() as ctx:
        sb = ctx.enter_context(tc.tile_pool(name="sb", bufs=1))
        ps = ctx.enter_context(tc.psum_pool(name="ps", bufs=1))

        wic = sb.tile([P, PASSES, 1024], U8, name="wic", align_bytes=64)
        wis = sb.tile([P, PASSES, 512], U8, name="wis", align_bytes=64)
        xcs = [sb.tile([P, PASSES, 1024], U8, name="xc%d" % i, align_bytes=64) for i in range(2)]
        xss = [sb.tile([P, PASSES, 512], U8, name="xs%d" % i, align_bytes=64) for i in range(2)]
        wrs = [[sb.tile([P, 8, 144], BF16, name="wr%d%d" % (i, r)) for r in range(3)] for i in range(2)]
        bias_bf = sb.tile([P, 512], BF16, name="bias_bf")
        brow = sb.tile([P, 512], BF16, name="brow")
        ones = sb.tile([P, P], BF16, name="ones")
        ident = sb.tile([P, P], F32, name="ident")
        e32 = sb.tile([P, 384], F32, name="e32")
        ebf = [sb.tile([P, 384], BF16, name="ebf%d" % j) for j in range(3)]
        edge = sb.tile([P, 2], F32, name="edge")
        mask = sb.tile([P, 2], F32, name="mask")
        bm = sb.tile([P, 256], BF16, name="bm")
        zt = sb.tile([P, 64], F32, name="zt")
        xps = [sb.tile([P, 2, XW], F32, name="xp%d" % i) for i in range(3)]
        wss = [sb.tile([P, NB, P], F32, name="wS%d" % i) for i in range(2)]
        wts = [sb.tile([P, NB * P], BF16, name="wT%d" % i) for i in range(2)]
        wsb = [sb.tile([P, NB, NWP], BF16, name="wB%d" % i) for i in range(2)]
        pvg = [sb.tile([P, 2, 9 * NG], F32, name="pg%d" % i) for i in range(2)]
        pvv = [sb.tile([P, 2, 9 * NV], F32, name="pw%d" % i) for i in range(2)]
        px4 = sb.tile([P, 2, 36], F32, name="px4")
        pms = [sb.tile([P, 2, 9, 256], F32, name="pm%d" % i) for i in range(3)]
        ys = [sb.tile([P, NB + 1, YW], F32, name="y%d" % i) for i in range(3)]
        lbs = [sb.tile([P, NB + 2, 72], F32, name="lb%d" % i) for i in range(2)]
        yts = sb.tile([P, 4 * P], F32, name="yts")

        xips = [ps.tile([P, 512], F32, name="xiP%d" % i) for i in range(3)]
        wps = [ps.tile([P, NB, NWP], BF16, name="wP%d" % i) for i in range(2)]
        misc = ps.tile([P, 512], F32, name="misc")
        lsh0 = misc[:, 0:(NB + 1) * 72].rearrange("p (n c) -> p n c", c=72)
        acct = ps.tile([P, 4 * P], F32, name="acct")
        yb = ps.tile([P, 4 * P], F32, name="yb")

        def load_scales(dst, src, c0, c1):
            for q in range(4):
                nc.sync.dma_start(
                    out=dst[32 * q:32 * q + 4, :, :].bitcast(I32),
                    in_=src[:, 4 * q:4 * q + 4, c0:c1].rearrange("g r n -> r g n").bitcast(I32),
                )

        def load_chunk(c):
            xc = xcs[c % 2]
            xs = xss[c % 2]
            nc.sync.dma_start(
                out=xc[:].bitcast(I32),
                in_=x_words[:, :, 1024 * c:1024 * (c + 1)].rearrange("g p n -> p g n").bitcast(I32),
            )
            load_scales(xs, x_scales, 512 * c, 512 * (c + 1))

        def load_w(q, rows=(1, 0, 2)):
            src = w_flat[1024 * q:1024 * (q + 1), :].rearrange("(n p) c -> p n c", p=P)
            for r in rows:
                dst = wrs[q % 2][r]
                if r == 0:
                    nc.sync.dma_start(out=dst[0:96, :, :], in_=src[32:P, :, :])
                    nc.sync.dma_start(out=dst[96:P, 0:7, :], in_=src[0:32, 1:8, :])
                if r == 1:
                    nc.sync.dma_start(out=dst[:], in_=src)
                if r == 2:
                    nc.sync.dma_start(out=dst[32:P, :, :], in_=src[0:96, :, :])
                    nc.sync.dma_start(out=dst[0:32, 1:8, :], in_=src[96:P, 0:7, :])

        ctx.enter_context(tc.manual_schedule())

        nc.vector.memset(brow[:], 0.0)
        nc.vector.memset(wis[:].bitcast(I32), 0)
        nc.vector.memset(xss[0][:].bitcast(I32), 0)
        nc.vector.memset(ones[:], 1.0)
        nc.scalar.dma_start(
            out=wrs[0][1][:], in_=w_flat[0:1024, :].rearrange("(n p) c -> p n c", p=P))
        nc.gpsimd.dma_start(out=brow[0:1, :], in_=bi.rearrange("(o n) -> o n", o=1))
        for i in range(3):
            nc.tensor.matmul(out=acct[:], lhsT=ones[:], rhs=brow[:], start=True, stop=True)
        nc.scalar.copy(out=bias_bf[:], in_=acct[:])
        xc0 = xcs[0][:].rearrange("p g n -> p (g n)").rearrange("p (k g n) -> p k g n", k=NB, g=PASSES)

        def load_first(kk):
            nc.sync.dma_start(
                out=xc0[:, kk, :, :].bitcast(I32),
                in_=x_words[:, :, 256 * kk:256 * (kk + 1)].rearrange("g p n -> p g n").bitcast(I32))

        def load_wi(g0, g1):
            nc.sync.dma_start(
                out=wic[:, g0:g1, :].bitcast(I32),
                in_=Wi_words[g0:g1, :, :].rearrange("g p n -> p g n").bitcast(I32))

        load_first(0)
        load_wi(0, 2)
        load_scales(wis, Wi_scales, 0, 512)
        load_scales(xss[0], x_scales, 0, 512)
        load_wi(2, 5)
        load_wi(5, 8)
        for kk in range(1, NB):
            load_first(kk)

        make_identity(nc, ident[:])
        nc.vector.memset(e32[:], 0.0)
        nc.vector.tensor_copy(out=e32[:, 128:256], in_=ident[:])
        nc.vector.tensor_reduce(out=edge[:, 0:1], in_=ident[:, 0:128:32], axis=AX.X, op=ALU.add)
        nc.vector.tensor_reduce(out=edge[:, 1:2], in_=ident[:, 31:128:32], axis=AX.X, op=ALU.add)
        nc.vector.tensor_scalar(out=mask[:], in0=edge[:], scalar1=-1.0, scalar2=1.0, op0=ALU.mult, op1=ALU.add)
        nc.vector.tensor_scalar(out=ebf[0][:], in0=e32[:], scalar1=mask[:, 0:1], scalar2=None, op0=ALU.mult)
        nc.vector.tensor_copy(out=ebf[1][:], in_=e32[:])
        nc.vector.tensor_scalar(out=ebf[2][:], in0=e32[:], scalar1=mask[:, 1:2], scalar2=None, op0=ALU.mult)
        for i in range(2):
            nc.gpsimd.memset(wss[i][:], 0.0)
        for i in range(3):
            nc.vector.memset(xps[i][:, :, 0:9], 0.0)
            nc.vector.memset(xps[i][:, :, 521:XW], 0.0)
        nc.vector.memset(xss[1][:].bitcast(I32), 0)
        for i in range(2):
            nc.vector.memset(wrs[i][0][96:P, 7, :], 0.0)
            nc.vector.memset(wrs[i][2][0:32, 0, :], 0.0)
        nc.vector.memset(zt[:], 0.0)
        nc.vector.memset(lbs[0][:, 0, :], 0.0)
        nc.vector.memset(lbs[(NT // NB - 1) % 2][:, NB + 1, :], 0.0)
        nc.vector.memset(ys[(NT // NB - 1) % 3][:, NB, :], 0.0)

        nu = NT // 2
        nbat = NT // NB

        def pos(u):
            return 2 * (u % 2) if u < nu - 2 else 2 * ((u + 1) % 2)

        def mx(u, k):
            if not 0 <= u < nu:
                return
            xc = xcs[(u // 2) % 2]
            xs = xss[(u // 2) % 2]
            kk = pos(u) + k
            acc = xips[(2 * u + k) % 3]
            for g in range(PASSES):
                nc.tensor.matmul_mx(
                    out=acc[:],
                    lhsT=(xc0[:, kk, g, :] if u < 2 else xc[:, g, 256 * kk:256 * (kk + 1)]).bitcast(FP4),
                    lhsT_scale=xs[:, g, 128 * kk:128 * (kk + 1)],
                    rhs=wic[:, g, :].bitcast(FP4),
                    rhs_scale=wis[:, g, :],
                    start=(g == 0),
                    stop=(g == PASSES - 1),
                )

        def wshift(b, ta=0, tb=9):
            if not 0 <= b < nbat:
                return
            wp = wps[b % 2]
            n0 = NB * b % 8
            wr = wrs[(b // 2) % 2]
            for t in range(ta, tb):
                e = ebf[t % 3]
                c0 = COL[(t, GLO[t])]
                ncol = WTP if t < GT else 9 * (GHI[t] - GLO[t] + 1)
                w0 = 9 * GLO[t]
                d = DELTA[t] if b == 0 else t % 3 - 1
                over = b == 0 and t // 3 != 1
                nc.tensor.matmul(
                    out=wp[:, :, c0:c0 + ncol],
                    lhsT=e[:, 128 - d:256 - d],
                    rhs=wr[1 if b == 0 else t // 3][:, n0:n0 + NB, w0:w0 + ncol],
                    start=True,
                    stop=not over,
                )
                if over:
                    k0, step, off = (0, 1, -d) if t // 3 == 0 else (1, -1, 256 - d)
                    nc.tensor.matmul(
                        out=wp[:, k0:NB, c0:c0 + ncol],
                        lhsT=e[:, off:off + 128],
                        rhs=wr[1][:, k0 + step:NB + step, w0:w0 + ncol],
                        start=False,
                        stop=True,
                    )

        def bias(u, k):
            if not 0 <= u < nu:
                return
            nc.vector.tensor_tensor(
                out=xps[u % 3][:, k, 9:521], in0=xips[(2 * u + k) % 3][:], in1=bias_bf[:], op=ALU.add)

        def biasmap():
            for gi, (g, t) in enumerate(WHOLE):
                c0 = 288 * g - 512 * t
                for m in range(9):
                    d = 9 * t + m
                    nc.tensor.matmul(
                        out=yb[:, 32 * gi:32 * gi + 32], lhsT=ebf[1][:, 128 - d:256 - d], rhs=brow[:, c0 + m:c0 + m + 280:9],
                        start=(m == 0), stop=(m == 8))

        def wtrans(b):
            for k in range(NB):
                nc.tensor.transpose(out=misc[:, P * k:P * (k + 1)], in_=wss[b % 2][:, k, :], identity=ident[:])

        def wtevac(b):
            nc.scalar.copy(out=wts[b % 2][:], in_=misc[:])

        def wsevac(b):
            if not 0 <= b < nbat:
                return
            wp4 = wps[b % 2][:].rearrange("p k (t x) -> p k t x", x=WTP)
            nc.scalar.copy(out=wss[b % 2][:, :, 0:9], in_=wp4[:, :, 0, 0:9])
            nc.scalar.copy(
                out=wss[b % 2][:, :, 9:81].rearrange("p k (t c) -> p k t c", c=9), in_=wp4[:, :, 1:9, 9:18])
            nc.scalar.copy(out=wsb[b % 2][:, :, 0:WTP * GT], in_=wps[b % 2][:, :, 0:WTP * GT])

        def pieces(eng, u):
            if u == nu - 1:
                return VB if eng == "V" else GB
            return VB if eng == "V" else GB

        def nmult(eng, u, k0=0, k1=2, some=None):
            if not 0 <= u < nu:
                return
            xp = xps[u % 3][:, k0:k1, :]
            e = nc.vector if eng == "V" else nc.gpsimd
            wp = (wps if eng == "V" else wsb)[(u // 2) % 2][:, pos(u) + k0:pos(u) + k1, :]
            pv = (pvv if eng == "V" else pvg)[u % 2][:, k0:k1, :]
            o = 0
            for i in pieces(eng, u):
                t, a, n, g, yc = SEGS[i]
                if some is None or i in some:
                    cw = COL[(t, g)]
                    e.tensor_tensor(
                        out=pv[:, :, 9 * o:9 * (o + n)].rearrange("p k (s m) -> p k s m", m=9),
                        in0=xp[:, :, a:a + 9 * n].rearrange("p k (s m) -> p k s m", m=9),
                        in1=wp[:, :, cw:cw + 9].unsqueeze(2).to_broadcast([P, k1 - k0, n, 9]),
                        op=ALU.mult,
                    )
                o += n

        def runs(eng, u):
            out_runs = []
            o = 0
            for i in pieces(eng, u):
                n, yc = SEGS[i][2], SEGS[i][4]
                if out_runs and out_runs[-1][2] + out_runs[-1][0] == yc:
                    out_runs[-1][0] += n
                else:
                    out_runs.append([n, o, yc, 1])
                o += n
            merged = []
            for r in out_runs:
                if merged and merged[-1][0] == r[0] and merged[-1][2] + 65 * merged[-1][3] == r[2]:
                    merged[-1][3] += 1
                else:
                    merged.append(r)
            return merged

        def vreduce(u, eng, lo=0, hi=99):
            if not 0 <= u < nu:
                return
            y = ys[(u // 2) % 3]
            s0 = pos(u)
            pv = (pvv if eng == "V" else pvg)[u % 2]
            for n, o, yc, q in runs(eng, u)[lo:hi]:
                if q == 1:
                    nc.vector.tensor_reduce(
                        out=y[:, s0:s0 + 2, yc:yc + n],
                        in_=pv[:, :, 9 * o:9 * (o + n)].rearrange("p k (s m) -> p k s m", m=9),
                        axis=AX.X, op=ALU.add)
                else:
                    nc.vector.tensor_reduce(
                        out=y[:, s0:s0 + 2, yc:yc + 65 * q].rearrange("p k (q c) -> p k q c", c=65)[:, :, :, 0:n],
                        in_=pv[:, :, 9 * o:9 * (o + n * q)].rearrange("p k (q s m) -> p k q s m", q=q, m=9),
                        axis=AX.X, op=ALU.add)

        def vplane(u, k):
            if not 0 <= u < nu:
                return
            for gi, kk in VPL[:VN[u % 2]]:
                if kk == k:
                    g, t = WHOLE[gi]
                    c0 = 288 * g - 512 * t
                    nc.vector.tensor_tensor(
                        out=pms[u % 3][:, k, :, 32 * gi:32 * gi + 32],
                        in0=xips[(2 * u + k) % 3][:, c0:c0 + 288].rearrange("p (j m) -> p m j", m=9),
                        in1=wss[(u // 2) % 2][:, pos(u) + k, 9 * t:9 * t + 9].unsqueeze(2).to_broadcast([P, 9, 32]),
                        op=ALU.mult)

        def smult(u, k, g0=0, g1=8):
            if not 0 <= u < nu:
                return
            acc = xips[(2 * u + k) % 3]
            ws = wss[(u // 2) % 2]
            pm = pms[u % 3]
            kk = pos(u) + k
            for gi in range(g0, g1):
                g, t = WHOLE[gi]
                if (gi, k) in VPL[:VN[u % 2]]:
                    continue
                c0 = 288 * g - 512 * t
                for m in range(9):
                    nc.scalar.activation(
                        out=pm[:, k, m, 32 * gi:32 * gi + 32],
                        in_=acc[:, c0 + m:c0 + m + 280:9],
                        func=ACT.Copy,
                        scale=ws[:, kk, 9 * t + m:9 * t + m + 1],
                    )

        def keep():
            nc.tensor.matmul(
                out=wps[(nbat - 2) % 2][:].rearrange("p n c -> p (n c)")[:, 0:512], lhsT=ebf[1][:, 128:256], rhs=bias_bf[:],
                start=True, stop=True)

        def fwd_s(u, c0=0, c1=4):
            if not 0 <= u < nu:
                return
            for c in range(c0, c1):
                for m in range(NPL):
                    nc.tensor.matmul(
                        out=acct[:, P * c:P * (c + 1)], lhsT=pms[u % 3][:, c // 2, m, P * (c % 2):P * (c % 2 + 1)],
                        rhs=ident[:], is_transpose=True, start=(m == 0), stop=(m == NPL - 1))
                if u >= nu - 3:
                    keep()

        def evact_s(u):
            if not 0 <= u < nu:
                return
            nc.scalar.copy(out=yts[:], in_=acct[:])

        def back_s(u):
            if not 0 <= u < nu:
                return
            for k in range(2):
                nc.tensor.matmul(
                    out=yb[:, 2 * P * k:2 * P * (k + 1)], lhsT=wts[(u // 2) % 2][:, P * (pos(u) + k):P * (pos(u) + k + 1)],
                    rhs=bm[:], start=True, stop=False)
                for c in (2 * k, 2 * k + 1):
                    nc.tensor.matmul(
                        out=yb[:, P * c:P * (c + 1)], lhsT=yts[:, P * c:P * (c + 1)], rhs=ident[:],
                        is_transpose=True, start=False, stop=(c % 2 == 1))

        def evacy_s(u):
            if not 0 <= u < nu:
                return
            s0 = pos(u)
            for h in range(2):
                nc.vector.tensor_tensor(
                    out=ys[(u // 2) % 3][:, s0:s0 + 2, 1 + 293 * h:1 + 293 * h + 260].rearrange(
                        "p k (q c) -> p k q c", c=65)[:, :, :, 0:32],
                    in0=yb[:].rearrange("p (k h q c) -> p k h q c", k=2, h=2, c=32)[:, :, h, :, :],
                    in1=pms[u % 3][:, :, 8, P * h:P * (h + 1)].rearrange("p k (q c) -> p k q c", c=32),
                    op=ALU.add)

        def fin_a(b, j0=0, j1=NB, eng="S"):
            if not 0 <= b < nbat:
                return
            (nc.scalar.copy if eng == "S" else nc.vector.tensor_copy)(
                out=lbs[b % 2][:, 1 + j0:1 + j1, 0:64].rearrange("p n (t c) -> p n t c", c=8),
                in_=ys[b % 3][:, j0:j1, 50:514].rearrange("p n (t c) -> p n t c", c=58)[:, :, :, 0:8],
            )
            if b + 1 < nbat:
                nc.scalar.copy(
                    out=lbs[(b + 1) % 2][:, 0, 0:64].rearrange("p (t c) -> p t c", c=8),
                    in_=ys[b % 3][:, NB - 1, 50:514].rearrange("p (t c) -> p t c", c=58)[:, :, 0:8],
                )

        def fin_b(b, j0=0, j1=NB, bank=None):
            if not 0 <= b < nbat:
                return
            lsh = lsh0 if bank is None else bank
            cur = lbs[b % 2][:, 1 + j0:1 + j1, :].rearrange("p n (a b) -> p n a b", b=24)
            prv = lbs[b % 2][:, j0:j1, :].rearrange("p n (a b) -> p n a b", b=24)
            l4 = lsh[:, j0:j1, :].rearrange("p n (a b) -> p n a b", b=24)
            nc.tensor.matmul(out=l4[:, :, :, 0:16], lhsT=e32[:, 127:255], rhs=cur[:, :, :, 0:16], start=True, stop=False)
            nc.tensor.matmul(out=l4[:, :, :, 8:16], lhsT=e32[:, 255:383], rhs=prv[:, :, :, 8:16], start=False, stop=True)
            nc.tensor.matmul(out=l4[:, :, 0:2, 16:24], lhsT=e32[:, 98:226], rhs=cur[:, :, 0:2, 16:24], start=True, stop=False)
            nc.tensor.matmul(out=l4[:, :, 0:2, 16:24], lhsT=e32[:, 226:354], rhs=prv[:, :, 0:2, 16:24], start=False, stop=True)

        def fin_c(b, j0=0, j1=NB, s0=None, fix=True, eng="S", bank=None, gq=(), taps=tuple(range(9))):
            if not 0 <= b < nbat:
                return
            t0 = NB * b
            y = ys[b % 3]
            lsh = lsh0 if bank is None else bank
            last = b == nbat - 1 and j1 > NB
            if fix:
                nc.vector.tensor_tensor(
                    out=y[:, j0:j1, 58:465:58], in0=lsh[:, j0:j1, 7:64:8], in1=y[:, j0:j1, 58:465:58], op=ALU.add)
            for t in range(2, 9 if fix else 2):
                if eng == "S":
                    nc.scalar.copy(
                        out=y[:, j0:j1, 57 * t + 1:58 * t],
                        in_=lsh[:, j0:j1, 8 * (t - 1) + 8 - t:8 * (t - 1) + 7],
                    )
                else:
                    nc.vector.tensor_copy(
                        out=y[:, j0:j1, 57 * t + 1:58 * t],
                        in_=lsh[:, j0:j1, 8 * (t - 1) + 8 - t:8 * (t - 1) + 7],
                    )
            if s0 is None:
                s0 = j0
            for t in (taps if s0 >= 0 else ()):
                d = DELTA[t]
                c0 = 56 * t
                wd = WID[t]
                st = START[t]
                k0, k1 = s0, min(j1, NB)
                if b == 0 and d > 0:
                    nc.sync.dma_start(out=out_flat[0:P - d, c0:c0 + wd], in_=y[d:P, 0, st:st + wd])
                    k0 = 1
                if last and d < 0:
                    r0 = P * (NT - 1) - d
                    nc.sync.dma_start(out=out_flat[r0:P * NT, c0:c0 + wd], in_=y[0:P + d, NB - 1, st:st + wd])
                    k1 = NB - 1
                if last and d > 1:
                    nc.sync.dma_start(out=out_flat[P * NT - d:P * NT, c0:c0 + wd], in_=y[0:d, NB, st:st + wd])
                if last and d == 1:
                    nc.gpsimd.dma_start(
                        out=out_flat[P * NT - 1:P * NT, c0:c0 + wd].rearrange("o (a c) -> (o a) c", c=8),
                        in_=y[0:7, NB, st:st + 8],
                    )
                r0 = P * (t0 + k0) - d
                if k1 > k0:
                    (nc.gpsimd if t in gq else nc.sync).dma_start(
                        out=out_flat[r0:r0 + P * (k1 - k0), c0:c0 + wd].rearrange("(n p) c -> p n c", p=P),
                        in_=y[:, k0:k1, st:st + wd],
                    )

        def early4_m(u):
            g, t = WHOLE[3]
            a0 = 9 + 288 * g - 512 * t + 9 * 28
            cw = COL[(t, g)]
            kk = pos(u)
            nc.vector.tensor_tensor(
                out=px4[:].rearrange("p k (s m) -> p k s m", m=9),
                in0=xps[u % 3][:, :, a0:a0 + 36].rearrange("p k (s m) -> p k s m", m=9),
                in1=wps[(u // 2) % 2][:, kk:kk + 2, cw:cw + 9].unsqueeze(2).to_broadcast([P, 2, 4, 9]),
                op=ALU.mult)

        def early4_r(u):
            kk = pos(u)
            nc.vector.tensor_reduce(
                out=ys[(u // 2) % 3][:, kk:kk + 2, 224:228], in_=px4[:].rearrange("p k (s m) -> p k s m", m=9),
                axis=AX.X, op=ALU.add)

        def zero_rows():
            for t in range(9):
                if DELTA[t] < -1:
                    nc.sync.dma_start(out=out_flat[0:-DELTA[t], 56 * t:56 * t + WID[t]], in_=zt[0:-DELTA[t], 0:WID[t]])
                if DELTA[t] == -1:
                    nc.sync.dma_start(
                        out=out_flat[0:1, 56 * t:56 * t + WID[t]].rearrange("o (a c) -> (o a) c", c=8),
                        in_=zt[0:7, 0:8],
                    )

        wshift(0)
        wsevac(0)
        for u in range(-1, nu - 1):
            if u == -1:
                load_chunk(1)
            if u == 0:
                load_w(0, (0, 2))
            if u == 1:
                load_w(1)
            if u > 0 and u % 2 == 1 and (u + 3) // 2 < nbat:
                load_chunk((u + 3) // 2)
            if u == 0:
                zero_rows()
            if u % 4 == 2 and (u + 2) // 4 + 1 < 8:
                load_w((u + 2) // 4 + 1)
            odd = u % 2 == 1 and u > 0
            even = u % 2 == 0
            back_s(u - 2)
            bias(u, 1)
            vplane(u, 1)
            evacy_s(u - 2)
            if u == 0:
                nmult("G", 0, 1, 2)
            fwd_s(u - 1, 0, 2)
            if even and u > 0:
                wshift((u + 2) // 2, 0, WA)
            if odd:
                wshift((u + 1) // 2, WA if u > 1 else 0, 9)
            mx(u + 1, 0)
            if u == -1:
                biasmap()
            if u == 0:
                nc.scalar.copy(out=bm[:], in_=yb[:, 0:256])
            fwd_s(u - 1, 2, 4)
            smult(u, 0, 0, 4)
            if odd:
                fin_a((u - 3) // 2)
                fin_b((u - 3) // 2)
            if even:
                fin_c((u - 4) // 2)
                wtrans(u // 2)
            smult(u, 0, 4, 8)
            mx(u + 1, 1)
            if u > 0:
                nmult("G", u)
            nmult("V", u)
            vreduce(u - 1, "V")
            vreduce(u - 1, "G", 0, 2)
            bias(u + 1, 0)
            vplane(u + 1, 0)
            if u == -1:
                nmult("G", 0, 0, 1)
            vreduce(u - 1, "G", 2)
            smult(u, 1, 0, 4)
            evact_s(u - 1)
            smult(u, 1, 4, 5)
            if odd:
                wsevac((u + 1) // 2)
            if even:
                wtevac(u // 2)
            smult(u, 1, 5, 8)
        a, b, c = nu - 3, nu - 2, nu - 1
        lsh1 = xips[(2 * c + 1) % 3][:, 0:(NB + 1) * 72].rearrange("p (n c) -> p n c", c=72)
        lsh2 = xips[(2 * c) % 3][:, 0:(NB + 1) * 72].rearrange("p (n c) -> p n c", c=72)
        back_s(a)
        bias(c, 1)
        vplane(c, 1)
        fwd_s(b)
        evacy_s(a)
        nmult("G", c)
        smult(c, 0, 0, 4)
        fin_a(nbat - 2)
        fin_b(nbat - 2)
        smult(c, 0, 4, 8)
        nmult("V", c)
        early4_m(c)
        vreduce(b, "V")
        fin_c(nbat - 2)
        smult(c, 1, 0, 3)
        evact_s(b)
        vreduce(b, "G")
        smult(c, 1, 3, 4)
        back_s(b)
        fwd_s(c, 0, 2)
        evacy_s(b)
        fin_a(nbat - 1, 2, NB, eng="V")
        vreduce(c, "V")
        smult(c, 1, 4, 8)
        fin_b(nbat - 1, 3, NB + 1, bank=lsh2)
        fwd_s(c, 2, 4)
        fin_c(nbat - 1, 3, NB + 1, 3, eng="V", bank=lsh2)
        vreduce(c, "G")
        early4_r(c)
        fin_a(nbat - 1, 0, 2, eng="V")
        evact_s(c)
        fin_b(nbat - 1, 0, 3, bank=lsh1)
        back_s(c)
        fin_c(nbat - 1, 0, 3, -1, eng="V", bank=lsh1)
        evacy_s(c)
        fin_c(nbat - 1, 0, 3, 0, fix=False)
